import numpy as np
import ml_dtypes


def mxq(x, axis, fmt="e4m3"):
    dtype, down = {"e4m3": (ml_dtypes.float8_e4m3fn, 7), "e5m2": (ml_dtypes.float8_e5m2, 14)}[fmt]
    v = np.moveaxis(np.asarray(x, np.float32).astype(ml_dtypes.bfloat16).astype(np.float64), axis, -1)
    blocks = v.reshape(v.shape[:-1] + (-1, 32))
    amax = np.abs(blocks).max(-1, keepdims=True)
    byte = np.maximum(np.where(amax > 0, np.frexp(amax)[1] - 1 + 127, 0) - down, 1)
    scale = np.exp2(byte - 127.0)
    codes = (blocks / scale).astype(np.float32).astype(dtype).astype(np.float64)
    return np.moveaxis((codes * scale).reshape(v.shape), -1, axis)


WIDE = False


def mx_kscale(k):
    if not WIDE:
        return np.ones(k)
    levels = np.array([10, -10, 5, -5, 0])
    a = np.random.permutation(np.resize(levels, k // 512 * 4)).reshape(k // 512, 4)
    idx = np.arange(k)
    return np.exp2(a[idx // 512, idx % 128 // 32])


BF16 = ml_dtypes.bfloat16


def bf(x):
    return np.asarray(x, np.float32).astype(BF16)


def f64(x):
    return np.asarray(x).astype(np.float64)


B, C, N, W, H = 2, 512, 512, 32, 32
M = W * H
SIGMA = 3.0


def setup_inputs():
    t = mx_kscale(C)
    a = np.sqrt(SIGMA) * C ** -0.25
    return {"q": bf(np.random.standard_normal((B, N, C)) * a),
            "k": bf(np.random.standard_normal((B, M, C)) * a),
            "v": bf(np.random.standard_normal((B, M, C)) * 8.0 * t),
            "Wo": bf(np.random.standard_normal((C, C)) * 0.25 / t),
            "bo": bf(np.random.standard_normal(C) * 0.2),
            "feat0": bf(np.random.standard_normal((B, C, N)))}


def reference(q, k, v, Wo, bo, feat0):
    energy = f64(q) @ f64(k).transpose(0, 2, 1)
    e = np.exp(energy - energy.max(-1, keepdims=True))
    ctx = (mxq(e, 2, "e4m3") @ mxq(f64(v), 1, "e4m3")) / e.sum(-1, keepdims=True) * C ** -0.5
    y = (mxq(ctx, 2, "e4m3") @ mxq(f64(Wo), 1, "e4m3").T) + f64(bo)
    return y.transpose(0, 2, 1) + f64(feat0)

@@ -1,0 +1,419 @@
+from contextlib import ExitStack
+import math
+
+import concourse.mybir as mybir
+from concourse.masks import make_identity
+
+F32 = mybir.dt.float32
+BF16 = mybir.dt.bfloat16
+U32 = mybir.dt.uint32
+U8 = mybir.dt.uint8
+FP8X4 = mybir.dt.float8_e4m3fn_x4
+ALU = mybir.AluOpType
+ACT = mybir.ActivationFunctionType
+AX = mybir.AxisListType
+
+P = 128
+B = 2
+C = 512
+N = 512
+M = 1024
+NT = 8
+FLOPS = 2 * B * (N * M * C + N * M * C + N * C * C)
+
+MANUAL = False
+TE_ENG = ("s", "s")
+W_ENG = "s"
+
+
+def tile_i2p_crossattention_pa_kernel(tc, q, k, v, Wo, bo, feat0, out):
+    nc = tc.nc
+    with ExitStack() as ctx:
+        if MANUAL:
+            ctx.enter_context(tc.manual_schedule())
+        keep = ctx.enter_context(tc.tile_pool(name="keep", bufs=1))
+        work = ctx.enter_context(tc.tile_pool(name="work", bufs=2))
+        psum = ctx.enter_context(tc.psum_pool(name="psum", bufs=1))
+
+        k_raw = [keep.tile([P, 8, C], BF16, name="k_raw%d" % b) for b in range(B)]
+        q_raw = [keep.tile([P, 4, C], BF16, name="q_raw%d" % b) for b in range(B)]
+        v_raw = [keep.tile([P, 8, C], BF16, name="v_raw%d" % b) for b in range(B)]
+        f_raw = [keep.tile([P, 4, N], BF16, name="f_raw%d" % b) for b in range(B)]
+        w_raw = keep.tile([P, 4, C], BF16, name="w_raw")
+        bo_rows = keep.tile([P, P], BF16, name="bo_rows")
+        bo_col = keep.tile([P, 4], F32, name="bo_col")
+        ident_b = keep.tile([P, P], BF16, name="ident_b")
+        ident_f = keep.tile([P, P], F32, name="ident_f")
+        kT = [keep.tile([P, 4, M], BF16, name="kT%d" % b) for b in range(B)]
+        qT = [keep.tile([P, 4, N], BF16, name="qT%d" % b) for b in range(B)]
+        vW = [keep.tile([P, 2, C], U32, name="vW%d" % b, align_bytes=64) for b in range(B)]
+        vS = [keep.tile([P, 2, C], U8, name="vS%d" % b, align_bytes=64) for b in range(B)]
+        wG = keep.tile([P, 4, P, 4], BF16, name="wG", align_bytes=64)
+        wW = keep.tile([P, C], U32, name="wW", align_bytes=64)
+        wS = keep.tile([P, C], U8, name="wS", align_bytes=64)
+        fb = [keep.tile([P, 4, N], F32, name="fb%d" % b) for b in range(B)]
+
+        def load_k(b, g):
+            nc.sync.dma_start(
+                out=k_raw[b][:, 4 * g : 4 * g + 4, :],
+                in_=k[b, 512 * g : 512 * g + 512, :].rearrange("(p t) c -> p t c", t=4),
+            )
+
+        def load_v(b, g):
+            nc.sync.dma_start(
+                out=v_raw[b][:, 4 * g : 4 * g + 4, :],
+                in_=v[b, 512 * g : 512 * g + 512, :].rearrange("(p t) c -> p t c", t=4),
+            )
+
+        def load_q(b, i0, i1):
+            nc.sync.dma_start(
+                out=q_raw[b][:, i0:i1, :],
+                in_=q[b, P * i0 : P * i1, :].rearrange("(i p) c -> p i c", p=P),
+            )
+
+        nc.vector.memset(bo_rows[:], 0.0)
+        make_identity(nc, ident_b[:])
+        make_identity(nc, ident_f[:])
+
+        nc.scalar.dma_start(out=bo_rows[0:4, :], in_=bo.rearrange("(t p) -> t p", p=P))
+        load_k(0, 0)
+        load_q(0, 0, 1)
+        load_k(0, 1)
+        load_q(0, 1, 4)
+        load_k(1, 0)
+        load_k(1, 1)
+        load_q(1, 0, 4)
+        load_v(0, 0)
+        load_v(0, 1)
+        nc.sync.dma_start(out=w_raw[:], in_=Wo.rearrange("(t p) c -> p t c", p=P))
+        nc.sync.dma_start(out=f_raw[0][:], in_=feat0[0].rearrange("(t p) n -> p t n", p=P))
+        load_v(1, 0)
+        load_v(1, 1)
+        nc.sync.dma_start(out=f_raw[1][:], in_=feat0[1].rearrange("(t p) n -> p t n", p=P))
+
+        def copy_on(eng, dst, src):
+            if eng == "s":
+                nc.scalar.copy(out=dst, in_=src)
+            else:
+                nc.vector.tensor_copy(out=dst, in_=src)
+
+        def job(count, src_of, post, tag="tp", lo=0, due=99):
+            hold = []
+
+            def one(x):
+                if not hold:
+                    hold.append(
+                        psum.tile([P, 4, P], BF16, name="tps", tag=tag, bufs=(4 if tag == "en" else 2))
+                    )
+                nc.tensor.transpose(hold[0][:, x, :], src_of(x), ident_b[:])
+
+            def run(x):
+                one(x)
+                if x == count - 1:
+                    post(hold[0])
+
+            return [{"run": (lambda x=x: run(x)), "lo": lo, "due": due} for x in range(count)]
+
+        def weave(mms, jobs, cap):
+            ops = sum(jobs, [])
+            at = 0
+            for m, mm in enumerate(mms):
+                while any(o["due"] <= m for o in ops[at:]):
+                    ops[at]["run"]()
+                    at += 1
+                mm()
+                budget = cap
+                while budget > 0 and at < len(ops) and ops[at]["lo"] <= m:
+                    ops[at]["run"]()
+                    at += 1
+                    budget -= 1
+            while at < len(ops):
+                ops[at]["run"]()
+                at += 1
+
+        def k_job(b, j, eng="s", tag="tp", due=99):
+            return job(
+                4,
+                lambda cc: k_raw[b][:, j, P * cc : P * cc + P],
+                lambda ps: copy_on(eng, kT[b][:, :, P * j : P * j + P], ps[:]),
+                tag=tag,
+                due=due,
+            )
+
+        def q_job(b, i, eng="s", tag="tp"):
+            return job(
+                4,
+                lambda cc: q_raw[b][:, i, P * cc : P * cc + P],
+                lambda ps: copy_on(eng, qT[b][:, :, P * i : P * i + P], ps[:]),
+                tag=tag,
+            )
+
+        def w_post(ot, ps):
+            copy_on(W_ENG, wG[:, ot, :, :], ps[:].rearrange("p t o -> p o t"))
+            if ot == 3:
+                nc.vector.quantize_mx(
+                    out=wW[:].bitcast(FP8X4),
+                    scales=wS[:],
+                    in_=wG[:].rearrange("p a o t -> p (a o t)"),
+                )
+
+        def w_job(ot):
+            return job(4, lambda t: w_raw[:, ot, P * t : P * t + P], lambda ps: w_post(ot, ps))
+
+        def bo_post(ps):
+            nc.vector.tensor_copy(out=bo_col[:], in_=ps[:, 0, 0:4])
+
+        def bo_job():
+            return job(1, lambda x: bo_rows[:], bo_post)
+
+        def add_bias(b):
+            for ot in range(4):
+                nc.gpsimd.tensor_scalar(
+                    out=fb[b][:, ot, :],
+                    in0=f_raw[b][:, ot, :],
+                    scalar1=1.0,
+                    scalar2=bo_col[:, ot : ot + 1],
+                    op0=ALU.mult,
+                    op1=ALU.add,
+                )
+
+        vG = {}
+
+        def v_regroup(b, g):
+            vG[(b, g)] = work.tile([P, C, 4], BF16, name="vG", tag="vG", bufs=2, align_bytes=64)
+            nc.vector.tensor_copy(
+                out=vG[(b, g)][:].rearrange("p (c i) t -> p c t i", i=4),
+                in_=v_raw[b][:, 4 * g : 4 * g + 4, :].rearrange("p t (c i) -> p c t i", i=4),
+            )
+
+        def v_quant(b, g):
+            nc.vector.quantize_mx(
+                out=vW[b][:, g, :].bitcast(FP8X4),
+                scales=vS[b][:, g, :],
+                in_=vG[(b, g)][:].rearrange("p c t -> p (c t)"),
+            )
+
+        st = [{} for s in range(NT)]
+
+        def energy_mms(s, hook0, hook1):
+            b, i = divmod(s, 4)
+            d = st[s]
+            d["en"] = []
+            d["mx"] = work.tile([P, 2], F32, name="mx", tag="mx", bufs=8)
+            d["nm"] = work.tile([P, 1], F32, name="nm", tag="nm", bufs=8)
+
+            def mm(h, cc):
+                if cc == 0:
+                    d["en"].append(psum.tile([P, 512], F32, name="en", tag="en", bufs=4))
+                nc.tensor.matmul(
+                    out=d["en"][h][:],
+                    lhsT=qT[b][:, cc, P * i : P * i + P],
+                    rhs=kT[b][:, cc, 512 * h : 512 * h + 512],
+                    start=(cc == 0),
+                    stop=(cc == 3),
+                )
+                if cc == 3:
+                    nc.vector.tensor_reduce(
+                        out=d["mx"][:, h : h + 1], in_=d["en"][h][:], axis=AX.X, op=ALU.max
+                    )
+                    if h == 1:
+                        nc.vector.tensor_reduce(
+                            out=d["nm"][:], in_=d["mx"][:], axis=AX.X, op=ALU.max, negate=True
+                        )
+                        hook1()
+                    else:
+                        hook0()
+
+            return [(lambda h=h, cc=cc: mm(h, cc)) for h in range(2) for cc in range(4)]
+
+        def exps(s):
+            d = st[s]
+            d["e"] = work.tile([P, M], BF16, name="e", tag="e", bufs=8)
+            d["rs"] = work.tile([P, 2], F32, name="rs", tag="rs", bufs=8)
+            for h in range(2):
+                nc.scalar.activation(
+                    out=d["e"][:, 512 * h : 512 * h + 512],
+                    in_=d["en"][h][:],
+                    func=ACT.Exp,
+                    bias=d["nm"][:, 0:1],
+                    scale=1.0,
+                    accum_out=d["rs"][:, h : h + 1],
+                )
+
+        def rsum(s):
+            d = st[s]
+            d["rq"] = work.tile([P, 1], F32, name="rq", tag="rq", bufs=8)
+            d["ri"] = work.tile([P, 1], F32, name="ri", tag="ri", bufs=8)
+            nc.vector.tensor_scalar(
+                out=d["rq"][:],
+                in0=d["rs"][:, 0:1],
+                scalar1=d["rs"][:, 1:2],
+                scalar2=math.sqrt(C),
+                op0=ALU.add,
+                op1=ALU.mult,
+            )
+            nc.vector.reciprocal(out=d["ri"][:], in_=d["rq"][:])
+
+        def te_post(s, g, ps):
+            d = st[s]
+            copy_on(TE_ENG[g], d["eG"][:, g, :, :], ps[:].rearrange("p t n -> p n t"))
+
+        def quant_e(s):
+            d = st[s]
+            d["eW"] = work.tile([P, 2 * P], U32, name="eW", tag="eW", bufs=8, align_bytes=64)
+            d["eS"] = work.tile([P, 2 * P], U8, name="eS", tag="eS", bufs=8, align_bytes=64)
+            nc.vector.quantize_mx(
+                out=d["eW"][:].bitcast(FP8X4),
+                scales=d["eS"][:],
+                in_=d["eG"][:].rearrange("p g n t -> p (g n t)"),
+            )
+
+        def te_jobs(s, lo0, lo1):
+            d = st[s]
+            d["eG"] = work.tile([P, 2, P, 4], BF16, name="eG", tag="eG", bufs=8, align_bytes=64)
+            return [
+                job(
+                    4,
+                    (lambda t, g=g: d["e"][:, P * (4 * g + t) : P * (4 * g + t) + P]),
+                    (lambda ps, g=g: te_post(s, g, ps)),
+                    lo=(lo0 if g == 0 else lo1),
+                )
+                for g in range(2)
+            ]
+
+        def spread_rinv(s):
+            d = st[s]
+            rbp = psum.tile([P, P], F32, name="rbp", tag="tp", bufs=2)
+            nc.tensor.transpose(rbp[:], d["ri"][:, 0:1].to_broadcast([P, P]), ident_f[:])
+            d["rb"] = work.tile([P, P], F32, name="rb", tag="rb", bufs=8)
+            nc.scalar.copy(out=d["rb"][:], in_=rbp[:])
+
+        def rb_job(s, lo):
+            return [{"run": (lambda: spread_rinv(s)), "lo": lo, "due": 99}]
+
+        def mx1(s):
+            b = s // 4
+            d = st[s]
+            d["c1"] = psum.tile([P, 4, P], F32, name="c1", tag="c1", bufs=1)
+            for t in range(4):
+                for g in range(2):
+                    nc.tensor.matmul_mx(
+                        out=d["c1"][:, t, :],
+                        lhsT=vW[b][:, g, P * t : P * t + P].bitcast(FP8X4),
+                        lhsT_scale=vS[b][:, g, P * t : P * t + P],
+                        rhs=d["eW"][:, P * g : P * g + P].bitcast(FP8X4),
+                        rhs_scale=d["eS"][:, P * g : P * g + P],
+                        start=(g == 0),
+                        stop=(g == 1),
+                    )
+
+        def ctx_out(s):
+            d = st[s]
+            d["cG"] = work.tile([P, P, 4], BF16, name="cG", tag="cG", bufs=8, align_bytes=64)
+            d["cW"] = work.tile([P, P], U32, name="cW", tag="cW", bufs=8, align_bytes=64)
+            d["cS"] = work.tile([P, P], U8, name="cS", tag="cS", bufs=8, align_bytes=64)
+            nc.vector.tensor_tensor(
+                out=d["cG"][:],
+                in0=d["c1"][:].rearrange("p t n -> p n t"),
+                in1=d["rb"][:].unsqueeze(2).to_broadcast([P, P, 4]),
+                op=ALU.mult,
+            )
+            nc.vector.quantize_mx(
+                out=d["cW"][:].bitcast(FP8X4),
+                scales=d["cS"][:],
+                in_=d["cG"][:].rearrange("p n t -> p (n t)"),
+            )
+
+        def mx2(s):
+            b, i = divmod(s, 4)
+            d = st[s]
+            y = psum.tile([P, 4, P], F32, name="y", tag="y", bufs=1)
+            for ot in range(4):
+                nc.tensor.matmul_mx(
+                    out=y[:, ot, :],
+                    lhsT=wW[:, P * ot : P * ot + P].bitcast(FP8X4),
+                    lhsT_scale=wS[:, P * ot : P * ot + P],
+                    rhs=d["cW"][:].bitcast(FP8X4),
+                    rhs_scale=d["cS"][:],
+                    start=True,
+                    stop=True,
+                )
+            d["y"] = y
+
+        def final(s):
+            b, i = divmod(s, 4)
+            y = st[s]["y"]
+            o_sb = work.tile([P, 4, P], F32, name="o_sb", tag="o_sb", bufs=3)
+            nc.vector.tensor_tensor(
+                out=o_sb[:], in0=y[:], in1=fb[b][:, :, P * i : P * i + P], op=ALU.add
+            )
+            nc.sync.dma_start(
+                out=out[b].rearrange("(t p) n -> p t n", p=P)[:, :, P * i : P * i + P],
+                in_=o_sb[:],
+            )
+
+        def live(x):
+            return 0 <= x < NT
+
+        head = [
+            k_job(0, 0, "v", "en"),
+            k_job(0, 1, "s", "en"),
+            k_job(0, 2, "v", "en"),
+            k_job(0, 3, "s", "en"),
+            q_job(0, 0, "v", "tp"),
+            k_job(0, 4, "s", "tp"),
+            k_job(0, 5, "v", "en"),
+            k_job(0, 6, "s", "en"),
+            k_job(0, 7, "v", "en"),
+        ]
+        weave([], head, 0)
+
+        fills = {
+            0: [q_job(0, 1, "s"), q_job(0, 2, "v"), q_job(0, 3, "s"), k_job(1, 0, "v"), k_job(1, 1, "s"), k_job(1, 2, "v"), k_job(1, 3, "s")],
+            1: [k_job(1, 4, "v"), k_job(1, 5, "s"), k_job(1, 6, "v"), k_job(1, 7, "s"), q_job(1, 0, "v")],
+            2: [q_job(1, 1), q_job(1, 2), q_job(1, 3), bo_job(), w_job(0)],
+            3: [w_job(1), w_job(2), w_job(3)],
+        };
+        caps = {0: 4, 1: 4, 2: 4, 3: 3};
+        LT = 1
+        L1 = 2
+        L2 = 3
+        vx = {(2, 2): [("rg", 0, 0)], (2, 3): [("rg", 0, 1), ("vq", 0, 0), ("vq", 0, 1)], (3, 3): [("fb", 0, 0)], (4, 2): [("rg", 1, 0)], (5, 2): [("rg", 1, 1)], (5, 3): [("vq", 1, 0), ("vq", 1, 1), ("fb", 1, 0)]}
+
+        def extras(s, where):
+            for name, a, b2 in vx.get((s, where), []):
+                if name == "rg":
+                    v_regroup(a, b2)
+                elif name == "vq":
+                    v_quant(a, b2)
+                elif name == "fb":
+                    add_bias(a)
+
+        for s in range(NT + L2 + 2):
+            if live(s - L2 - 1):
+                final(s - L2 - 1)
+            if live(s - L1 - 1):
+                ctx_out(s - L1 - 1)
+            if live(s - 1):
+                exps(s - 1)
+                rsum(s - 1)
+            extras(s, 0)
+            fill = fills.get(s, [])
+            jobs = fill
+            if live(s - LT):
+                lo0, lo1, lor = ((5, 7, 7) if s < 3 else (2, 4, 5))
+                te = te_jobs(s - LT, lo0, lo1)
+                rbj = rb_job(s - LT, lor)
+                nf = (3 if s < 3 else 1)
+                jobs = fill[0:nf] + [te[0]] + fill[nf : nf + 1] + [te[1], rbj] + fill[nf + 1 :]
+            if s < NT:
+                weave(energy_mms(s, lambda: extras(s, 1), lambda: extras(s, 2)), jobs, caps.get(s, 2))
+            else:
+                weave([], jobs, 0)
+            if live(s - LT):
+                quant_e(s - LT)
+            extras(s, 3)
+            if live(s - L2):
+                mx2(s - L2)
+            if live(s - L1):
+                mx1(s - L1)

@@ -21,9 +21,11 @@ M = 1024
 NT = 8
 FLOPS = 2 * B * (N * M * C + N * M * C + N * C * C)
 
-MANUAL = False
+MANUAL = True
 TE_ENG = ("s", "s")
 W_ENG = "s"
+V_ENG = "g"
+NB = {"en": 3, "tp": 3, "mx": 2}
 
 
 def tile_i2p_crossattention_pa_kernel(tc, q, k, v, Wo, bo, feat0, out):
@@ -44,8 +46,8 @@ def tile_i2p_crossattention_pa_kernel(tc, q, k, v, Wo, bo, feat0, out):
         bo_col = keep.tile([P, 4], F32, name="bo_col")
         ident_b = keep.tile([P, P], BF16, name="ident_b")
         ident_f = keep.tile([P, P], F32, name="ident_f")
-        kT = [keep.tile([P, 4, M], BF16, name="kT%d" % b) for b in range(B)]
-        qT = [keep.tile([P, 4, N], BF16, name="qT%d" % b) for b in range(B)]
+        kT = [keep.tile([P, 2, M], F32, name="kT%d" % b) for b in range(B)]
+        qT = [keep.tile([P, 2, N], F32, name="qT%d" % b) for b in range(B)]
         vW = [keep.tile([P, 2, C], U32, name="vW%d" % b, align_bytes=64) for b in range(B)]
         vS = [keep.tile([P, 2, C], U8, name="vS%d" % b, align_bytes=64) for b in range(B)]
         wG = keep.tile([P, 4, P, 4], BF16, name="wG", align_bytes=64)
@@ -53,10 +55,10 @@ def tile_i2p_crossattention_pa_kernel(tc, q, k, v, Wo, bo, feat0, out):
         wS = keep.tile([P, C], U8, name="wS", align_bytes=64)
         fb = [keep.tile([P, 4, N], F32, name="fb%d" % b) for b in range(B)]
 
-        def load_k(b, g):
+        def load_k(b, g, t0=0, t1=4):
             nc.sync.dma_start(
-                out=k_raw[b][:, 4 * g : 4 * g + 4, :],
-                in_=k[b, 512 * g : 512 * g + 512, :].rearrange("(p t) c -> p t c", t=4),
+                out=k_raw[b][:, 4 * g + t0 : 4 * g + t1, :],
+                in_=k[b, 512 * g : 512 * g + 512, :].rearrange("(p t) c -> p t c", t=4)[:, t0:t1, :],
             )
 
         def load_v(b, g):
@@ -76,10 +78,12 @@ def tile_i2p_crossattention_pa_kernel(tc, q, k, v, Wo, bo, feat0, out):
         make_identity(nc, ident_f[:])
 
         nc.scalar.dma_start(out=bo_rows[0:4, :], in_=bo.rearrange("(t p) -> t p", p=P))
-        load_k(0, 0)
-        load_q(0, 0, 1)
-        load_k(0, 1)
-        load_q(0, 1, 4)
+        load_k(0, 0, 0, 2)
+        load_k(0, 0, 2, 4)
+        load_q(0, 0, 2)
+        load_k(0, 1, 0, 2)
+        load_k(0, 1, 2, 4)
+        load_q(0, 2, 4)
         load_k(1, 0)
         load_k(1, 1)
         load_q(1, 0, 4)
@@ -103,7 +107,7 @@ def tile_i2p_crossattention_pa_kernel(tc, q, k, v, Wo, bo, feat0, out):
             def one(x):
                 if not hold:
                     hold.append(
-                        psum.tile([P, 4, P], BF16, name="tps", tag=tag, bufs=(4 if tag == "en" else 2))
+                        psum.tile([P, 4, P], BF16, name="tps", tag=tag, bufs=NB[tag])
                     )
                 nc.tensor.transpose(hold[0][:, x, :], src_of(x), ident_b[:])
 
@@ -131,22 +135,32 @@ def tile_i2p_crossattention_pa_kernel(tc, q, k, v, Wo, bo, feat0, out):
                 ops[at]["run"]()
                 at += 1
 
-        def k_job(b, j, eng="s", tag="tp", due=99):
-            return job(
-                4,
-                lambda cc: k_raw[b][:, j, P * cc : P * cc + P],
-                lambda ps: copy_on(eng, kT[b][:, :, P * j : P * j + P], ps[:]),
-                tag=tag,
-                due=due,
-            )
+        def word_job(raw, dst, a, eng, tag, due):
+            hold = []
 
-        def q_job(b, i, eng="s", tag="tp"):
-            return job(
-                4,
-                lambda cc: q_raw[b][:, i, P * cc : P * cc + P],
-                lambda ps: copy_on(eng, qT[b][:, :, P * i : P * i + P], ps[:]),
-                tag=tag,
-            )
+            def run(x):
+                if not hold:
+                    hold.append(psum.tile([P, 2, 2, P], F32, name="wps", tag=tag, bufs=NB[tag]))
+                u, r = divmod(x, 2)
+                nc.tensor.transpose(
+                    hold[0][:, u, r, :],
+                    raw[:, 2 * a + r, :].bitcast(F32)[:, P * u : P * u + P],
+                    ident_f[:],
+                )
+                if x == 3:
+                    copy_on(
+                        eng,
+                        dst[:, :, 2 * P * a : 2 * P * a + 2 * P],
+                        hold[0][:].rearrange("p u r n -> p u (r n)"),
+                    )
+
+            return [{"run": (lambda x=x: run(x)), "lo": 0, "due": due} for x in range(4)]
+
+        def k_job(b, a, eng="s", tag="tp", due=99):
+            return word_job(k_raw[b], kT[b], a, eng, tag, due)
+
+        def q_job(b, a, eng="s", tag="tp", due=99):
+            return word_job(q_raw[b], qT[b], a, eng, tag, due)
 
         def w_post(ot, ps):
             copy_on(W_ENG, wG[:, ot, :, :], ps[:].rearrange("p t o -> p o t"))
@@ -180,11 +194,22 @@ def tile_i2p_crossattention_pa_kernel(tc, q, k, v, Wo, bo, feat0, out):
         vG = {}
 
         def v_regroup(b, g):
-            vG[(b, g)] = work.tile([P, C, 4], BF16, name="vG", tag="vG", bufs=2, align_bytes=64)
-            nc.vector.tensor_copy(
-                out=vG[(b, g)][:].rearrange("p (c i) t -> p c t i", i=4),
-                in_=v_raw[b][:, 4 * g : 4 * g + 4, :].rearrange("p t (c i) -> p c t i", i=4),
-            )
+            vG[(b, g)] = work.tile([P, C, 4], BF16, name="vG", tag="vG", bufs=4, align_bytes=64)
+            if V_ENG == "v":
+                nc.vector.tensor_copy(
+                    out=vG[(b, g)][:].rearrange("p (c i) t -> p c t i", i=4),
+                    in_=v_raw[b][:, 4 * g : 4 * g + 4, :].rearrange("p t (c i) -> p c t i", i=4),
+                )
+            else:
+                for hf in range(2):
+                    nc.gpsimd.tensor_scalar(
+                        out=vG[(b, g)][:, 256 * hf : 256 * hf + 256, :],
+                        in0=v_raw[b][:, 4 * g : 4 * g + 4, 256 * hf : 256 * hf + 256].rearrange("p t c -> p c t"),
+                        scalar1=1.0,
+                        scalar2=0.0,
+                        op0=ALU.mult,
+                        op1=ALU.add,
+                    )
 
         def v_quant(b, g):
             nc.vector.quantize_mx(
@@ -193,22 +218,25 @@ def tile_i2p_crossattention_pa_kernel(tc, q, k, v, Wo, bo, feat0, out):
                 in_=vG[(b, g)][:].rearrange("p c t -> p (c t)"),
             )
 
+        kTb = [t[:].bitcast(BF16).rearrange("p u (m e) -> p u m e", e=2) for t in kT]
+        qTb = [t[:].bitcast(BF16).rearrange("p u (m e) -> p u m e", e=2) for t in qT]
         st = [{} for s in range(NT)]
 
         def energy_mms(s, hook0, hook1):
             b, i = divmod(s, 4)
             d = st[s]
             d["en"] = []
-            d["mx"] = work.tile([P, 2], F32, name="mx", tag="mx", bufs=8)
-            d["nm"] = work.tile([P, 1], F32, name="nm", tag="nm", bufs=8)
+            d["mx"] = work.tile([P, 2], F32, name="mx", tag="mx", bufs=4)
+            d["nm"] = work.tile([P, 1], F32, name="nm", tag="nm", bufs=4)
 
             def mm(h, cc):
                 if cc == 0:
-                    d["en"].append(psum.tile([P, 512], F32, name="en", tag="en", bufs=4))
+                    d["en"].append(psum.tile([P, 512], F32, name="en", tag="en", bufs=NB["en"]))
+                u, e2 = divmod(cc, 2)
                 nc.tensor.matmul(
                     out=d["en"][h][:],
-                    lhsT=qT[b][:, cc, P * i : P * i + P],
-                    rhs=kT[b][:, cc, 512 * h : 512 * h + 512],
+                    lhsT=qTb[b][:, u, P * i : P * i + P, e2],
+                    rhs=kTb[b][:, u, 512 * h : 512 * h + 512, e2],
                     start=(cc == 0),
                     stop=(cc == 3),
                 )
@@ -228,8 +256,8 @@ def tile_i2p_crossattention_pa_kernel(tc, q, k, v, Wo, bo, feat0, out):
 
         def exps(s):
             d = st[s]
-            d["e"] = work.tile([P, M], BF16, name="e", tag="e", bufs=8)
-            d["rs"] = work.tile([P, 2], F32, name="rs", tag="rs", bufs=8)
+            d["e"] = work.tile([P, M], BF16, name="e", tag="e", bufs=3)
+            d["rs"] = work.tile([P, 2], F32, name="rs", tag="rs", bufs=4)
             for h in range(2):
                 nc.scalar.activation(
                     out=d["e"][:, 512 * h : 512 * h + 512],
@@ -242,8 +270,8 @@ def tile_i2p_crossattention_pa_kernel(tc, q, k, v, Wo, bo, feat0, out):
 
         def rsum(s):
             d = st[s]
-            d["rq"] = work.tile([P, 1], F32, name="rq", tag="rq", bufs=8)
-            d["ri"] = work.tile([P, 1], F32, name="ri", tag="ri", bufs=8)
+            d["rq"] = work.tile([P, 1], F32, name="rq", tag="rq", bufs=4)
+            d["ri"] = work.tile([P, 1], F32, name="ri", tag="ri", bufs=4)
             nc.vector.tensor_scalar(
                 out=d["rq"][:],
                 in0=d["rs"][:, 0:1],
@@ -260,8 +288,8 @@ def tile_i2p_crossattention_pa_kernel(tc, q, k, v, Wo, bo, feat0, out):
 
         def quant_e(s):
             d = st[s]
-            d["eW"] = work.tile([P, 2 * P], U32, name="eW", tag="eW", bufs=8, align_bytes=64)
-            d["eS"] = work.tile([P, 2 * P], U8, name="eS", tag="eS", bufs=8, align_bytes=64)
+            d["eW"] = work.tile([P, 2 * P], U32, name="eW", tag="eW", bufs=4, align_bytes=64)
+            d["eS"] = work.tile([P, 2 * P], U8, name="eS", tag="eS", bufs=4, align_bytes=64)
             nc.vector.quantize_mx(
                 out=d["eW"][:].bitcast(FP8X4),
                 scales=d["eS"][:],
@@ -270,7 +298,7 @@ def tile_i2p_crossattention_pa_kernel(tc, q, k, v, Wo, bo, feat0, out):
 
         def te_jobs(s, lo0, lo1):
             d = st[s]
-            d["eG"] = work.tile([P, 2, P, 4], BF16, name="eG", tag="eG", bufs=8, align_bytes=64)
+            d["eG"] = work.tile([P, 2, P, 4], BF16, name="eG", tag="eG", bufs=3, align_bytes=64)
             return [
                 job(
                     4,
@@ -283,18 +311,18 @@ def tile_i2p_crossattention_pa_kernel(tc, q, k, v, Wo, bo, feat0, out):
 
         def spread_rinv(s):
             d = st[s]
-            rbp = psum.tile([P, P], F32, name="rbp", tag="tp", bufs=2)
+            rbp = psum.tile([P, P], F32, name="rbp", tag="tp", bufs=NB["tp"])
             nc.tensor.transpose(rbp[:], d["ri"][:, 0:1].to_broadcast([P, P]), ident_f[:])
-            d["rb"] = work.tile([P, P], F32, name="rb", tag="rb", bufs=8)
+            d["rb"] = work.tile([P, P], F32, name="rb", tag="rb", bufs=4)
             nc.scalar.copy(out=d["rb"][:], in_=rbp[:])
 
         def rb_job(s, lo):
             return [{"run": (lambda: spread_rinv(s)), "lo": lo, "due": 99}]
 
-        def mx1(s):
+        def mx1(s, tag="mx"):
             b = s // 4
             d = st[s]
-            d["c1"] = psum.tile([P, 4, P], F32, name="c1", tag="c1", bufs=1)
+            d["c1"] = psum.tile([P, 4, P], F32, name="c1", tag=tag, bufs=NB[tag])
             for t in range(4):
                 for g in range(2):
                     nc.tensor.matmul_mx(
@@ -309,9 +337,9 @@ def tile_i2p_crossattention_pa_kernel(tc, q, k, v, Wo, bo, feat0, out):
 
         def ctx_out(s):
             d = st[s]
-            d["cG"] = work.tile([P, P, 4], BF16, name="cG", tag="cG", bufs=8, align_bytes=64)
-            d["cW"] = work.tile([P, P], U32, name="cW", tag="cW", bufs=8, align_bytes=64)
-            d["cS"] = work.tile([P, P], U8, name="cS", tag="cS", bufs=8, align_bytes=64)
+            d["cG"] = work.tile([P, P, 4], BF16, name="cG", tag="cG", bufs=3, align_bytes=64)
+            d["cW"] = work.tile([P, P], U32, name="cW", tag="cW", bufs=3, align_bytes=64)
+            d["cS"] = work.tile([P, P], U8, name="cS", tag="cS", bufs=3, align_bytes=64)
             nc.vector.tensor_tensor(
                 out=d["cG"][:],
                 in0=d["c1"][:].rearrange("p t n -> p n t"),
@@ -324,10 +352,10 @@ def tile_i2p_crossattention_pa_kernel(tc, q, k, v, Wo, bo, feat0, out):
                 in_=d["cG"][:].rearrange("p n t -> p (n t)"),
             )
 
-        def mx2(s):
+        def mx2(s, tag="mx"):
             b, i = divmod(s, 4)
             d = st[s]
-            y = psum.tile([P, 4, P], F32, name="y", tag="y", bufs=1)
+            y = psum.tile([P, 4, P], F32, name="y", tag=tag, bufs=NB[tag])
             for ot in range(4):
                 nc.tensor.matmul_mx(
                     out=y[:, ot, :],
@@ -340,10 +368,24 @@ def tile_i2p_crossattention_pa_kernel(tc, q, k, v, Wo, bo, feat0, out):
                 )
             d["y"] = y
 
+        def final_sg(s):
+            b, i = divmod(s, 4)
+            y = st[s]["y"]
+            y_sb = work.tile([P, 4, P], F32, name="y_sb", tag="y_sb", bufs=3)
+            nc.scalar.copy(out=y_sb[:], in_=y[:])
+            o_sb = work.tile([P, 4, P], F32, name="o_sb", tag="o_sb", bufs=4)
+            nc.gpsimd.tensor_tensor(
+                out=o_sb[:], in0=y_sb[:], in1=fb[b][:, :, P * i : P * i + P], op=ALU.add
+            )
+            nc.sync.dma_start(
+                out=out[b].rearrange("(t p) n -> p t n", p=P)[:, :, P * i : P * i + P],
+                in_=o_sb[:],
+            )
+
         def final(s):
             b, i = divmod(s, 4)
             y = st[s]["y"]
-            o_sb = work.tile([P, 4, P], F32, name="o_sb", tag="o_sb", bufs=3)
+            o_sb = work.tile([P, 4, P], F32, name="o_sb", tag="o_sb", bufs=4)
             nc.vector.tensor_tensor(
                 out=o_sb[:], in0=y[:], in1=fb[b][:, :, P * i : P * i + P], op=ALU.add
             )
@@ -358,27 +400,21 @@ def tile_i2p_crossattention_pa_kernel(tc, q, k, v, Wo, bo, feat0, out):
         head = [
             k_job(0, 0, "v", "en"),
             k_job(0, 1, "s", "en"),
-            k_job(0, 2, "v", "en"),
-            k_job(0, 3, "s", "en"),
             q_job(0, 0, "v", "tp"),
-            k_job(0, 4, "s", "tp"),
-            k_job(0, 5, "v", "en"),
-            k_job(0, 6, "s", "en"),
-            k_job(0, 7, "v", "en"),
+            k_job(0, 2, "s", "tp"),
+            k_job(0, 3, "v", "en"),
         ]
         weave([], head, 0)
 
         fills = {
-            0: [q_job(0, 1, "s"), q_job(0, 2, "v"), q_job(0, 3, "s"), k_job(1, 0, "v"), k_job(1, 1, "s"), k_job(1, 2, "v"), k_job(1, 3, "s")],
-            1: [k_job(1, 4, "v"), k_job(1, 5, "s"), k_job(1, 6, "v"), k_job(1, 7, "s"), q_job(1, 0, "v")],
-            2: [q_job(1, 1), q_job(1, 2), q_job(1, 3), bo_job(), w_job(0)],
-            3: [w_job(1), w_job(2), w_job(3)],
-        };
-        caps = {0: 4, 1: 4, 2: 4, 3: 3};
-        LT = 1
-        L1 = 2
-        L2 = 3
-        vx = {(2, 2): [("rg", 0, 0)], (2, 3): [("rg", 0, 1), ("vq", 0, 0), ("vq", 0, 1)], (3, 3): [("fb", 0, 0)], (4, 2): [("rg", 1, 0)], (5, 2): [("rg", 1, 1)], (5, 3): [("vq", 1, 0), ("vq", 1, 1), ("fb", 1, 0)]}
+            0: [q_job(0, 1, "s"), k_job(1, 0, "v"), k_job(1, 1, "s"), bo_job()],
+            1: [k_job(1, 2, "v"), k_job(1, 3, "v"), q_job(1, 0, "s")],
+            2: [q_job(1, 1, "v"), w_job(0), w_job(1)],
+            3: [w_job(2), w_job(3)],
+        }
+        caps = {0: 2, 1: 3, 2: 3, 3: 3}
+        vx = {(0, 3): [("rg", 0, 0), ("rg", 0, 1)], (2, 3): [("fb", 0, 0), ("rg", 1, 0), ("rg", 1, 1), ("fb", 1, 0)], (2, 1): [("vq", 0, 0), ("vq", 0, 1)], (4, 1): [("vq", 1, 0)], (5, 1): [("vq", 1, 1)]}
+        back = {(2, 1): [("m1", 0)], (3, 1): [("m2", 0), ("m1", 1)], (4, 1): [("m2", 1), ("m1", 2)], (5, 1): [("m2", 2), ("m1", 3)], (6, 1): [("m2", 3), ("m1", 4)], (7, 1): [("m2", 4), ("m1", 5)], (3, 0): [("ctx", 0)], (4, 0): [("fin", 0), ("ctx", 1)], (5, 0): [("fin", 1), ("ctx", 2)], (6, 0): [("fin", 2), ("ctx", 3)], (7, 0): [("fin", 3), ("ctx", 4)]}
 
         def extras(s, where):
             for name, a, b2 in vx.get((s, where), []):
@@ -389,31 +425,55 @@ def tile_i2p_crossattention_pa_kernel(tc, q, k, v, Wo, bo, feat0, out):
                 elif name == "fb":
                     add_bias(a)
 
-        for s in range(NT + L2 + 2):
-            if live(s - L2 - 1):
-                final(s - L2 - 1)
-            if live(s - L1 - 1):
-                ctx_out(s - L1 - 1)
+        def hook0(s):
+            if live(s - 1):
+                rsum(s - 1)
+            extras(s, 1)
+
+        for s in range(NT):
+            for name, j in back.get((s, 0), []):
+                if name == "fin":
+                    final(j)
+                else:
+                    ctx_out(j)
             if live(s - 1):
                 exps(s - 1)
-                rsum(s - 1)
             extras(s, 0)
             fill = fills.get(s, [])
             jobs = fill
-            if live(s - LT):
-                lo0, lo1, lor = ((5, 7, 7) if s < 3 else (2, 4, 5))
-                te = te_jobs(s - LT, lo0, lo1)
-                rbj = rb_job(s - LT, lor)
-                nf = (3 if s < 3 else 1)
-                jobs = fill[0:nf] + [te[0]] + fill[nf : nf + 1] + [te[1], rbj] + fill[nf + 1 :]
-            if s < NT:
-                weave(energy_mms(s, lambda: extras(s, 1), lambda: extras(s, 2)), jobs, caps.get(s, 2))
-            else:
-                weave([], jobs, 0)
-            if live(s - LT):
-                quant_e(s - LT)
+            if live(s - 1):
+                lo0, lo1 = ((4, 6) if s < 3 else (2, 4))
+                te = te_jobs(s - 1, lo0, lo1)
+                nf = (2 if s < 3 else 1)
+                jobs = fill[0:nf] + [te[0]] + fill[nf : nf + 1] + [te[1]] + fill[nf + 1 :]
+            if live(s - 2):
+                jobs = [rb_job(s - 2, 0)] + jobs
+            weave(energy_mms(s, lambda: hook0(s), lambda: extras(s, 2)), jobs, caps.get(s, 2))
+            if live(s - 1):
+                quant_e(s - 1)
             extras(s, 3)
-            if live(s - L2):
-                mx2(s - L2)
-            if live(s - L1):
-                mx1(s - L1)
+            for name, j in back.get((s, 1), []):
+                if name == "m1":
+                    mx1(j)
+                else:
+                    mx2(j)
+
+        exps(7)
+        te = te_jobs(7, 0, 0)
+        final(4)
+        weave([], [rb_job(6, 0)], 0)
+        ctx_out(5)
+        weave([], te, 0)
+        mx1(6, "en")
+        rsum(7)
+        weave([], [rb_job(7, 0)], 0)
+        mx2(5)
+        ctx_out(6)
+        quant_e(7)
+        mx1(7, "en")
+        mx2(6, "tp")
+        final(5)
+        ctx_out(7)
+        final(6)
+        mx2(7)
+        final(7)

@@ -23,6 +23,7 @@ FLOPS = 2 * B * (N * M * C + N * M * C + N * C * C)
 
 MANUAL = True
 TE_ENG = ("s", "s")
+TE_BY = {6: ("s", "v")}
 W_ENG = "s"
 V_ENG = "g"
 NB = {"en": 3, "tp": 3, "mx": 2}
@@ -74,6 +75,9 @@ def tile_i2p_crossattention_pa_kernel(tc, q, k, v, Wo, bo, feat0, out):
             )
 
         nc.vector.memset(bo_rows[:], 0.0)
+        warm = keep.tile([P, 1], F32, name="warm")
+        nc.vector.memset(warm[:], 0.0)
+        nc.scalar.activation(out=warm[:], in_=warm[:], func=ACT.Exp, bias=0.0, scale=1.0)
         make_identity(nc, ident_b[:])
         make_identity(nc, ident_f[:])
 
@@ -284,7 +288,7 @@ def tile_i2p_crossattention_pa_kernel(tc, q, k, v, Wo, bo, feat0, out):
 
         def te_post(s, g, ps):
             d = st[s]
-            copy_on(TE_ENG[g], d["eG"][:, g, :, :], ps[:].rearrange("p t n -> p n t"))
+            copy_on(TE_BY.get(s, TE_ENG)[g], d["eG"][:, g, :, :], ps[:].rearrange("p t n -> p n t"))
 
         def quant_e(s):
             d = st[s]
@@ -401,20 +405,18 @@ def tile_i2p_crossattention_pa_kernel(tc, q, k, v, Wo, bo, feat0, out):
             k_job(0, 0, "v", "en"),
             k_job(0, 1, "s", "en"),
             q_job(0, 0, "v", "tp"),
-            k_job(0, 2, "s", "tp"),
-            k_job(0, 3, "v", "en"),
         ]
         weave([], head, 0)
 
         fills = {
-            0: [q_job(0, 1, "s"), k_job(1, 0, "v"), k_job(1, 1, "s"), bo_job()],
+            0: [k_job(0, 2, "s", due=4), k_job(0, 3, "v", due=4), q_job(0, 1, "s"), k_job(1, 0, "v"), k_job(1, 1, "s"), bo_job()],
             1: [k_job(1, 2, "v"), k_job(1, 3, "v"), q_job(1, 0, "s")],
-            2: [q_job(1, 1, "v"), w_job(0), w_job(1)],
-            3: [w_job(2), w_job(3)],
+            2: [q_job(1, 1, "v"), w_job(0), w_job(1), w_job(2)],
+            3: [w_job(3)],
         }
-        caps = {0: 2, 1: 3, 2: 3, 3: 3}
+        caps = {0: 3, 1: 3, 2: 4, 3: 3}
         vx = {(0, 3): [("rg", 0, 0), ("rg", 0, 1)], (2, 3): [("fb", 0, 0), ("rg", 1, 0), ("rg", 1, 1), ("fb", 1, 0)], (2, 1): [("vq", 0, 0), ("vq", 0, 1)], (4, 1): [("vq", 1, 0)], (5, 1): [("vq", 1, 1)]}
-        back = {(2, 1): [("m1", 0)], (3, 1): [("m2", 0), ("m1", 1)], (4, 1): [("m2", 1), ("m1", 2)], (5, 1): [("m2", 2), ("m1", 3)], (6, 1): [("m2", 3), ("m1", 4)], (7, 1): [("m2", 4), ("m1", 5)], (3, 0): [("ctx", 0)], (4, 0): [("fin", 0), ("ctx", 1)], (5, 0): [("fin", 1), ("ctx", 2)], (6, 0): [("fin", 2), ("ctx", 3)], (7, 0): [("fin", 3), ("ctx", 4)]}
+        back = {(3, 1): [("m2", 0), ("m1", 1)], (4, 1): [("m2", 1), ("m1", 2)], (5, 1): [("m2", 2), ("m1", 3)], (6, 1): [("m2", 3), ("m1", 4)], (2, 1): [("m1", 0)], (4, 0): [("fin", 0), ("ctx", 1)], (5, 0): [("fin", 1), ("ctx", 2)], (6, 0): [("fin", 2), ("ctx", 3)], (7, 0): [("fin", 3), ("ctx", 4)], (3, 0): [("ctx", 0)]}
 
         def extras(s, where):
             for name, a, b2 in vx.get((s, where), []):
@@ -441,15 +443,15 @@ def tile_i2p_crossattention_pa_kernel(tc, q, k, v, Wo, bo, feat0, out):
             extras(s, 0)
             fill = fills.get(s, [])
             jobs = fill
-            if live(s - 1):
-                lo0, lo1 = ((4, 6) if s < 3 else (2, 4))
+            if live(s - 1) and s not in (7,):
+                lo0, lo1 = (4, 6)
                 te = te_jobs(s - 1, lo0, lo1)
                 nf = (2 if s < 3 else 1)
                 jobs = fill[0:nf] + [te[0]] + fill[nf : nf + 1] + [te[1]] + fill[nf + 1 :]
-            if live(s - 2):
+            if live(s - 2) and s not in (7,):
                 jobs = [rb_job(s - 2, 0)] + jobs
             weave(energy_mms(s, lambda: hook0(s), lambda: extras(s, 2)), jobs, caps.get(s, 2))
-            if live(s - 1):
+            if live(s - 1) and s not in (7,):
                 quant_e(s - 1)
             extras(s, 3)
             for name, j in back.get((s, 1), []):
@@ -458,18 +460,23 @@ def tile_i2p_crossattention_pa_kernel(tc, q, k, v, Wo, bo, feat0, out):
                 else:
                     mx2(j)
 
+        te6 = te_jobs(6, 0, 0)
+        weave([], te6, 0)
+        mx2(4)
+        mx1(5)
         exps(7)
-        te = te_jobs(7, 0, 0)
+        weave([], [rb_job(5, 0)], 0)
+        quant_e(6)
         final(4)
-        weave([], [rb_job(6, 0)], 0)
         ctx_out(5)
-        weave([], te, 0)
+        te = te_jobs(7, 0, 0)
+        weave([], te + [rb_job(6, 0)], 0)
         mx1(6, "en")
-        rsum(7)
-        weave([], [rb_job(7, 0)], 0)
         mx2(5)
-        ctx_out(6)
+        rsum(7)
         quant_e(7)
+        weave([], [rb_job(7, 0)], 0)
+        ctx_out(6)
         mx1(7, "en")
         mx2(6, "tp")
         final(5)

@@ -25,7 +25,9 @@ MANUAL = True
 TE_ENG = ("s", "s")
 TE_BY = {6: ("s", "v")}
 W_ENG = "s"
-V_ENG = "g"
+V_ENG = ("v", "g")
+FB_ENG = ("v", "s")
+GCH = 2
 NB = {"en": 3, "tp": 3, "mx": 2}
 
 
@@ -88,15 +90,15 @@ def tile_i2p_crossattention_pa_kernel(tc, q, k, v, Wo, bo, feat0, out):
         load_k(0, 1, 0, 2)
         load_k(0, 1, 2, 4)
         load_q(0, 2, 4)
+        load_v(0, 0)
+        load_v(0, 1)
+        load_v(1, 0)
+        load_v(1, 1)
+        nc.sync.dma_start(out=w_raw[:], in_=Wo.rearrange("(t p) c -> p t c", p=P))
         load_k(1, 0)
         load_k(1, 1)
         load_q(1, 0, 4)
-        load_v(0, 0)
-        load_v(0, 1)
-        nc.sync.dma_start(out=w_raw[:], in_=Wo.rearrange("(t p) c -> p t c", p=P))
         nc.sync.dma_start(out=f_raw[0][:], in_=feat0[0].rearrange("(t p) n -> p t n", p=P))
-        load_v(1, 0)
-        load_v(1, 1)
         nc.sync.dma_start(out=f_raw[1][:], in_=feat0[1].rearrange("(t p) n -> p t n", p=P))
 
         def copy_on(eng, dst, src):
@@ -184,8 +186,25 @@ def tile_i2p_crossattention_pa_kernel(tc, q, k, v, Wo, bo, feat0, out):
         def bo_job():
             return job(1, lambda x: bo_rows[:], bo_post)
 
-        def add_bias(b):
-            for ot in range(4):
+        def add_bias(b, ot):
+            eng = FB_ENG[b]
+            if eng == "s":
+                nc.scalar.activation(
+                    out=fb[b][:, ot, :],
+                    in_=f_raw[b][:, ot, :],
+                    func=ACT.Identity,
+                    bias=bo_col[:, ot : ot + 1],
+                    scale=1.0,
+                )
+            elif eng == "v":
+                nc.vector.tensor_scalar(
+                    out=fb[b][:, ot, :],
+                    in0=f_raw[b][:, ot, :],
+                    scalar1=bo_col[:, ot : ot + 1],
+                    scalar2=None,
+                    op0=ALU.add,
+                )
+            else:
                 nc.gpsimd.tensor_scalar(
                     out=fb[b][:, ot, :],
                     in0=f_raw[b][:, ot, :],
@@ -199,16 +218,17 @@ def tile_i2p_crossattention_pa_kernel(tc, q, k, v, Wo, bo, feat0, out):
 
         def v_regroup(b, g):
             vG[(b, g)] = work.tile([P, C, 4], BF16, name="vG", tag="vG", bufs=4, align_bytes=64)
-            if V_ENG == "v":
+            if V_ENG[b] == "v":
                 nc.vector.tensor_copy(
                     out=vG[(b, g)][:].rearrange("p (c i) t -> p c t i", i=4),
                     in_=v_raw[b][:, 4 * g : 4 * g + 4, :].rearrange("p t (c i) -> p c t i", i=4),
                 )
             else:
-                for hf in range(2):
+                cw = C // GCH
+                for hf in range(GCH):
                     nc.gpsimd.tensor_scalar(
-                        out=vG[(b, g)][:, 256 * hf : 256 * hf + 256, :],
-                        in0=v_raw[b][:, 4 * g : 4 * g + 4, 256 * hf : 256 * hf + 256].rearrange("p t c -> p c t"),
+                        out=vG[(b, g)][:, cw * hf : cw * hf + cw, :],
+                        in0=v_raw[b][:, 4 * g : 4 * g + 4, cw * hf : cw * hf + cw].rearrange("p t c -> p c t"),
                         scalar1=1.0,
                         scalar2=0.0,
                         op0=ALU.mult,
@@ -409,13 +429,13 @@ def tile_i2p_crossattention_pa_kernel(tc, q, k, v, Wo, bo, feat0, out):
         weave([], head, 0)
 
         fills = {
-            0: [k_job(0, 2, "s", due=4), k_job(0, 3, "v", due=4), q_job(0, 1, "s"), k_job(1, 0, "v"), k_job(1, 1, "s"), bo_job()],
-            1: [k_job(1, 2, "v"), k_job(1, 3, "v"), q_job(1, 0, "s")],
-            2: [q_job(1, 1, "v"), w_job(0), w_job(1), w_job(2)],
-            3: [w_job(3)],
+            0: [k_job(0, 2, "s", due=4), k_job(0, 3, "v", due=4), q_job(0, 1, "s"), bo_job()],
+            2: [w_job(0), w_job(1), w_job(2), w_job(3)],
+            3: [k_job(1, 0, "s"), k_job(1, 1, "s"), k_job(1, 2, "v"), k_job(1, 3, "s"), q_job(1, 0, "v")],
+            4: [q_job(1, 1, "s")],
         }
-        caps = {0: 3, 1: 3, 2: 4, 3: 3}
-        vx = {(0, 3): [("rg", 0, 0), ("rg", 0, 1)], (2, 3): [("fb", 0, 0), ("rg", 1, 0), ("rg", 1, 1), ("fb", 1, 0)], (2, 1): [("vq", 0, 0), ("vq", 0, 1)], (4, 1): [("vq", 1, 0)], (5, 1): [("vq", 1, 1)]}
+        caps = {0: 3, 1: 2, 2: 4, 3: 4, 4: 3}
+        vx = {(0, 0): [("rg", 1, 0), ("rg", 1, 1)], (0, 1): [("rg", 0, 0)], (0, 2): [("rg", 0, 1)], (2, 1): [("vq", 0, 0), ("vq", 0, 1)], (3, 1): [("fb", 0, 0), ("fb", 0, 1)], (3, 2): [("fb", 0, 2), ("fb", 0, 3)], (4, 1): [("vq", 1, 0)], (5, 1): [("vq", 1, 1)], (4, 3): [("fb", 1, 0)], (5, 3): [("fb", 1, 1)], (6, 3): [("fb", 1, 2)], (7, 3): [("fb", 1, 3)]}
         back = {(3, 1): [("m2", 0), ("m1", 1)], (4, 1): [("m2", 1), ("m1", 2)], (5, 1): [("m2", 2), ("m1", 3)], (6, 1): [("m2", 3), ("m1", 4)], (2, 1): [("m1", 0)], (4, 0): [("fin", 0), ("ctx", 1)], (5, 0): [("fin", 1), ("ctx", 2)], (6, 0): [("fin", 2), ("ctx", 3)], (7, 0): [("fin", 3), ("ctx", 4)], (3, 0): [("ctx", 0)]}
 
         def extras(s, where):
@@ -425,7 +445,7 @@ def tile_i2p_crossattention_pa_kernel(tc, q, k, v, Wo, bo, feat0, out):
                 elif name == "vq":
                     v_quant(a, b2)
                 elif name == "fb":
-                    add_bias(a)
+                    add_bias(a, b2)
 
         def hook0(s):
             if live(s - 1):
@@ -446,7 +466,7 @@ def tile_i2p_crossattention_pa_kernel(tc, q, k, v, Wo, bo, feat0, out):
             if live(s - 1) and s not in (7,):
                 lo0, lo1 = (4, 6)
                 te = te_jobs(s - 1, lo0, lo1)
-                nf = (2 if s < 3 else 1)
+                nf = (2 if s < 4 else 1)
                 jobs = fill[0:nf] + [te[0]] + fill[nf : nf + 1] + [te[1]] + fill[nf + 1 :]
             if live(s - 2) and s not in (7,):
                 jobs = [rb_job(s - 2, 0)] + jobs

@@ -22,8 +22,7 @@ NT = 8
 FLOPS = 2 * B * (N * M * C + N * M * C + N * C * C)
 
 MANUAL = True
-TE_ENG = ("s", "s")
-TE_BY = {6: ("s", "v")}
+TE_LAST = "v"
 W_ENG = "s"
 V_ENG = ("v", "g")
 FB_ENG = ("v", "s")
@@ -49,7 +48,7 @@ def tile_i2p_crossattention_pa_kernel(tc, q, k, v, Wo, bo, feat0, out):
         bo_col = keep.tile([P, 4], F32, name="bo_col")
         ident_b = keep.tile([P, P], BF16, name="ident_b")
         ident_f = keep.tile([P, P], F32, name="ident_f")
-        kT = [keep.tile([P, 2, M], F32, name="kT%d" % b) for b in range(B)]
+        kT = [[keep.tile([P, 2, M // 2], F32, name="kT%d%d" % (b, h)) for h in range(2)] for b in range(B)]
         qT = [keep.tile([P, 2, N], F32, name="qT%d" % b) for b in range(B)]
         vW = [keep.tile([P, 2, C], U32, name="vW%d" % b, align_bytes=64) for b in range(B)]
         vS = [keep.tile([P, 2, C], U8, name="vS%d" % b, align_bytes=64) for b in range(B)]
@@ -141,8 +140,9 @@ def tile_i2p_crossattention_pa_kernel(tc, q, k, v, Wo, bo, feat0, out):
                 ops[at]["run"]()
                 at += 1
 
-        def word_job(raw, dst, a, eng, tag, due):
+        def word_job(raw, dst, a, eng, tag, due, mix=False, at=None):
             hold = []
+            c0 = 2 * P * (a if at is None else at)
 
             def run(x):
                 if not hold:
@@ -156,14 +156,16 @@ def tile_i2p_crossattention_pa_kernel(tc, q, k, v, Wo, bo, feat0, out):
                 if x == 3:
                     copy_on(
                         eng,
-                        dst[:, :, 2 * P * a : 2 * P * a + 2 * P],
-                        hold[0][:].rearrange("p u r n -> p u (r n)"),
+                        dst[:, :, c0 : c0 + 2 * P].rearrange("p u (n r) -> p u n r", r=2)
+                        if mix
+                        else dst[:, :, c0 : c0 + 2 * P].rearrange("p u (r n) -> p u r n", r=2),
+                        hold[0][:].rearrange("p u r n -> p u n r") if mix else hold[0][:],
                     )
 
             return [{"run": (lambda x=x: run(x)), "lo": 0, "due": due} for x in range(4)]
 
         def k_job(b, a, eng="s", tag="tp", due=99):
-            return word_job(k_raw[b], kT[b], a, eng, tag, due)
+            return word_job(k_raw[b], kT[b][a // 2], a, eng, tag, due, True, a % 2)
 
         def q_job(b, a, eng="s", tag="tp", due=99):
             return word_job(q_raw[b], qT[b], a, eng, tag, due)
@@ -242,7 +244,7 @@ def tile_i2p_crossattention_pa_kernel(tc, q, k, v, Wo, bo, feat0, out):
                 in_=vG[(b, g)][:].rearrange("p c t -> p (c t)"),
             )
 
-        kTb = [t[:].bitcast(BF16).rearrange("p u (m e) -> p u m e", e=2) for t in kT]
+        kTb = [[t[:].bitcast(BF16).rearrange("p u (m e) -> p u m e", e=2) for t in ts] for ts in kT]
         qTb = [t[:].bitcast(BF16).rearrange("p u (m e) -> p u m e", e=2) for t in qT]
         st = [{} for s in range(NT)]
 
@@ -250,7 +252,7 @@ def tile_i2p_crossattention_pa_kernel(tc, q, k, v, Wo, bo, feat0, out):
             b, i = divmod(s, 4)
             d = st[s]
             d["en"] = []
-            d["mx"] = work.tile([P, 2], F32, name="mx", tag="mx", bufs=4)
+            d["mx"] = work.tile([P, 1], F32, name="mx", tag="mx", bufs=4)
             d["nm"] = work.tile([P, 1], F32, name="nm", tag="nm", bufs=4)
 
             def mm(h, cc):
@@ -260,21 +262,28 @@ def tile_i2p_crossattention_pa_kernel(tc, q, k, v, Wo, bo, feat0, out):
                 nc.tensor.matmul(
                     out=d["en"][h][:],
                     lhsT=qTb[b][:, u, P * i : P * i + P, e2],
-                    rhs=kTb[b][:, u, 512 * h : 512 * h + 512, e2],
+                    rhs=kTb[b][h][:, u, :, e2],
                     start=(cc == 0),
                     stop=(cc == 3),
                 )
                 if cc == 3:
-                    nc.vector.tensor_reduce(
-                        out=d["mx"][:, h : h + 1], in_=d["en"][h][:], axis=AX.X, op=ALU.max
-                    )
-                    if h == 1:
+                    if h == 0:
                         nc.vector.tensor_reduce(
-                            out=d["nm"][:], in_=d["mx"][:], axis=AX.X, op=ALU.max, negate=True
+                            out=d["mx"][:], in_=d["en"][h][:], axis=AX.X, op=ALU.max, negate=True
+                        )
+                        hook0()
+                    else:
+                        junk = work.tile([P, 512], BF16, name="junk", tag="junk", bufs=2)
+                        nc.vector.tensor_scalar(
+                            out=junk[:],
+                            in0=d["en"][h][:],
+                            scalar1=-1.0,
+                            scalar2=d["mx"][:, 0:1],
+                            op0=ALU.mult,
+                            op1=ALU.min,
+                            accum_out=d["nm"][:],
                         )
                         hook1()
-                    else:
-                        hook0()
 
             return [(lambda h=h, cc=cc: mm(h, cc)) for h in range(2) for cc in range(4)]
 
@@ -304,11 +313,18 @@ def tile_i2p_crossattention_pa_kernel(tc, q, k, v, Wo, bo, feat0, out):
                 op0=ALU.add,
                 op1=ALU.mult,
             )
+
+        def rinv(s):
+            d = st[s]
             nc.vector.reciprocal(out=d["ri"][:], in_=d["rq"][:])
 
-        def te_post(s, g, ps):
+        def te_copy(s, eng, ps, g0, g1):
             d = st[s]
-            copy_on(TE_BY.get(s, TE_ENG)[g], d["eG"][:, g, :, :], ps[:].rearrange("p t n -> p n t"))
+            copy_on(
+                eng,
+                d["eG"][:, g0:g1, :, :],
+                ps[:, 2 * g0 : 2 * g1, :].rearrange("p (g u) n -> p g n u", u=2),
+            )
 
         def quant_e(s):
             d = st[s]
@@ -317,20 +333,27 @@ def tile_i2p_crossattention_pa_kernel(tc, q, k, v, Wo, bo, feat0, out):
             nc.vector.quantize_mx(
                 out=d["eW"][:].bitcast(FP8X4),
                 scales=d["eS"][:],
-                in_=d["eG"][:].rearrange("p g n t -> p (g n t)"),
+                in_=d["eG"][:].rearrange("p g n u -> p (g n u)").bitcast(BF16),
             )
 
-        def te_jobs(s, lo0, lo1):
+        def te_jobs(s, lo0, lo1, parts=1):
             d = st[s]
-            d["eG"] = work.tile([P, 2, P, 4], BF16, name="eG", tag="eG", bufs=3, align_bytes=64)
+            d["eG"] = work.tile([P, 2, P, 2], F32, name="eG", tag="eG", bufs=3, align_bytes=64)
+            words = d["e"][:].bitcast(F32)
+            hold = []
+
+            def run(x):
+                if x == 0 or (x == 2 and parts == 2):
+                    hold.append(psum.tile([P, 4, P], F32, name="tes", tag="tp", bufs=NB["tp"]))
+                nc.tensor.transpose(hold[-1][:, x, :], words[:, P * x : P * x + P], ident_f[:])
+                if parts == 2 and x == 1:
+                    te_copy(s, "s", hold[-1], 0, 1)
+                elif x == 3:
+                    te_copy(s, TE_LAST if parts == 2 else "s", hold[-1], 0 if parts == 1 else 1, 2)
+
             return [
-                job(
-                    4,
-                    (lambda t, g=g: d["e"][:, P * (4 * g + t) : P * (4 * g + t) + P]),
-                    (lambda ps, g=g: te_post(s, g, ps)),
-                    lo=(lo0 if g == 0 else lo1),
-                )
-                for g in range(2)
+                [{"run": (lambda x=x: run(x)), "lo": (lo0 if x < 2 else lo1), "due": 99} for x in xs]
+                for xs in ((0, 1), (2, 3))
             ]
 
         def spread_rinv(s):
@@ -370,6 +393,9 @@ def tile_i2p_crossattention_pa_kernel(tc, q, k, v, Wo, bo, feat0, out):
                 in1=d["rb"][:].unsqueeze(2).to_broadcast([P, P, 4]),
                 op=ALU.mult,
             )
+
+        def ctx_quant(s):
+            d = st[s]
             nc.vector.quantize_mx(
                 out=d["cW"][:].bitcast(FP8X4),
                 scales=d["cS"][:],
@@ -448,9 +474,17 @@ def tile_i2p_crossattention_pa_kernel(tc, q, k, v, Wo, bo, feat0, out):
                     add_bias(a, b2)
 
         def hook0(s):
+            for name, j in back.get((s, 0), []):
+                if name == "ctx":
+                    ctx_quant(j)
             if live(s - 1):
                 rsum(s - 1)
             extras(s, 1)
+
+        def hook1(s):
+            if live(s - 1):
+                rinv(s - 1)
+            extras(s, 2)
 
         for s in range(NT):
             for name, j in back.get((s, 0), []):
@@ -470,7 +504,7 @@ def tile_i2p_crossattention_pa_kernel(tc, q, k, v, Wo, bo, feat0, out):
                 jobs = fill[0:nf] + [te[0]] + fill[nf : nf + 1] + [te[1]] + fill[nf + 1 :]
             if live(s - 2) and s not in (7,):
                 jobs = [rb_job(s - 2, 0)] + jobs
-            weave(energy_mms(s, lambda: hook0(s), lambda: extras(s, 2)), jobs, caps.get(s, 2))
+            weave(energy_mms(s, lambda: hook0(s), lambda: hook1(s)), jobs, caps.get(s, 2))
             if live(s - 1) and s not in (7,):
                 quant_e(s - 1)
             extras(s, 3)
@@ -480,27 +514,31 @@ def tile_i2p_crossattention_pa_kernel(tc, q, k, v, Wo, bo, feat0, out):
                 else:
                     mx2(j)
 
-        te6 = te_jobs(6, 0, 0)
+        te6 = te_jobs(6, 0, 0, 2)
         weave([], te6, 0)
         mx2(4)
         mx1(5)
         exps(7)
         weave([], [rb_job(5, 0)], 0)
         quant_e(6)
-        final(4)
         ctx_out(5)
-        te = te_jobs(7, 0, 0)
+        final(4)
+        ctx_quant(5)
+        rsum(7)
+        te = te_jobs(7, 0, 0, 2)
         weave([], te + [rb_job(6, 0)], 0)
         mx1(6, "en")
         mx2(5)
-        rsum(7)
-        quant_e(7)
-        weave([], [rb_job(7, 0)], 0)
+        rinv(7)
         ctx_out(6)
+        quant_e(7)
+        ctx_quant(6)
+        weave([], [rb_job(7, 0)], 0)
         mx1(7, "en")
         mx2(6, "tp")
         final(5)
         ctx_out(7)
         final(6)
+        ctx_quant(7)
         mx2(7)
         final(7)

@@ -21,20 +21,13 @@ M = 1024
 NT = 8
 FLOPS = 2 * B * (N * M * C + N * M * C + N * C * C)
 
-MANUAL = True
-TE_LAST = "v"
-W_ENG = "s"
-V_ENG = ("v", "g")
-FB_ENG = ("v", "s")
-GCH = 2
 NB = {"en": 3, "tp": 3, "mx": 2}
 
 
 def tile_i2p_crossattention_pa_kernel(tc, q, k, v, Wo, bo, feat0, out):
     nc = tc.nc
     with ExitStack() as ctx:
-        if MANUAL:
-            ctx.enter_context(tc.manual_schedule())
+        ctx.enter_context(tc.manual_schedule())
         keep = ctx.enter_context(tc.tile_pool(name="keep", bufs=1))
         work = ctx.enter_context(tc.tile_pool(name="work", bufs=2))
         psum = ctx.enter_context(tc.psum_pool(name="psum", bufs=1))
@@ -106,128 +99,83 @@ def tile_i2p_crossattention_pa_kernel(tc, q, k, v, Wo, bo, feat0, out):
             else:
                 nc.vector.tensor_copy(out=dst, in_=src)
 
-        def job(count, src_of, post, tag="tp", lo=0, due=99):
+        def word_job(raw, dst, r0, rows, eng, tag, c0, mix):
             hold = []
-
-            def one(x):
-                if not hold:
-                    hold.append(
-                        psum.tile([P, 4, P], BF16, name="tps", tag=tag, bufs=NB[tag])
-                    )
-                nc.tensor.transpose(hold[0][:, x, :], src_of(x), ident_b[:])
-
-            def run(x):
-                one(x)
-                if x == count - 1:
-                    post(hold[0])
-
-            return [{"run": (lambda x=x: run(x)), "lo": lo, "due": due} for x in range(count)]
-
-        def weave(mms, jobs, cap):
-            ops = sum(jobs, [])
-            at = 0
-            for m, mm in enumerate(mms):
-                while any(o["due"] <= m for o in ops[at:]):
-                    ops[at]["run"]()
-                    at += 1
-                mm()
-                budget = cap
-                while budget > 0 and at < len(ops) and ops[at]["lo"] <= m:
-                    ops[at]["run"]()
-                    at += 1
-                    budget -= 1
-            while at < len(ops):
-                ops[at]["run"]()
-                at += 1
-
-        def word_job(raw, dst, a, eng, tag, due, mix=False, at=None):
-            hold = []
-            c0 = 2 * P * (a if at is None else at)
 
             def run(x):
                 if not hold:
-                    hold.append(psum.tile([P, 2, 2, P], F32, name="wps", tag=tag, bufs=NB[tag]))
-                u, r = divmod(x, 2)
+                    hold.append(psum.tile([P, 2, rows, P], F32, name="wps", tag=tag, bufs=NB[tag]))
+                u, r = divmod(x, rows)
                 nc.tensor.transpose(
                     hold[0][:, u, r, :],
-                    raw[:, 2 * a + r, :].bitcast(F32)[:, P * u : P * u + P],
+                    raw[:, r0 + r, :].bitcast(F32)[:, P * u : P * u + P],
                     ident_f[:],
                 )
-                if x == 3:
-                    copy_on(
-                        eng,
-                        dst[:, :, c0 : c0 + 2 * P].rearrange("p u (n r) -> p u n r", r=2)
-                        if mix
-                        else dst[:, :, c0 : c0 + 2 * P].rearrange("p u (r n) -> p u r n", r=2),
-                        hold[0][:].rearrange("p u r n -> p u n r") if mix else hold[0][:],
-                    )
+                if x == 2 * rows - 1:
+                    cols = dst[:, :, c0 : c0 + rows * P]
+                    if mix:
+                        copy_on(
+                            eng,
+                            cols.rearrange("p u (n r) -> p u n r", r=rows),
+                            hold[0][:].rearrange("p u r n -> p u n r"),
+                        )
+                    else:
+                        copy_on(eng, cols, hold[0][:].rearrange("p u r n -> p u (r n)"))
 
-            return [{"run": (lambda x=x: run(x)), "lo": 0, "due": due} for x in range(4)]
+            return [(lambda x=x: run(x)) for x in range(2 * rows)]
 
-        def k_job(b, a, eng="s", tag="tp", due=99):
-            return word_job(k_raw[b], kT[b][a // 2], a, eng, tag, due, True, a % 2)
+        def k_job(b, a, eng="s", tag="tp"):
+            return word_job(k_raw[b], kT[b][a // 2], 2 * a, 2, eng, tag, 2 * P * (a % 2), True)
 
-        def q_job(b, a, eng="s", tag="tp", due=99):
-            return word_job(q_raw[b], qT[b], a, eng, tag, due)
-
-        def w_post(ot, ps):
-            copy_on(W_ENG, wG[:, ot, :, :], ps[:].rearrange("p t o -> p o t"))
-            if ot == 3:
-                nc.vector.quantize_mx(
-                    out=wW[:].bitcast(FP8X4),
-                    scales=wS[:],
-                    in_=wG[:].rearrange("p a o t -> p (a o t)"),
-                )
+        def q_job(b, r0, rows, eng="s", tag="tp"):
+            return word_job(q_raw[b], qT[b], r0, rows, eng, tag, P * r0, False)
 
         def w_job(ot):
-            return job(4, lambda t: w_raw[:, ot, P * t : P * t + P], lambda ps: w_post(ot, ps))
+            hold = []
 
-        def bo_post(ps):
-            nc.vector.tensor_copy(out=bo_col[:], in_=ps[:, 0, 0:4])
+            def run(t):
+                if not hold:
+                    hold.append(psum.tile([P, 4, P], BF16, name="tps", tag="tp", bufs=NB["tp"]))
+                nc.tensor.transpose(hold[0][:, t, :], w_raw[:, ot, P * t : P * t + P], ident_b[:])
+                if t == 3:
+                    nc.scalar.copy(out=wG[:, ot, :, :], in_=hold[0][:].rearrange("p t o -> p o t"))
+
+            return [(lambda t=t: run(t)) for t in range(4)]
+
+        def w_quant():
+            nc.vector.quantize_mx(
+                out=wW[:].bitcast(FP8X4),
+                scales=wS[:],
+                in_=wG[:].rearrange("p a o t -> p (a o t)"),
+            )
 
         def bo_job():
-            return job(1, lambda x: bo_rows[:], bo_post)
+            ps = psum.tile([P, 4, P], BF16, name="tps", tag="tp", bufs=NB["tp"])
+            nc.tensor.transpose(ps[:, 0, :], bo_rows[:], ident_b[:])
+            nc.vector.tensor_copy(out=bo_col[:], in_=ps[:, 0, 0:4])
 
         def add_bias(b, ot):
-            eng = FB_ENG[b]
-            if eng == "s":
-                nc.scalar.activation(
-                    out=fb[b][:, ot, :],
-                    in_=f_raw[b][:, ot, :],
-                    func=ACT.Identity,
-                    bias=bo_col[:, ot : ot + 1],
-                    scale=1.0,
-                )
-            elif eng == "v":
-                nc.vector.tensor_scalar(
-                    out=fb[b][:, ot, :],
-                    in0=f_raw[b][:, ot, :],
-                    scalar1=bo_col[:, ot : ot + 1],
-                    scalar2=None,
-                    op0=ALU.add,
-                )
-            else:
-                nc.gpsimd.tensor_scalar(
-                    out=fb[b][:, ot, :],
-                    in0=f_raw[b][:, ot, :],
-                    scalar1=1.0,
-                    scalar2=bo_col[:, ot : ot + 1],
-                    op0=ALU.mult,
-                    op1=ALU.add,
-                )
+            nc.gpsimd.tensor_scalar(
+                out=fb[b][:, ot, :],
+                in0=f_raw[b][:, ot, :],
+                scalar1=1.0,
+                scalar2=bo_col[:, ot : ot + 1],
+                op0=ALU.mult,
+                op1=ALU.add,
+            )
 
         vG = {}
 
-        def v_regroup(b, g):
+        def v_regroup(b, g, eng):
             vG[(b, g)] = work.tile([P, C, 4], BF16, name="vG", tag="vG", bufs=4, align_bytes=64)
-            if V_ENG[b] == "v":
+            if eng == "v":
                 nc.vector.tensor_copy(
                     out=vG[(b, g)][:].rearrange("p (c i) t -> p c t i", i=4),
                     in_=v_raw[b][:, 4 * g : 4 * g + 4, :].rearrange("p t (c i) -> p c t i", i=4),
                 )
             else:
-                cw = C // GCH
-                for hf in range(GCH):
+                cw = C // 2
+                for hf in range(2):
                     nc.gpsimd.tensor_scalar(
                         out=vG[(b, g)][:, cw * hf : cw * hf + cw, :],
                         in0=v_raw[b][:, 4 * g : 4 * g + 4, cw * hf : cw * hf + cw].rearrange("p t c -> p c t"),
@@ -248,44 +196,41 @@ def tile_i2p_crossattention_pa_kernel(tc, q, k, v, Wo, bo, feat0, out):
         qTb = [t[:].bitcast(BF16).rearrange("p u (m e) -> p u m e", e=2) for t in qT]
         st = [{} for s in range(NT)]
 
-        def energy_mms(s, hook0, hook1):
+        def energy(s, h, cc):
             b, i = divmod(s, 4)
             d = st[s]
-            d["en"] = []
+            if cc == 0:
+                tag = "mx" if (s, h) == (1, 1) else "en"
+                d["en%d" % h] = psum.tile([P, 512], F32, name="en", tag=tag, bufs=NB[tag])
+            u, e2 = divmod(cc, 2)
+            nc.tensor.matmul(
+                out=d["en%d" % h][:],
+                lhsT=qTb[b][:, u, P * i : P * i + P, e2],
+                rhs=kTb[b][h][:, u, :, e2],
+                start=(cc == 0),
+                stop=(cc == 3),
+            )
+
+        def max0(s):
+            d = st[s]
             d["mx"] = work.tile([P, 1], F32, name="mx", tag="mx", bufs=4)
+            nc.vector.tensor_reduce(
+                out=d["mx"][:], in_=d["en0"][:], axis=AX.X, op=ALU.max, negate=True
+            )
+
+        def max1(s):
+            d = st[s]
             d["nm"] = work.tile([P, 1], F32, name="nm", tag="nm", bufs=4)
-
-            def mm(h, cc):
-                if cc == 0:
-                    d["en"].append(psum.tile([P, 512], F32, name="en", tag="en", bufs=NB["en"]))
-                u, e2 = divmod(cc, 2)
-                nc.tensor.matmul(
-                    out=d["en"][h][:],
-                    lhsT=qTb[b][:, u, P * i : P * i + P, e2],
-                    rhs=kTb[b][h][:, u, :, e2],
-                    start=(cc == 0),
-                    stop=(cc == 3),
-                )
-                if cc == 3:
-                    if h == 0:
-                        nc.vector.tensor_reduce(
-                            out=d["mx"][:], in_=d["en"][h][:], axis=AX.X, op=ALU.max, negate=True
-                        )
-                        hook0()
-                    else:
-                        junk = work.tile([P, 512], BF16, name="junk", tag="junk", bufs=2)
-                        nc.vector.tensor_scalar(
-                            out=junk[:],
-                            in0=d["en"][h][:],
-                            scalar1=-1.0,
-                            scalar2=d["mx"][:, 0:1],
-                            op0=ALU.mult,
-                            op1=ALU.min,
-                            accum_out=d["nm"][:],
-                        )
-                        hook1()
-
-            return [(lambda h=h, cc=cc: mm(h, cc)) for h in range(2) for cc in range(4)]
+            junk = work.tile([P, 512], BF16, name="junk", tag="junk", bufs=2)
+            nc.vector.tensor_scalar(
+                out=junk[:],
+                in0=d["en1"][:],
+                scalar1=-1.0,
+                scalar2=d["mx"][:, 0:1],
+                op0=ALU.mult,
+                op1=ALU.min,
+                accum_out=d["nm"][:],
+            )
 
         def exps(s):
             d = st[s]
@@ -294,7 +239,7 @@ def tile_i2p_crossattention_pa_kernel(tc, q, k, v, Wo, bo, feat0, out):
             for h in range(2):
                 nc.scalar.activation(
                     out=d["e"][:, 512 * h : 512 * h + 512],
-                    in_=d["en"][h][:],
+                    in_=d["en%d" % h][:],
                     func=ACT.Exp,
                     bias=d["nm"][:, 0:1],
                     scale=1.0,
@@ -318,12 +263,21 @@ def tile_i2p_crossattention_pa_kernel(tc, q, k, v, Wo, bo, feat0, out):
             d = st[s]
             nc.vector.reciprocal(out=d["ri"][:], in_=d["rq"][:])
 
-        def te_copy(s, eng, ps, g0, g1):
+        def te_tile(s):
             d = st[s]
+            d["eG"] = work.tile([P, 2, P, 2], F32, name="eG", tag="eG", bufs=3, align_bytes=64)
+
+        def te_half(s, g, ps, at):
+            words = st[s]["e"][:].bitcast(F32)
+            for u in range(2):
+                w = P * (2 * g + u)
+                nc.tensor.transpose(ps[:, at + u, :], words[:, w : w + P], ident_f[:])
+
+        def te_copy(s, eng, ps, g0, g1):
             copy_on(
                 eng,
-                d["eG"][:, g0:g1, :, :],
-                ps[:, 2 * g0 : 2 * g1, :].rearrange("p (g u) n -> p g n u", u=2),
+                st[s]["eG"][:, g0:g1, :, :],
+                ps.rearrange("p (g u) n -> p g n u", u=2),
             )
 
         def quant_e(s):
@@ -336,26 +290,6 @@ def tile_i2p_crossattention_pa_kernel(tc, q, k, v, Wo, bo, feat0, out):
                 in_=d["eG"][:].rearrange("p g n u -> p (g n u)").bitcast(BF16),
             )
 
-        def te_jobs(s, lo0, lo1, parts=1):
-            d = st[s]
-            d["eG"] = work.tile([P, 2, P, 2], F32, name="eG", tag="eG", bufs=3, align_bytes=64)
-            words = d["e"][:].bitcast(F32)
-            hold = []
-
-            def run(x):
-                if x == 0 or (x == 2 and parts == 2):
-                    hold.append(psum.tile([P, 4, P], F32, name="tes", tag="tp", bufs=NB["tp"]))
-                nc.tensor.transpose(hold[-1][:, x, :], words[:, P * x : P * x + P], ident_f[:])
-                if parts == 2 and x == 1:
-                    te_copy(s, "s", hold[-1], 0, 1)
-                elif x == 3:
-                    te_copy(s, TE_LAST if parts == 2 else "s", hold[-1], 0 if parts == 1 else 1, 2)
-
-            return [
-                [{"run": (lambda x=x: run(x)), "lo": (lo0 if x < 2 else lo1), "due": 99} for x in xs]
-                for xs in ((0, 1), (2, 3))
-            ]
-
         def spread_rinv(s):
             d = st[s]
             rbp = psum.tile([P, P], F32, name="rbp", tag="tp", bufs=NB["tp"])
@@ -363,13 +297,10 @@ def tile_i2p_crossattention_pa_kernel(tc, q, k, v, Wo, bo, feat0, out):
             d["rb"] = work.tile([P, P], F32, name="rb", tag="rb", bufs=4)
             nc.scalar.copy(out=d["rb"][:], in_=rbp[:])
 
-        def rb_job(s, lo):
-            return [{"run": (lambda: spread_rinv(s)), "lo": lo, "due": 99}]
-
-        def mx1(s, tag="mx"):
+        def mx1(s):
             b = s // 4
             d = st[s]
-            d["c1"] = psum.tile([P, 4, P], F32, name="c1", tag=tag, bufs=NB[tag])
+            d["c1"] = psum.tile([P, 4, P], F32, name="c1", tag="mx", bufs=NB["mx"])
             for t in range(4):
                 for g in range(2):
                     nc.tensor.matmul_mx(
@@ -385,8 +316,6 @@ def tile_i2p_crossattention_pa_kernel(tc, q, k, v, Wo, bo, feat0, out):
         def ctx_out(s):
             d = st[s]
             d["cG"] = work.tile([P, P, 4], BF16, name="cG", tag="cG", bufs=3, align_bytes=64)
-            d["cW"] = work.tile([P, P], U32, name="cW", tag="cW", bufs=3, align_bytes=64)
-            d["cS"] = work.tile([P, P], U8, name="cS", tag="cS", bufs=3, align_bytes=64)
             nc.vector.tensor_tensor(
                 out=d["cG"][:],
                 in0=d["c1"][:].rearrange("p t n -> p n t"),
@@ -396,19 +325,20 @@ def tile_i2p_crossattention_pa_kernel(tc, q, k, v, Wo, bo, feat0, out):
 
         def ctx_quant(s):
             d = st[s]
+            d["cW"] = work.tile([P, P], U32, name="cW", tag="cW", bufs=3, align_bytes=64)
+            d["cS"] = work.tile([P, P], U8, name="cS", tag="cS", bufs=3, align_bytes=64)
             nc.vector.quantize_mx(
                 out=d["cW"][:].bitcast(FP8X4),
                 scales=d["cS"][:],
                 in_=d["cG"][:].rearrange("p n t -> p (n t)"),
             )
 
-        def mx2(s, tag="mx"):
-            b, i = divmod(s, 4)
+        def mx2(s):
             d = st[s]
-            y = psum.tile([P, 4, P], F32, name="y", tag=tag, bufs=NB[tag])
+            d["y"] = psum.tile([P, 4, P], F32, name="y", tag="mx", bufs=NB["mx"])
             for ot in range(4):
                 nc.tensor.matmul_mx(
-                    out=y[:, ot, :],
+                    out=d["y"][:, ot, :],
                     lhsT=wW[:, P * ot : P * ot + P].bitcast(FP8X4),
                     lhsT_scale=wS[:, P * ot : P * ot + P],
                     rhs=d["cW"][:].bitcast(FP8X4),
@@ -416,28 +346,12 @@ def tile_i2p_crossattention_pa_kernel(tc, q, k, v, Wo, bo, feat0, out):
                     start=True,
                     stop=True,
                 )
-            d["y"] = y
-
-        def final_sg(s):
-            b, i = divmod(s, 4)
-            y = st[s]["y"]
-            y_sb = work.tile([P, 4, P], F32, name="y_sb", tag="y_sb", bufs=3)
-            nc.scalar.copy(out=y_sb[:], in_=y[:])
-            o_sb = work.tile([P, 4, P], F32, name="o_sb", tag="o_sb", bufs=4)
-            nc.gpsimd.tensor_tensor(
-                out=o_sb[:], in0=y_sb[:], in1=fb[b][:, :, P * i : P * i + P], op=ALU.add
-            )
-            nc.sync.dma_start(
-                out=out[b].rearrange("(t p) n -> p t n", p=P)[:, :, P * i : P * i + P],
-                in_=o_sb[:],
-            )
 
         def final(s):
             b, i = divmod(s, 4)
-            y = st[s]["y"]
             o_sb = work.tile([P, 4, P], F32, name="o_sb", tag="o_sb", bufs=4)
             nc.vector.tensor_tensor(
-                out=o_sb[:], in0=y[:], in1=fb[b][:, :, P * i : P * i + P], op=ALU.add
+                out=o_sb[:], in0=st[s]["y"][:], in1=fb[b][:, :, P * i : P * i + P], op=ALU.add
             )
             nc.sync.dma_start(
                 out=out[b].rearrange("(t p) n -> p t n", p=P)[:, :, P * i : P * i + P],
@@ -447,98 +361,93 @@ def tile_i2p_crossattention_pa_kernel(tc, q, k, v, Wo, bo, feat0, out):
         def live(x):
             return 0 <= x < NT
 
-        head = [
-            k_job(0, 0, "v", "en"),
-            k_job(0, 1, "s", "en"),
-            q_job(0, 0, "v", "tp"),
-        ]
-        weave([], head, 0)
+        for op in k_job(0, 0, "v", "en") + k_job(0, 1, "s", "en") + q_job(0, 0, 2, "v"):
+            op()
 
+        def at(s, place):
+            for call in singles.get((s, place), []):
+                call()
+
+        k02, k03, q02 = k_job(0, 2, "s"), k_job(0, 3, "v"), q_job(0, 2, 2)
+        w0, w1, w2, w3 = [w_job(ot) for ot in range(4)]
+        k10, k11, k12, k13 = [k_job(1, a) for a in range(4)]
+        q10, q12 = q_job(1, 0, 2), q_job(1, 2, 2)
         fills = {
-            0: [k_job(0, 2, "s", due=4), k_job(0, 3, "v", due=4), q_job(0, 1, "s"), bo_job()],
-            2: [w_job(0), w_job(1), w_job(2), w_job(3)],
-            3: [k_job(1, 0, "s"), k_job(1, 1, "s"), k_job(1, 2, "v"), k_job(1, 3, "s"), q_job(1, 0, "v")],
-            4: [q_job(1, 1, "s")],
+            (0, 0): k02, (0, 1): k03, (0, 5): q02[0:2], (0, 6): q02[2:4], (0, 7): [bo_job],
+            (1, 4): w0, (1, 5): w1, (1, 6): w2, (1, 7): w3,
+            (2, 0): k10, (2, 2): k11, (2, 6): k12,
+            (3, 0): k13, (3, 2): q10, (3, 6): q12,
         }
-        caps = {0: 3, 1: 2, 2: 4, 3: 4, 4: 3}
-        vx = {(0, 0): [("rg", 1, 0), ("rg", 1, 1)], (0, 1): [("rg", 0, 0)], (0, 2): [("rg", 0, 1)], (2, 1): [("vq", 0, 0), ("vq", 0, 1)], (3, 1): [("fb", 0, 0), ("fb", 0, 1)], (3, 2): [("fb", 0, 2), ("fb", 0, 3)], (4, 1): [("vq", 1, 0)], (5, 1): [("vq", 1, 1)], (4, 3): [("fb", 1, 0)], (5, 3): [("fb", 1, 1)], (6, 3): [("fb", 1, 2)], (7, 3): [("fb", 1, 3)]}
-        back = {(3, 1): [("m2", 0), ("m1", 1)], (4, 1): [("m2", 1), ("m1", 2)], (5, 1): [("m2", 2), ("m1", 3)], (6, 1): [("m2", 3), ("m1", 4)], (2, 1): [("m1", 0)], (4, 0): [("fin", 0), ("ctx", 1)], (5, 0): [("fin", 1), ("ctx", 2)], (6, 0): [("fin", 2), ("ctx", 3)], (7, 0): [("fin", 3), ("ctx", 4)], (3, 0): [("ctx", 0)]}
-
-        def extras(s, where):
-            for name, a, b2 in vx.get((s, where), []):
-                if name == "rg":
-                    v_regroup(a, b2)
-                elif name == "vq":
-                    v_quant(a, b2)
-                elif name == "fb":
-                    add_bias(a, b2)
-
-        def hook0(s):
-            for name, j in back.get((s, 0), []):
-                if name == "ctx":
-                    ctx_quant(j)
-            if live(s - 1):
-                rsum(s - 1)
-            extras(s, 1)
-
-        def hook1(s):
-            if live(s - 1):
-                rinv(s - 1)
-            extras(s, 2)
+        singles = {
+            (0, 0): [lambda: v_regroup(1, 0, "g"), lambda: v_regroup(1, 1, "g")],
+            (0, 1): [lambda: v_regroup(0, 0, "v")],
+            (0, 2): [lambda: v_regroup(0, 1, "v")] + [lambda b=b, ot=ot: add_bias(b, ot) for b in range(B) for ot in range(4)],
+            (1, 1): [lambda: v_quant(0, 0)],
+            (1, 2): [lambda: v_quant(0, 1)],
+            (2, 2): [w_quant],
+            (3, 1): [lambda: v_quant(1, 0)],
+            (4, 1): [lambda: v_quant(1, 1)],
+        }
 
         for s in range(NT):
-            for name, j in back.get((s, 0), []):
-                if name == "fin":
-                    final(j)
-                else:
-                    ctx_out(j)
             if live(s - 1):
                 exps(s - 1)
-            extras(s, 0)
-            fill = fills.get(s, [])
-            jobs = fill
-            if live(s - 1) and s not in (7,):
-                lo0, lo1 = (4, 6)
-                te = te_jobs(s - 1, lo0, lo1)
-                nf = (2 if s < 4 else 1)
-                jobs = fill[0:nf] + [te[0]] + fill[nf : nf + 1] + [te[1]] + fill[nf + 1 :]
-            if live(s - 2) and s not in (7,):
-                jobs = [rb_job(s - 2, 0)] + jobs
-            weave(energy_mms(s, lambda: hook0(s), lambda: hook1(s)), jobs, caps.get(s, 2))
-            if live(s - 1) and s not in (7,):
+                te_tile(s - 1)
+            at(s, 0)
+            for x in range(8):
+                energy(s, x // 4, x % 4)
+                if x == 1 and live(s - 2):
+                    spread_rinv(s - 2)
+                if x in (4, 5) and live(s - 1):
+                    if x == 4:
+                        te_bank = psum.tile([P, 4, P], F32, name="tes", tag="tp", bufs=NB["tp"])
+                    te_half(s - 1, x - 4, te_bank, 2 * x - 8)
+                    if x == 5:
+                        te_copy(s - 1, "s", te_bank[:], 0, 2)
+                for op in fills.get((s, x), []):
+                    op()
+                if x == 3:
+                    if live(s - 3):
+                        mx2(s - 3)
+                    if live(s - 2):
+                        mx1(s - 2)
+                    max0(s)
+                    if live(s - 3):
+                        final(s - 3)
+                    if live(s - 1):
+                        rsum(s - 1)
+                    if live(s - 2):
+                        ctx_out(s - 2)
+                    if live(s - 1):
+                        rinv(s - 1)
+                    if live(s - 2):
+                        ctx_quant(s - 2)
+                    at(s, 1)
+            max1(s)
+            if live(s - 1):
                 quant_e(s - 1)
-            extras(s, 3)
-            for name, j in back.get((s, 1), []):
-                if name == "m1":
-                    mx1(j)
-                else:
-                    mx2(j)
+            at(s, 2)
 
-        te6 = te_jobs(6, 0, 0, 2)
-        weave([], te6, 0)
-        mx2(4)
-        mx1(5)
         exps(7)
-        weave([], [rb_job(5, 0)], 0)
-        quant_e(6)
-        ctx_out(5)
-        final(4)
-        ctx_quant(5)
-        rsum(7)
-        te = te_jobs(7, 0, 0, 2)
-        weave([], te + [rb_job(6, 0)], 0)
-        mx1(6, "en")
+        te_tile(7)
+        spread_rinv(6)
         mx2(5)
-        rinv(7)
-        ctx_out(6)
-        quant_e(7)
-        ctx_quant(6)
-        weave([], [rb_job(7, 0)], 0)
-        mx1(7, "en")
-        mx2(6, "tp")
+        mx1(6)
         final(5)
+        for g in range(2):
+            te_bank = psum.tile([P, 2, P], F32, name="tel", tag="tp", bufs=NB["tp"])
+            te_half(7, g, te_bank, 0)
+            te_copy(7, "vs"[g], te_bank[:], g, g + 1)
+        ctx_out(6)
+        rsum(7)
+        ctx_quant(6)
+        rinv(7)
+        quant_e(7)
+        spread_rinv(7)
+        mx1(7)
+        mx2(6)
         ctx_out(7)
-        final(6)
         ctx_quant(7)
+        final(6)
         mx2(7)
         final(7)

@@ -76,12 +76,12 @@ def tile_i2p_crossattention_pa_kernel(tc, q, k, v, Wo, bo, feat0, out):
         make_identity(nc, ident_f[:])
 
         nc.scalar.dma_start(out=bo_rows[0:4, :], in_=bo.rearrange("(t p) -> t p", p=P))
+        load_q(0, 0, 1)
         load_k(0, 0, 0, 2)
         load_k(0, 0, 2, 4)
-        load_q(0, 0, 2)
         load_k(0, 1, 0, 2)
         load_k(0, 1, 2, 4)
-        load_q(0, 2, 4)
+        load_q(0, 1, 4)
         load_v(0, 0)
         load_v(0, 1)
         load_v(1, 0)
@@ -130,7 +130,7 @@ def tile_i2p_crossattention_pa_kernel(tc, q, k, v, Wo, bo, feat0, out):
         def q_job(b, r0, rows, eng="s", tag="tp"):
             return word_job(q_raw[b], qT[b], r0, rows, eng, tag, P * r0, False)
 
-        def w_job(ot):
+        def w_job(ot, eng="s"):
             hold = []
 
             def run(t):
@@ -138,7 +138,7 @@ def tile_i2p_crossattention_pa_kernel(tc, q, k, v, Wo, bo, feat0, out):
                     hold.append(psum.tile([P, 4, P], BF16, name="tps", tag="tp", bufs=NB["tp"]))
                 nc.tensor.transpose(hold[0][:, t, :], w_raw[:, ot, P * t : P * t + P], ident_b[:])
                 if t == 3:
-                    nc.scalar.copy(out=wG[:, ot, :, :], in_=hold[0][:].rearrange("p t o -> p o t"))
+                    copy_on(eng, wG[:, ot, :, :], hold[0][:].rearrange("p t o -> p o t"))
 
             return [(lambda t=t: run(t)) for t in range(4)]
 
@@ -155,14 +155,22 @@ def tile_i2p_crossattention_pa_kernel(tc, q, k, v, Wo, bo, feat0, out):
             nc.vector.tensor_copy(out=bo_col[:], in_=ps[:, 0, 0:4])
 
         def add_bias(b, ot):
-            nc.gpsimd.tensor_scalar(
-                out=fb[b][:, ot, :],
-                in0=f_raw[b][:, ot, :],
-                scalar1=1.0,
-                scalar2=bo_col[:, ot : ot + 1],
-                op0=ALU.mult,
-                op1=ALU.add,
-            )
+            if b == 0:
+                nc.vector.tensor_scalar(
+                    out=fb[b][:, ot, :],
+                    in0=f_raw[b][:, ot, :],
+                    scalar1=bo_col[:, ot : ot + 1],
+                    scalar2=None,
+                    op0=ALU.add,
+                )
+            else:
+                nc.scalar.activation(
+                    out=fb[b][:, ot, :],
+                    in_=f_raw[b][:, ot, :],
+                    func=ACT.Identity,
+                    bias=bo_col[:, ot : ot + 1],
+                    scale=1.0,
+                )
 
         vG = {}
 
@@ -200,13 +208,24 @@ def tile_i2p_crossattention_pa_kernel(tc, q, k, v, Wo, bo, feat0, out):
             b, i = divmod(s, 4)
             d = st[s]
             if cc == 0:
-                tag = "mx" if (s, h) == (1, 1) else "en"
+                tag = {(1, 1): "mx", (7, 1): "tp"}.get((s, h), "en")
                 d["en%d" % h] = psum.tile([P, 512], F32, name="en", tag=tag, bufs=NB[tag])
             u, e2 = divmod(cc, 2)
             nc.tensor.matmul(
                 out=d["en%d" % h][:],
                 lhsT=qTb[b][:, u, P * i : P * i + P, e2],
                 rhs=kTb[b][h][:, u, :, e2],
+                start=(cc == 0),
+                stop=(cc == 3),
+            )
+
+        def energy_quarter(s, w, cc):
+            b, i = divmod(s, 4)
+            u, e2 = divmod(cc, 2)
+            nc.tensor.matmul(
+                out=st[s]["en0"][:, 256 * w : 256 * w + 256],
+                lhsT=qTb[b][:, u, P * i : P * i + P, e2],
+                rhs=kTb[b][0][:, u, 256 * w : 256 * w + 256, e2],
                 start=(cc == 0),
                 stop=(cc == 3),
             )
@@ -297,10 +316,10 @@ def tile_i2p_crossattention_pa_kernel(tc, q, k, v, Wo, bo, feat0, out):
             d["rb"] = work.tile([P, P], F32, name="rb", tag="rb", bufs=4)
             nc.scalar.copy(out=d["rb"][:], in_=rbp[:])
 
-        def mx1(s):
+        def mx1(s, tag="mx"):
             b = s // 4
             d = st[s]
-            d["c1"] = psum.tile([P, 4, P], F32, name="c1", tag="mx", bufs=NB["mx"])
+            d["c1"] = psum.tile([P, 4, P], F32, name="c1", tag=tag, bufs=NB[tag])
             for t in range(4):
                 for g in range(2):
                     nc.tensor.matmul_mx(
@@ -333,9 +352,9 @@ def tile_i2p_crossattention_pa_kernel(tc, q, k, v, Wo, bo, feat0, out):
                 in_=d["cG"][:].rearrange("p n t -> p (n t)"),
             )
 
-        def mx2(s):
+        def mx2(s, tag="mx"):
             d = st[s]
-            d["y"] = psum.tile([P, 4, P], F32, name="y", tag="mx", bufs=NB["mx"])
+            d["y"] = psum.tile([P, 4, P], F32, name="y", tag=tag, bufs=NB[tag])
             for ot in range(4):
                 nc.tensor.matmul_mx(
                     out=d["y"][:, ot, :],
@@ -358,22 +377,35 @@ def tile_i2p_crossattention_pa_kernel(tc, q, k, v, Wo, bo, feat0, out):
                 in_=o_sb[:],
             )
 
+        def final_sg(s):
+            b, i = divmod(s, 4)
+            y_sb = work.tile([P, 4, P], F32, name="y_sb", tag="y_sb", bufs=2)
+            nc.scalar.copy(out=y_sb[:], in_=st[s]["y"][:])
+            o_sb = work.tile([P, 4, P], F32, name="o_sb", tag="o_sb", bufs=4)
+            nc.gpsimd.tensor_tensor(
+                out=o_sb[:], in0=y_sb[:], in1=fb[b][:, :, P * i : P * i + P], op=ALU.add
+            )
+            nc.sync.dma_start(
+                out=out[b].rearrange("(t p) n -> p t n", p=P)[:, :, P * i : P * i + P],
+                in_=o_sb[:],
+            )
+
         def live(x):
             return 0 <= x < NT
 
-        for op in k_job(0, 0, "v", "en") + k_job(0, 1, "s", "en") + q_job(0, 0, 2, "v"):
+        for op in q_job(0, 0, 1, "v") + k_job(0, 0, "s", "en") + k_job(0, 1, "v", "en"):
             op()
 
         def at(s, place):
             for call in singles.get((s, place), []):
                 call()
 
-        k02, k03, q02 = k_job(0, 2, "s"), k_job(0, 3, "v"), q_job(0, 2, 2)
+        k02, k03, q01, q02 = k_job(0, 2, "s"), k_job(0, 3, "v"), q_job(0, 1, 1), q_job(0, 2, 2)
         w0, w1, w2, w3 = [w_job(ot) for ot in range(4)]
         k10, k11, k12, k13 = [k_job(1, a) for a in range(4)]
         q10, q12 = q_job(1, 0, 2), q_job(1, 2, 2)
         fills = {
-            (0, 0): k02, (0, 1): k03, (0, 5): q02[0:2], (0, 6): q02[2:4], (0, 7): [bo_job],
+            (0, 0): k02, (0, 2): k03, (0, 4): q01, (0, 6): q02, (0, 7): [bo_job],
             (1, 4): w0, (1, 5): w1, (1, 6): w2, (1, 7): w3,
             (2, 0): k10, (2, 2): k11, (2, 6): k12,
             (3, 0): k13, (3, 2): q10, (3, 6): q12,
@@ -381,12 +413,14 @@ def tile_i2p_crossattention_pa_kernel(tc, q, k, v, Wo, bo, feat0, out):
         singles = {
             (0, 0): [lambda: v_regroup(1, 0, "g"), lambda: v_regroup(1, 1, "g")],
             (0, 1): [lambda: v_regroup(0, 0, "v")],
-            (0, 2): [lambda: v_regroup(0, 1, "v")] + [lambda b=b, ot=ot: add_bias(b, ot) for b in range(B) for ot in range(4)],
+            (0, 2): [lambda: v_regroup(0, 1, "v")],
             (1, 1): [lambda: v_quant(0, 0)],
             (1, 2): [lambda: v_quant(0, 1)],
+            (2, 1): [lambda: add_bias(0, 0), lambda: add_bias(0, 1), lambda: add_bias(0, 2), lambda: add_bias(0, 3)],
             (2, 2): [w_quant],
             (3, 1): [lambda: v_quant(1, 0)],
-            (4, 1): [lambda: v_quant(1, 1)],
+            (4, 1): [lambda: v_quant(1, 1), lambda: add_bias(1, 0), lambda: add_bias(1, 1)],
+            (5, 1): [lambda: add_bias(1, 2), lambda: add_bias(1, 3)],
         }
 
         for s in range(NT):
@@ -395,23 +429,23 @@ def tile_i2p_crossattention_pa_kernel(tc, q, k, v, Wo, bo, feat0, out):
                 te_tile(s - 1)
             at(s, 0)
             for x in range(8):
-                energy(s, x // 4, x % 4)
+                if s == 0 and x < 4:
+                    if x == 0:
+                        st[0]["en0"] = psum.tile([P, 512], F32, name="en", tag="en", bufs=NB["en"])
+                    energy_quarter(0, x // 2, 2 * (x % 2))
+                    energy_quarter(0, x // 2, 2 * (x % 2) + 1)
+                else:
+                    energy(s, x // 4, x % 4)
                 if x == 1 and live(s - 2):
                     spread_rinv(s - 2)
-                if x in (4, 5) and live(s - 1):
-                    if x == 4:
-                        te_bank = psum.tile([P, 4, P], F32, name="tes", tag="tp", bufs=NB["tp"])
-                    te_half(s - 1, x - 4, te_bank, 2 * x - 8)
-                    if x == 5:
-                        te_copy(s - 1, "s", te_bank[:], 0, 2)
-                for op in fills.get((s, x), []):
-                    op()
                 if x == 3:
+                    max0(s)
+                    at(s, 1)
+                if x == 3 and s < NT - 1:
                     if live(s - 3):
                         mx2(s - 3)
                     if live(s - 2):
                         mx1(s - 2)
-                    max0(s)
                     if live(s - 3):
                         final(s - 3)
                     if live(s - 1):
@@ -422,7 +456,18 @@ def tile_i2p_crossattention_pa_kernel(tc, q, k, v, Wo, bo, feat0, out):
                         rinv(s - 1)
                     if live(s - 2):
                         ctx_quant(s - 2)
-                    at(s, 1)
+                if x == 3 and s == NT - 1:
+                    rsum(s - 1)
+                    rinv(s - 1)
+
+                if x in (4, 5) and live(s - 1):
+                    if x == 4:
+                        te_bank = psum.tile([P, 4, P], F32, name="tes", tag="tp", bufs=NB["tp"])
+                    te_half(s - 1, x - 4, te_bank, 2 * (x - 4))
+                    if x == 5:
+                        te_copy(s - 1, "s", te_bank[:], 0, 2)
+                for op in fills.get((s, x), []):
+                    op()
             max1(s)
             if live(s - 1):
                 quant_e(s - 1)
@@ -430,24 +475,30 @@ def tile_i2p_crossattention_pa_kernel(tc, q, k, v, Wo, bo, feat0, out):
 
         exps(7)
         te_tile(7)
+        te_banks = [psum.tile([P, 2, P], F32, name="tel", tag="tp", bufs=NB["tp"]) for g in range(2)]
         spread_rinv(6)
-        mx2(5)
+        mx2(4)
+        mx1(5)
+        final(4)
+        ctx_out(5)
+        te_half(7, 0, te_banks[0], 0)
+        te_copy(7, "v", te_banks[0][:], 0, 1)
+        ctx_quant(5)
+        te_half(7, 1, te_banks[1], 0)
+        te_copy(7, "s", te_banks[1][:], 1, 2)
         mx1(6)
-        final(5)
-        for g in range(2):
-            te_bank = psum.tile([P, 2, P], F32, name="tel", tag="tp", bufs=NB["tp"])
-            te_half(7, g, te_bank, 0)
-            te_copy(7, "vs"[g], te_bank[:], g, g + 1)
-        ctx_out(6)
         rsum(7)
-        ctx_quant(6)
         rinv(7)
         quant_e(7)
+        ctx_out(6)
+        mx2(5)
         spread_rinv(7)
-        mx1(7)
-        mx2(6)
+        mx1(7, "en")
+        ctx_quant(6)
         ctx_out(7)
+        mx2(6)
         ctx_quant(7)
+        final(5)
         final(6)
-        mx2(7)
+        mx2(7, "en")
         final(7)

@@ -37,7 +37,7 @@ def tile_i2p_crossattention_pa_kernel(tc, q, k, v, Wo, bo, feat0, out):
         v_raw = [keep.tile([P, 8, C], BF16, name="v_raw%d" % b) for b in range(B)]
         f_raw = [keep.tile([P, 4, N], BF16, name="f_raw%d" % b) for b in range(B)]
         w_raw = keep.tile([P, 4, C], BF16, name="w_raw")
-        bo_rows = keep.tile([P, P], BF16, name="bo_rows")
+        bo_raw = keep.tile([P, 4], BF16, name="bo_raw")
         bo_col = keep.tile([P, 4], F32, name="bo_col")
         ident_b = keep.tile([P, P], BF16, name="ident_b")
         ident_f = keep.tile([P, P], F32, name="ident_f")
@@ -62,36 +62,43 @@ def tile_i2p_crossattention_pa_kernel(tc, q, k, v, Wo, bo, feat0, out):
                 in_=v[b, 512 * g : 512 * g + 512, :].rearrange("(p t) c -> p t c", t=4),
             )
 
-        def load_q(b, i0, i1):
+        def load_q(b, i):
             nc.sync.dma_start(
-                out=q_raw[b][:, i0:i1, :],
-                in_=q[b, P * i0 : P * i1, :].rearrange("(i p) c -> p i c", p=P),
+                out=q_raw[b][:, i : i + 1, :],
+                in_=q[b, P * i : P * i + P, :].rearrange("(p t) c -> p t c", t=1),
             )
 
-        nc.vector.memset(bo_rows[:], 0.0)
+        def load_q_pair(b, a):
+            nc.sync.dma_start(
+                out=q_raw[b][:, 2 * a : 2 * a + 2, :],
+                in_=q[b, 256 * a : 256 * a + 256, :].rearrange("(p t) c -> p t c", t=2),
+            )
+
         warm = keep.tile([P, 1], F32, name="warm")
         nc.vector.memset(warm[:], 0.0)
         nc.scalar.activation(out=warm[:], in_=warm[:], func=ACT.Exp, bias=0.0, scale=1.0)
         make_identity(nc, ident_b[:])
         make_identity(nc, ident_f[:])
 
-        nc.scalar.dma_start(out=bo_rows[0:4, :], in_=bo.rearrange("(t p) -> t p", p=P))
-        load_q(0, 0, 1)
+        nc.scalar.dma_start(out=bo_raw[:], in_=bo.rearrange("(p t) -> p t", t=4))
+        load_q(0, 0)
         load_k(0, 0, 0, 2)
         load_k(0, 0, 2, 4)
         load_k(0, 1, 0, 2)
         load_k(0, 1, 2, 4)
-        load_q(0, 1, 4)
+        load_q(0, 1)
+        load_q_pair(0, 1)
         load_v(0, 0)
         load_v(0, 1)
+        nc.sync.dma_start(out=w_raw[:], in_=Wo.rearrange("(p t) c -> p t c", t=4))
         load_v(1, 0)
         load_v(1, 1)
-        nc.sync.dma_start(out=w_raw[:], in_=Wo.rearrange("(t p) c -> p t c", p=P))
         load_k(1, 0)
         load_k(1, 1)
-        load_q(1, 0, 4)
-        nc.sync.dma_start(out=f_raw[0][:], in_=feat0[0].rearrange("(t p) n -> p t n", p=P))
-        nc.sync.dma_start(out=f_raw[1][:], in_=feat0[1].rearrange("(t p) n -> p t n", p=P))
+        load_q_pair(1, 0)
+        load_q_pair(1, 1)
+        nc.sync.dma_start(out=f_raw[0][:], in_=feat0[0].rearrange("(p t) n -> p t n", t=4))
+        nc.sync.dma_start(out=f_raw[1][:], in_=feat0[1].rearrange("(p t) n -> p t n", t=4))
 
         def copy_on(eng, dst, src):
             if eng == "s":
@@ -128,7 +135,7 @@ def tile_i2p_crossattention_pa_kernel(tc, q, k, v, Wo, bo, feat0, out):
             return word_job(k_raw[b], kT[b][a // 2], 2 * a, 2, eng, tag, 2 * P * (a % 2), True)
 
         def q_job(b, r0, rows, eng="s", tag="tp"):
-            return word_job(q_raw[b], qT[b], r0, rows, eng, tag, P * r0, False)
+            return word_job(q_raw[b], qT[b], r0, rows, eng, tag, P * r0, rows == 2)
 
         def w_job(ot, eng="s"):
             hold = []
@@ -148,11 +155,6 @@ def tile_i2p_crossattention_pa_kernel(tc, q, k, v, Wo, bo, feat0, out):
                 scales=wS[:],
                 in_=wG[:].rearrange("p a o t -> p (a o t)"),
             )
-
-        def bo_job():
-            ps = psum.tile([P, 4, P], BF16, name="tps", tag="tp", bufs=NB["tp"])
-            nc.tensor.transpose(ps[:, 0, :], bo_rows[:], ident_b[:])
-            nc.vector.tensor_copy(out=bo_col[:], in_=ps[:, 0, 0:4])
 
         def add_bias(b, ot):
             if b == 0:
@@ -174,24 +176,24 @@ def tile_i2p_crossattention_pa_kernel(tc, q, k, v, Wo, bo, feat0, out):
 
         vG = {}
 
-        def v_regroup(b, g, eng):
-            vG[(b, g)] = work.tile([P, C, 4], BF16, name="vG", tag="vG", bufs=4, align_bytes=64)
+        def v_regroup(b, g, hf, eng):
+            if hf == 0:
+                vG[(b, g)] = work.tile([P, C, 4], BF16, name="vG", tag="vG", bufs=4, align_bytes=64)
+            c0 = 256 * hf
             if eng == "v":
                 nc.vector.tensor_copy(
-                    out=vG[(b, g)][:].rearrange("p (c i) t -> p c t i", i=4),
-                    in_=v_raw[b][:, 4 * g : 4 * g + 4, :].rearrange("p t (c i) -> p c t i", i=4),
+                    out=vG[(b, g)][:, c0 : c0 + 256, :].rearrange("p (c i) t -> p c t i", i=4),
+                    in_=v_raw[b][:, 4 * g : 4 * g + 4, c0 : c0 + 256].rearrange("p t (c i) -> p c t i", i=4),
                 )
             else:
-                cw = C // 2
-                for hf in range(2):
-                    nc.gpsimd.tensor_scalar(
-                        out=vG[(b, g)][:, cw * hf : cw * hf + cw, :],
-                        in0=v_raw[b][:, 4 * g : 4 * g + 4, cw * hf : cw * hf + cw].rearrange("p t c -> p c t"),
-                        scalar1=1.0,
-                        scalar2=0.0,
-                        op0=ALU.mult,
-                        op1=ALU.add,
-                    )
+                nc.gpsimd.tensor_scalar(
+                    out=vG[(b, g)][:, c0 : c0 + 256, :],
+                    in0=v_raw[b][:, 4 * g : 4 * g + 4, c0 : c0 + 256].rearrange("p t c -> p c t"),
+                    scalar1=1.0,
+                    scalar2=0.0,
+                    op0=ALU.mult,
+                    op1=ALU.add,
+                )
 
         def v_quant(b, g):
             nc.vector.quantize_mx(
@@ -373,7 +375,7 @@ def tile_i2p_crossattention_pa_kernel(tc, q, k, v, Wo, bo, feat0, out):
                 out=o_sb[:], in0=st[s]["y"][:], in1=fb[b][:, :, P * i : P * i + P], op=ALU.add
             )
             nc.sync.dma_start(
-                out=out[b].rearrange("(t p) n -> p t n", p=P)[:, :, P * i : P * i + P],
+                out=out[b].rearrange("(p t) n -> p t n", t=4)[:, :, P * i : P * i + P],
                 in_=o_sb[:],
             )
 
@@ -386,7 +388,7 @@ def tile_i2p_crossattention_pa_kernel(tc, q, k, v, Wo, bo, feat0, out):
                 out=o_sb[:], in0=y_sb[:], in1=fb[b][:, :, P * i : P * i + P], op=ALU.add
             )
             nc.sync.dma_start(
-                out=out[b].rearrange("(t p) n -> p t n", p=P)[:, :, P * i : P * i + P],
+                out=out[b].rearrange("(p t) n -> p t n", t=4)[:, :, P * i : P * i + P],
                 in_=o_sb[:],
             )
 
@@ -405,25 +407,31 @@ def tile_i2p_crossattention_pa_kernel(tc, q, k, v, Wo, bo, feat0, out):
         k10, k11, k12, k13 = [k_job(1, a) for a in range(4)]
         q10, q12 = q_job(1, 0, 2), q_job(1, 2, 2)
         fills = {
-            (0, 0): k02, (0, 2): k03, (0, 4): q01, (0, 6): q02, (0, 7): [bo_job],
-            (1, 4): w0, (1, 5): w1, (1, 6): w2, (1, 7): w3,
-            (2, 0): k10, (2, 2): k11, (2, 6): k12,
-            (3, 0): k13, (3, 2): q10, (3, 6): q12,
+            (0, 0): k02, (0, 2): k03, (0, 4): q01, (0, 6): q02,
+            (1, 6): w0, (1, 7): w1,
+            (2, 0): w2, (2, 2): w3, (2, 6): k10, (2, 7): k11,
+            (3, 0): k12, (3, 2): k13, (3, 6): q10,
+            (4, 0): q12,
         }
         singles = {
-            (0, 0): [lambda: v_regroup(1, 0, "g"), lambda: v_regroup(1, 1, "g")],
-            (0, 1): [lambda: v_regroup(0, 0, "v")],
-            (0, 2): [lambda: v_regroup(0, 1, "v")],
+            (0, 0): [lambda b=b, hf=hf: v_regroup(b, 0, hf, "g") for b in range(B) for hf in range(2)],
+            (0, 1): [lambda: nc.vector.tensor_copy(out=bo_col[:], in_=bo_raw[:])],
+            (0, 2): [lambda: v_regroup(0, 1, 0, "v"), lambda: v_regroup(0, 1, 1, "v")],
             (1, 1): [lambda: v_quant(0, 0)],
             (1, 2): [lambda: v_quant(0, 1)],
-            (2, 1): [lambda: add_bias(0, 0), lambda: add_bias(0, 1), lambda: add_bias(0, 2), lambda: add_bias(0, 3)],
-            (2, 2): [w_quant],
-            (3, 1): [lambda: v_quant(1, 0)],
-            (4, 1): [lambda: v_quant(1, 1), lambda: add_bias(1, 0), lambda: add_bias(1, 1)],
+            (2, 1): [w_quant],
+            (2, 2): [lambda: v_regroup(1, 1, 0, "v")],
+            (3, 1): [lambda: v_regroup(1, 1, 1, "v")],
+            (3, 2): [lambda: add_bias(0, 0), lambda: add_bias(0, 1), lambda: add_bias(0, 2), lambda: add_bias(0, 3)],
+            (4, 1): [lambda: v_quant(1, 0), lambda: v_quant(1, 1), lambda: add_bias(1, 0), lambda: add_bias(1, 1)],
             (5, 1): [lambda: add_bias(1, 2), lambda: add_bias(1, 3)],
         }
 
         for s in range(NT):
+            if live(s - 4):
+                final(s - 4)
+            if live(s - 3):
+                ctx_out(s - 3)
             if live(s - 1):
                 exps(s - 1)
                 te_tile(s - 1)
@@ -440,45 +448,34 @@ def tile_i2p_crossattention_pa_kernel(tc, q, k, v, Wo, bo, feat0, out):
                     spread_rinv(s - 2)
                 if x == 3:
                     max0(s)
-                    at(s, 1)
-                if x == 3 and s < NT - 1:
                     if live(s - 3):
-                        mx2(s - 3)
-                    if live(s - 2):
-                        mx1(s - 2)
-                    if live(s - 3):
-                        final(s - 3)
+                        ctx_quant(s - 3)
                     if live(s - 1):
                         rsum(s - 1)
-                    if live(s - 2):
-                        ctx_out(s - 2)
-                    if live(s - 1):
-                        rinv(s - 1)
-                    if live(s - 2):
-                        ctx_quant(s - 2)
-                if x == 3 and s == NT - 1:
-                    rsum(s - 1)
-                    rinv(s - 1)
-
-                if x in (4, 5) and live(s - 1):
-                    if x == 4:
-                        te_bank = psum.tile([P, 4, P], F32, name="tes", tag="tp", bufs=NB["tp"])
-                    te_half(s - 1, x - 4, te_bank, 2 * (x - 4))
+                    at(s, 1)
+                if x in (5, 6) and live(s - 1):
                     if x == 5:
+                        te_bank = psum.tile([P, 4, P], F32, name="tes", tag="tp", bufs=NB["tp"])
+                    te_half(s - 1, x - 5, te_bank, 2 * (x - 5))
+                    if x == 6:
                         te_copy(s - 1, "s", te_bank[:], 0, 2)
                 for op in fills.get((s, x), []):
                     op()
             max1(s)
             if live(s - 1):
+                rinv(s - 1)
+            if live(s - 1):
                 quant_e(s - 1)
             at(s, 2)
+            if live(s - 3):
+                mx2(s - 3)
+            if live(s - 2):
+                mx1(s - 2)
 
         exps(7)
         te_tile(7)
         te_banks = [psum.tile([P, 2, P], F32, name="tel", tag="tp", bufs=NB["tp"]) for g in range(2)]
         spread_rinv(6)
-        mx2(4)
-        mx1(5)
         final(4)
         ctx_out(5)
         te_half(7, 0, te_banks[0], 0)

@@ -74,6 +74,8 @@ def tile_i2p_crossattention_pa_kernel(tc, q, k, v, Wo, bo, feat0, out):
                 in_=q[b, 256 * a : 256 * a + 256, :].rearrange("(p t) c -> p t c", t=2),
             )
 
+        idle = keep.tile([P, 512], BF16, name="idle")
+        nc.vector.memset(idle[:], 0.0)
         warm = keep.tile([P, 1], F32, name="warm")
         nc.vector.memset(warm[:], 0.0)
         nc.scalar.activation(out=warm[:], in_=warm[:], func=ACT.Exp, bias=0.0, scale=1.0)
@@ -99,6 +101,13 @@ def tile_i2p_crossattention_pa_kernel(tc, q, k, v, Wo, bo, feat0, out):
         load_q_pair(1, 1)
         nc.sync.dma_start(out=f_raw[0][:], in_=feat0[0].rearrange("(p t) n -> p t n", t=4))
         nc.sync.dma_start(out=f_raw[1][:], in_=feat0[1].rearrange("(p t) n -> p t n", t=4))
+
+        def keep_busy():
+            ps = psum.tile([P, 512], F32, name="idle_ps", tag="mx", bufs=NB["mx"])
+            nc.tensor.matmul(out=ps[:], lhsT=idle[:, 0:P], rhs=idle[:], start=True, stop=True)
+
+        for x in range(5):
+            keep_busy()
 
         def copy_on(eng, dst, src):
             if eng == "s":
@@ -395,7 +404,7 @@ def tile_i2p_crossattention_pa_kernel(tc, q, k, v, Wo, bo, feat0, out):
         def live(x):
             return 0 <= x < NT
 
-        for op in q_job(0, 0, 1, "v") + k_job(0, 0, "s", "en") + k_job(0, 1, "v", "en"):
+        for op in q_job(0, 0, 1, "v") + [keep_busy] + k_job(0, 0, "s", "en") + [keep_busy] + k_job(0, 1, "v", "en") + [keep_busy]:
             op()
 
         def at(s, place):
@@ -423,7 +432,8 @@ def tile_i2p_crossattention_pa_kernel(tc, q, k, v, Wo, bo, feat0, out):
             (2, 2): [lambda: v_regroup(1, 1, 0, "v")],
             (3, 1): [lambda: v_regroup(1, 1, 1, "v")],
             (3, 2): [lambda: add_bias(0, 0), lambda: add_bias(0, 1), lambda: add_bias(0, 2), lambda: add_bias(0, 3)],
-            (4, 1): [lambda: v_quant(1, 0), lambda: v_quant(1, 1), lambda: add_bias(1, 0), lambda: add_bias(1, 1)],
+            (4, 1): [lambda: v_quant(1, 0), lambda: add_bias(1, 0), lambda: add_bias(1, 1)],
+            (5, 0): [lambda: v_quant(1, 1)],
             (5, 1): [lambda: add_bias(1, 2), lambda: add_bias(1, 3)],
         }
 
@@ -444,7 +454,7 @@ def tile_i2p_crossattention_pa_kernel(tc, q, k, v, Wo, bo, feat0, out):
                     energy_quarter(0, x // 2, 2 * (x % 2) + 1)
                 else:
                     energy(s, x // 4, x % 4)
-                if x == 1 and live(s - 2):
+                if x == 3 and live(s - 2):
                     spread_rinv(s - 2)
                 if x == 3:
                     max0(s)

@@ -167,6 +167,15 @@ def tile_i2p_crossattention_pa_kernel(tc, q, k, v, Wo, bo, feat0, out):
 
         def add_bias(b, ot):
             if b == 0:
+                nc.gpsimd.tensor_scalar(
+                    out=fb[b][:, ot, :],
+                    in0=f_raw[b][:, ot, :],
+                    scalar1=1.0,
+                    scalar2=bo_col[:, ot : ot + 1],
+                    op0=ALU.mult,
+                    op1=ALU.add,
+                )
+            elif b == 0:
                 nc.vector.tensor_scalar(
                     out=fb[b][:, ot, :],
                     in0=f_raw[b][:, ot, :],
@@ -310,14 +319,15 @@ def tile_i2p_crossattention_pa_kernel(tc, q, k, v, Wo, bo, feat0, out):
                 ps.rearrange("p (g u) n -> p g n u", u=2),
             )
 
-        def quant_e(s):
+        def quant_e(s, g0=0, g1=2):
             d = st[s]
-            d["eW"] = work.tile([P, 2 * P], U32, name="eW", tag="eW", bufs=4, align_bytes=64)
-            d["eS"] = work.tile([P, 2 * P], U8, name="eS", tag="eS", bufs=4, align_bytes=64)
+            if g0 == 0:
+                d["eW"] = work.tile([P, 2 * P], U32, name="eW", tag="eW", bufs=4, align_bytes=64)
+                d["eS"] = work.tile([P, 2 * P], U8, name="eS", tag="eS", bufs=4, align_bytes=64)
             nc.vector.quantize_mx(
-                out=d["eW"][:].bitcast(FP8X4),
-                scales=d["eS"][:],
-                in_=d["eG"][:].rearrange("p g n u -> p (g n u)").bitcast(BF16),
+                out=d["eW"][:, P * g0 : P * g1].bitcast(FP8X4),
+                scales=d["eS"][:, P * g0 : P * g1],
+                in_=d["eG"][:, g0:g1, :, :].rearrange("p g n u -> p (g n u)").bitcast(BF16),
             )
 
         def spread_rinv(s):
@@ -363,12 +373,15 @@ def tile_i2p_crossattention_pa_kernel(tc, q, k, v, Wo, bo, feat0, out):
                 in_=d["cG"][:].rearrange("p n t -> p (n t)"),
             )
 
-        def mx2(s, tag="mx"):
+        def mx2(s, tag="mx", parts=1):
             d = st[s]
-            d["y"] = psum.tile([P, 4, P], F32, name="y", tag=tag, bufs=NB[tag])
+            n = 4 // parts
+            d["y"] = []
             for ot in range(4):
+                if ot % n == 0:
+                    d["y"].append(psum.tile([P, n, P], F32, name="y", tag=tag, bufs=NB[tag]))
                 nc.tensor.matmul_mx(
-                    out=d["y"][:, ot, :],
+                    out=d["y"][-1][:, ot % n, :],
                     lhsT=wW[:, P * ot : P * ot + P].bitcast(FP8X4),
                     lhsT_scale=wS[:, P * ot : P * ot + P],
                     rhs=d["cW"][:].bitcast(FP8X4),
@@ -379,27 +392,18 @@ def tile_i2p_crossattention_pa_kernel(tc, q, k, v, Wo, bo, feat0, out):
 
         def final(s):
             b, i = divmod(s, 4)
+            ys = st[s]["y"]
+            n = 4 // len(ys)
             o_sb = work.tile([P, 4, P], F32, name="o_sb", tag="o_sb", bufs=4)
-            nc.vector.tensor_tensor(
-                out=o_sb[:], in0=st[s]["y"][:], in1=fb[b][:, :, P * i : P * i + P], op=ALU.add
-            )
-            nc.sync.dma_start(
-                out=out[b].rearrange("(p t) n -> p t n", t=4)[:, :, P * i : P * i + P],
-                in_=o_sb[:],
-            )
-
-        def final_sg(s):
-            b, i = divmod(s, 4)
-            y_sb = work.tile([P, 4, P], F32, name="y_sb", tag="y_sb", bufs=2)
-            nc.scalar.copy(out=y_sb[:], in_=st[s]["y"][:])
-            o_sb = work.tile([P, 4, P], F32, name="o_sb", tag="o_sb", bufs=4)
-            nc.gpsimd.tensor_tensor(
-                out=o_sb[:], in0=y_sb[:], in1=fb[b][:, :, P * i : P * i + P], op=ALU.add
-            )
-            nc.sync.dma_start(
-                out=out[b].rearrange("(p t) n -> p t n", t=4)[:, :, P * i : P * i + P],
-                in_=o_sb[:],
-            )
+            for x, y in enumerate(ys):
+                ots = slice(n * x, n * x + n)
+                nc.vector.tensor_tensor(
+                    out=o_sb[:, ots, :], in0=y[:], in1=fb[b][:, ots, P * i : P * i + P], op=ALU.add
+                )
+                nc.sync.dma_start(
+                    out=out[b].rearrange("(p t) n -> p t n", t=4)[:, ots, P * i : P * i + P],
+                    in_=o_sb[:, ots, :],
+                )
 
         def live(x):
             return 0 <= x < NT
@@ -412,28 +416,25 @@ def tile_i2p_crossattention_pa_kernel(tc, q, k, v, Wo, bo, feat0, out):
                 call()
 
         k02, k03, q01, q02 = k_job(0, 2, "s"), k_job(0, 3, "v"), q_job(0, 1, 1), q_job(0, 2, 2)
-        w0, w1, w2, w3 = [w_job(ot) for ot in range(4)]
-        k10, k11, k12, k13 = [k_job(1, a) for a in range(4)]
+        w0, w1, w2, w3 = [w_job(ot, "svvs"[ot]) for ot in range(4)]
+        k10, k11, k12, k13 = [k_job(1, a, "ssss"[a]) for a in range(4)]
         q10, q12 = q_job(1, 0, 2), q_job(1, 2, 2)
         fills = {
             (0, 0): k02, (0, 2): k03, (0, 4): q01, (0, 6): q02,
-            (1, 6): w0, (1, 7): w1,
-            (2, 0): w2, (2, 2): w3, (2, 6): k10, (2, 7): k11,
+            (1, 6): w0, (2, 0): w1, (2, 1): w2, (2, 2): w3, (2, 6): k10, (2, 7): k11,
             (3, 0): k12, (3, 2): k13, (3, 6): q10,
             (4, 0): q12,
         }
         singles = {
-            (0, 0): [lambda b=b, hf=hf: v_regroup(b, 0, hf, "g") for b in range(B) for hf in range(2)],
+            (0, 0): [lambda b=b, g=g, hf=hf: v_regroup(b, g, hf, "g") for b, g in ((0, 0), (1, 0), (1, 1)) for hf in range(2)],
             (0, 1): [lambda: nc.vector.tensor_copy(out=bo_col[:], in_=bo_raw[:])],
             (0, 2): [lambda: v_regroup(0, 1, 0, "v"), lambda: v_regroup(0, 1, 1, "v")],
             (1, 1): [lambda: v_quant(0, 0)],
             (1, 2): [lambda: v_quant(0, 1)],
-            (2, 1): [w_quant],
-            (2, 2): [lambda: v_regroup(1, 1, 0, "v")],
-            (3, 1): [lambda: v_regroup(1, 1, 1, "v")],
-            (3, 2): [lambda: add_bias(0, 0), lambda: add_bias(0, 1), lambda: add_bias(0, 2), lambda: add_bias(0, 3)],
-            (4, 1): [lambda: v_quant(1, 0), lambda: add_bias(1, 0), lambda: add_bias(1, 1)],
-            (5, 0): [lambda: v_quant(1, 1)],
+            (2, 2): [w_quant],
+            (3, 0): [lambda: add_bias(0, 0), lambda: add_bias(0, 1), lambda: add_bias(0, 2), lambda: add_bias(0, 3)],
+            (3, 1): [lambda: v_quant(1, 0)],
+            (4, 1): [lambda: v_quant(1, 1), lambda: add_bias(1, 0), lambda: add_bias(1, 1)],
             (5, 1): [lambda: add_bias(1, 2), lambda: add_bias(1, 3)],
         }
 
@@ -494,18 +495,19 @@ def tile_i2p_crossattention_pa_kernel(tc, q, k, v, Wo, bo, feat0, out):
         te_half(7, 1, te_banks[1], 0)
         te_copy(7, "s", te_banks[1][:], 1, 2)
         mx1(6)
+        quant_e(7, 0, 1)
         rsum(7)
         rinv(7)
-        quant_e(7)
+        quant_e(7, 1, 2)
         ctx_out(6)
         mx2(5)
         spread_rinv(7)
         mx1(7, "en")
+        final(5)
         ctx_quant(6)
         ctx_out(7)
         mx2(6)
         ctx_quant(7)
-        final(5)
         final(6)
-        mx2(7, "en")
+        mx2(7, "en", 2)
         final(7)

@@ -39,13 +39,12 @@ def tile_i2p_crossattention_pa_kernel(tc, q, k, v, Wo, bo, feat0, out):
         w_raw = keep.tile([P, 4, C], BF16, name="w_raw")
         bo_raw = keep.tile([P, 4], BF16, name="bo_raw")
         bo_col = keep.tile([P, 4], F32, name="bo_col")
-        ident_b = keep.tile([P, P], BF16, name="ident_b")
         ident_f = keep.tile([P, P], F32, name="ident_f")
         kT = [[keep.tile([P, 2, M // 2], F32, name="kT%d%d" % (b, h)) for h in range(2)] for b in range(B)]
         qT = [keep.tile([P, 2, N], F32, name="qT%d" % b) for b in range(B)]
         vW = [keep.tile([P, 2, C], U32, name="vW%d" % b, align_bytes=64) for b in range(B)]
         vS = [keep.tile([P, 2, C], U8, name="vS%d" % b, align_bytes=64) for b in range(B)]
-        wG = keep.tile([P, 4, P, 4], BF16, name="wG", align_bytes=64)
+        wG = keep.tile([P, C, 2], F32, name="wG", align_bytes=64)
         wW = keep.tile([P, C], U32, name="wW", align_bytes=64)
         wS = keep.tile([P, C], U8, name="wS", align_bytes=64)
         fb = [keep.tile([P, 4, N], F32, name="fb%d" % b) for b in range(B)]
@@ -76,37 +75,34 @@ def tile_i2p_crossattention_pa_kernel(tc, q, k, v, Wo, bo, feat0, out):
 
         idle = keep.tile([P, 512], BF16, name="idle")
         nc.vector.memset(idle[:], 0.0)
-        warm = keep.tile([P, 1], F32, name="warm")
-        nc.vector.memset(warm[:], 0.0)
-        nc.scalar.activation(out=warm[:], in_=warm[:], func=ACT.Exp, bias=0.0, scale=1.0)
-        make_identity(nc, ident_b[:])
+        nc.scalar.activation(out=idle[:], in_=idle[:], func=ACT.Exp, bias=0.0, scale=1.0)
         make_identity(nc, ident_f[:])
 
         nc.scalar.dma_start(out=bo_raw[:], in_=bo.rearrange("(p t) -> p t", t=4))
         load_q(0, 0)
         load_k(0, 0, 0, 2)
         load_k(0, 0, 2, 4)
+        load_q(0, 1)
         load_k(0, 1, 0, 2)
         load_k(0, 1, 2, 4)
-        load_q(0, 1)
         load_q_pair(0, 1)
         load_v(0, 0)
         load_v(0, 1)
         nc.sync.dma_start(out=w_raw[:], in_=Wo.rearrange("(p t) c -> p t c", t=4))
-        load_v(1, 0)
-        load_v(1, 1)
         load_k(1, 0)
         load_k(1, 1)
         load_q_pair(1, 0)
         load_q_pair(1, 1)
         nc.sync.dma_start(out=f_raw[0][:], in_=feat0[0].rearrange("(p t) n -> p t n", t=4))
+        load_v(1, 0)
+        load_v(1, 1)
         nc.sync.dma_start(out=f_raw[1][:], in_=feat0[1].rearrange("(p t) n -> p t n", t=4))
 
         def keep_busy():
             ps = psum.tile([P, 512], F32, name="idle_ps", tag="mx", bufs=NB["mx"])
             nc.tensor.matmul(out=ps[:], lhsT=idle[:, 0:P], rhs=idle[:], start=True, stop=True)
 
-        for x in range(5):
+        for x in range(4):
             keep_busy()
 
         def copy_on(eng, dst, src):
@@ -146,23 +142,32 @@ def tile_i2p_crossattention_pa_kernel(tc, q, k, v, Wo, bo, feat0, out):
         def q_job(b, r0, rows, eng="s", tag="tp"):
             return word_job(q_raw[b], qT[b], r0, rows, eng, tag, P * r0, rows == 2)
 
-        def w_job(ot, eng="s"):
+        def w_job(a, eng="s"):
             hold = []
 
-            def run(t):
+            def run(x):
                 if not hold:
-                    hold.append(psum.tile([P, 4, P], BF16, name="tps", tag="tp", bufs=NB["tp"]))
-                nc.tensor.transpose(hold[0][:, t, :], w_raw[:, ot, P * t : P * t + P], ident_b[:])
-                if t == 3:
-                    copy_on(eng, wG[:, ot, :, :], hold[0][:].rearrange("p t o -> p o t"))
+                    hold.append(psum.tile([P, 2, 2, P], F32, name="wps", tag="tp", bufs=NB["tp"]))
+                u, r = divmod(x, 2)
+                nc.tensor.transpose(
+                    hold[0][:, u, r, :],
+                    w_raw[:, 2 * a + r, :].bitcast(F32)[:, P * u : P * u + P],
+                    ident_f[:],
+                )
+                if x == 3:
+                    copy_on(
+                        eng,
+                        wG[:, 2 * P * a : 2 * P * a + 2 * P, :].rearrange("p (r n) u -> p r n u", r=2),
+                        hold[0][:].rearrange("p u r n -> p r n u"),
+                    )
 
-            return [(lambda t=t: run(t)) for t in range(4)]
+            return [(lambda x=x: run(x)) for x in range(4)]
 
         def w_quant():
             nc.vector.quantize_mx(
                 out=wW[:].bitcast(FP8X4),
                 scales=wS[:],
-                in_=wG[:].rearrange("p a o t -> p (a o t)"),
+                in_=wG[:].rearrange("p o u -> p (o u)").bitcast(BF16),
             )
 
         def add_bias(b, ot):
@@ -200,13 +205,13 @@ def tile_i2p_crossattention_pa_kernel(tc, q, k, v, Wo, bo, feat0, out):
             c0 = 256 * hf
             if eng == "v":
                 nc.vector.tensor_copy(
-                    out=vG[(b, g)][:, c0 : c0 + 256, :].rearrange("p (c i) t -> p c t i", i=4),
-                    in_=v_raw[b][:, 4 * g : 4 * g + 4, c0 : c0 + 256].rearrange("p t (c i) -> p c t i", i=4),
+                    out=vG[(b, g)][:, c0 : c0 + 256, :].rearrange("p (e q) t -> p e q t", e=2),
+                    in_=v_raw[b][:, 4 * g : 4 * g + 4, c0 : c0 + 256].rearrange("p t (q e) -> p e q t", e=2),
                 )
             else:
                 nc.gpsimd.tensor_scalar(
-                    out=vG[(b, g)][:, c0 : c0 + 256, :],
-                    in0=v_raw[b][:, 4 * g : 4 * g + 4, c0 : c0 + 256].rearrange("p t c -> p c t"),
+                    out=vG[(b, g)][:, c0 : c0 + 256, :].rearrange("p (e q) t -> p e q t", e=2),
+                    in0=v_raw[b][:, 4 * g : 4 * g + 4, c0 : c0 + 256].rearrange("p t (q e) -> p e q t", e=2),
                     scalar1=1.0,
                     scalar2=0.0,
                     op0=ALU.mult,
@@ -228,7 +233,7 @@ def tile_i2p_crossattention_pa_kernel(tc, q, k, v, Wo, bo, feat0, out):
             b, i = divmod(s, 4)
             d = st[s]
             if cc == 0:
-                tag = {(1, 1): "mx", (7, 1): "tp"}.get((s, h), "en")
+                tag = {(0, 1): "mx", (1, 1): "mx", (7, 1): "tp"}.get((s, h), "en")
                 d["en%d" % h] = psum.tile([P, 512], F32, name="en", tag=tag, bufs=NB[tag])
             u, e2 = divmod(cc, 2)
             nc.tensor.matmul(
@@ -408,37 +413,62 @@ def tile_i2p_crossattention_pa_kernel(tc, q, k, v, Wo, bo, feat0, out):
         def live(x):
             return 0 <= x < NT
 
-        for op in q_job(0, 0, 1, "v") + [keep_busy] + k_job(0, 0, "s", "en") + [keep_busy] + k_job(0, 1, "v", "en") + [keep_busy]:
-            op()
-
         def at(s, place):
             for call in singles.get((s, place), []):
                 call()
 
-        k02, k03, q01, q02 = k_job(0, 2, "s"), k_job(0, 3, "v"), q_job(0, 1, 1), q_job(0, 2, 2)
-        w0, w1, w2, w3 = [w_job(ot, "svvs"[ot]) for ot in range(4)]
-        k10, k11, k12, k13 = [k_job(1, a, "ssss"[a]) for a in range(4)]
+        q02 = q_job(0, 2, 2)
+        w0, w1 = w_job(0, "vs"[0]), w_job(1, "vs"[1])
+        k10, k11, k12, k13 = [k_job(1, a, "svsv"[a]) for a in range(4)]
         q10, q12 = q_job(1, 0, 2), q_job(1, 2, 2)
         fills = {
-            (0, 0): k02, (0, 2): k03, (0, 4): q01, (0, 6): q02,
-            (1, 6): w0, (2, 0): w1, (2, 1): w2, (2, 2): w3, (2, 6): k10, (2, 7): k11,
-            (3, 0): k12, (3, 2): k13, (3, 6): q10,
-            (4, 0): q12,
+            (2, 4): w0, (2, 6): w1,
+            (3, 1): k10, (3, 2): k11, (3, 4): k12, (3, 5): k13, (3, 7): q10,
+            (4, 3): q12,
         }
         singles = {
-            (0, 0): [lambda b=b, g=g, hf=hf: v_regroup(b, g, hf, "g") for b, g in ((0, 0), (1, 0), (1, 1)) for hf in range(2)],
+            (0, 0): [lambda hf=hf: v_regroup(0, 0, hf, "g") for hf in range(2)],
             (0, 1): [lambda: nc.vector.tensor_copy(out=bo_col[:], in_=bo_raw[:])],
             (0, 2): [lambda: v_regroup(0, 1, 0, "v"), lambda: v_regroup(0, 1, 1, "v")],
-            (1, 1): [lambda: v_quant(0, 0)],
-            (1, 2): [lambda: v_quant(0, 1)],
-            (2, 2): [w_quant],
-            (3, 0): [lambda: add_bias(0, 0), lambda: add_bias(0, 1), lambda: add_bias(0, 2), lambda: add_bias(0, 3)],
-            (3, 1): [lambda: v_quant(1, 0)],
-            (4, 1): [lambda: v_quant(1, 1), lambda: add_bias(1, 0), lambda: add_bias(1, 1)],
-            (5, 1): [lambda: add_bias(1, 2), lambda: add_bias(1, 3)],
+            (2, 1): [lambda: v_quant(0, 0), lambda: v_quant(0, 1)],
+            (3, 0): [lambda: add_bias(0, 0), lambda: add_bias(0, 1), lambda: add_bias(0, 2), lambda: add_bias(0, 3), *[lambda g=g, hf=hf: v_regroup(1, g, hf, "g") for g in range(2) for hf in range(2)]],
+            (3, 1): [w_quant],
+            (4, 1): [lambda: add_bias(1, 0), lambda: add_bias(1, 1)],
+            (5, 1): [lambda: v_quant(1, 0), lambda: add_bias(1, 2), lambda: add_bias(1, 3)],
+            (5, 2): [lambda: v_quant(1, 1)],
         }
 
-        for s in range(NT):
+        def ops(*jobs):
+            for job in jobs:
+                for op in job:
+                    op()
+
+        at(0, 0)
+        ops(q_job(0, 0, 1, "v"), [keep_busy], k_job(0, 0, "s", "en"), [keep_busy], k_job(0, 1, "v", "en"), [keep_busy])
+        st[0]["en0"] = psum.tile([P, 512], F32, name="en", tag="en", bufs=NB["en"])
+        for cc in range(4):
+            energy_quarter(0, 0, cc)
+        ops(q_job(0, 1, 1, "s"))
+        for cc in range(4):
+            energy_quarter(0, 1, cc)
+        max0(0)
+        ops(k_job(0, 2, "s"), k_job(0, 3, "v"))
+        for cc in range(4):
+            energy(1, 0, cc)
+        max0(1)
+        ops(q02)
+        at(0, 1)
+        for cc in range(4):
+            energy(0, 1, cc)
+        max1(0)
+        exps(0)
+        for cc in range(4):
+            energy(1, 1, cc)
+        max1(1)
+        at(0, 2)
+        rsum(0)
+        rinv(0)
+        for s in range(2, NT):
             if live(s - 4):
                 final(s - 4)
             if live(s - 3):
@@ -448,17 +478,20 @@ def tile_i2p_crossattention_pa_kernel(tc, q, k, v, Wo, bo, feat0, out):
                 te_tile(s - 1)
             at(s, 0)
             for x in range(8):
-                if s == 0 and x < 4:
-                    if x == 0:
-                        st[0]["en0"] = psum.tile([P, 512], F32, name="en", tag="en", bufs=NB["en"])
-                    energy_quarter(0, x // 2, 2 * (x % 2))
-                    energy_quarter(0, x // 2, 2 * (x % 2) + 1)
-                else:
-                    energy(s, x // 4, x % 4)
-                if x == 3 and live(s - 2):
+                energy(s, x // 4, x % 4)
+                if s == 2 and x in (2, 3):
+                    if x == 2:
+                        te_tile(0)
+                        te_bank = psum.tile([P, 4, P], F32, name="tes", tag="tp", bufs=NB["tp"])
+                    te_half(0, x - 2, te_bank, 2 * (x - 2))
+                    if x == 3:
+                        te_copy(0, "s", te_bank[:], 0, 2)
+                if x == (7 if s == 2 else 3) and live(s - 2):
                     spread_rinv(s - 2)
                 if x == 3:
                     max0(s)
+                    if s == 2:
+                        quant_e(0)
                     if live(s - 3):
                         ctx_quant(s - 3)
                     if live(s - 1):

@@ -75,7 +75,9 @@ def tile_i2p_crossattention_pa_kernel(tc, q, k, v, Wo, bo, feat0, out):
 
         idle = keep.tile([P, 512], BF16, name="idle")
         nc.vector.memset(idle[:], 0.0)
-        nc.scalar.activation(out=idle[:], in_=idle[:], func=ACT.Exp, bias=0.0, scale=1.0)
+        warm = keep.tile([P, 1], F32, name="warm")
+        nc.vector.memset(warm[:], 0.0)
+        nc.scalar.activation(out=warm[:], in_=warm[:], func=ACT.Exp, bias=0.0, scale=1.0)
         make_identity(nc, ident_f[:])
 
         nc.scalar.dma_start(out=bo_raw[:], in_=bo.rearrange("(p t) -> p t", t=4))
@@ -418,11 +420,11 @@ def tile_i2p_crossattention_pa_kernel(tc, q, k, v, Wo, bo, feat0, out):
                 call()
 
         q02 = q_job(0, 2, 2)
-        w0, w1 = w_job(0, "vs"[0]), w_job(1, "vs"[1])
+        w0, w1 = w_job(0, "sv"[0]), w_job(1, "sv"[1])
         k10, k11, k12, k13 = [k_job(1, a, "svsv"[a]) for a in range(4)]
         q10, q12 = q_job(1, 0, 2), q_job(1, 2, 2)
         fills = {
-            (2, 4): w0, (2, 6): w1,
+            (2, 6): w0, (2, 7): w1,
             (3, 1): k10, (3, 2): k11, (3, 4): k12, (3, 5): k13, (3, 7): q10,
             (4, 3): q12,
         }
@@ -486,7 +488,7 @@ def tile_i2p_crossattention_pa_kernel(tc, q, k, v, Wo, bo, feat0, out):
                     te_half(0, x - 2, te_bank, 2 * (x - 2))
                     if x == 3:
                         te_copy(0, "s", te_bank[:], 0, 2)
-                if x == (7 if s == 2 else 3) and live(s - 2):
+                if x == (4 if s == 2 else 3) and live(s - 2):
                     spread_rinv(s - 2)
                 if x == 3:
                     max0(s)

@@ -19,6 +19,7 @@ C = 512
 N = 512
 M = 1024
 NT = 8
+LAST = NT - 1
 FLOPS = 2 * B * (N * M * C + N * M * C + N * C * C)
 
 NB = {"en": 3, "tp": 3, "mx": 2}
@@ -38,16 +39,14 @@ def tile_i2p_crossattention_pa_kernel(tc, q, k, v, Wo, bo, feat0, out):
         f_raw = [keep.tile([P, 4, N], BF16, name="f_raw%d" % b) for b in range(B)]
         w_raw = keep.tile([P, 4, C], BF16, name="w_raw")
         bo_raw = keep.tile([P, 4], BF16, name="bo_raw")
-        bo_col = keep.tile([P, 4], F32, name="bo_col")
         ident_f = keep.tile([P, P], F32, name="ident_f")
-        kT = [[keep.tile([P, 2, M // 2], F32, name="kT%d%d" % (b, h)) for h in range(2)] for b in range(B)]
-        qT = [keep.tile([P, 2, N], F32, name="qT%d" % b) for b in range(B)]
+        kT = [[keep.tile([P, 2, 2, 256], F32, name="kT%d%d" % (b, h)) for h in range(2)] for b in range(B)]
+        qT = [keep.tile([P, 2, 2, 256], F32, name="qT%d" % b) for b in range(B)]
         vW = [keep.tile([P, 2, C], U32, name="vW%d" % b, align_bytes=64) for b in range(B)]
         vS = [keep.tile([P, 2, C], U8, name="vS%d" % b, align_bytes=64) for b in range(B)]
         wG = keep.tile([P, C, 2], F32, name="wG", align_bytes=64)
         wW = keep.tile([P, C], U32, name="wW", align_bytes=64)
         wS = keep.tile([P, C], U8, name="wS", align_bytes=64)
-        fb = [keep.tile([P, 4, N], F32, name="fb%d" % b) for b in range(B)]
 
         def load_k(b, g, t0=0, t1=4):
             nc.sync.dma_start(
@@ -61,17 +60,14 @@ def tile_i2p_crossattention_pa_kernel(tc, q, k, v, Wo, bo, feat0, out):
                 in_=v[b, 512 * g : 512 * g + 512, :].rearrange("(p t) c -> p t c", t=4),
             )
 
-        def load_q(b, i):
-            nc.sync.dma_start(
-                out=q_raw[b][:, i : i + 1, :],
-                in_=q[b, P * i : P * i + P, :].rearrange("(p t) c -> p t c", t=1),
-            )
-
-        def load_q_pair(b, a):
+        def load_q(b, a):
             nc.sync.dma_start(
                 out=q_raw[b][:, 2 * a : 2 * a + 2, :],
                 in_=q[b, 256 * a : 256 * a + 256, :].rearrange("(p t) c -> p t c", t=2),
             )
+
+        def load_f(b):
+            nc.sync.dma_start(out=f_raw[b][:], in_=feat0[b].rearrange("(p t) n -> p t n", t=4))
 
         idle = keep.tile([P, 512], BF16, name="idle")
         nc.vector.memset(idle[:], 0.0)
@@ -84,28 +80,25 @@ def tile_i2p_crossattention_pa_kernel(tc, q, k, v, Wo, bo, feat0, out):
         load_q(0, 0)
         load_k(0, 0, 0, 2)
         load_k(0, 0, 2, 4)
-        load_q(0, 1)
         load_k(0, 1, 0, 2)
         load_k(0, 1, 2, 4)
-        load_q_pair(0, 1)
+        load_q(0, 1)
+        load_k(1, 0)
         load_v(0, 0)
         load_v(0, 1)
-        nc.sync.dma_start(out=w_raw[:], in_=Wo.rearrange("(p t) c -> p t c", t=4))
-        load_k(1, 0)
         load_k(1, 1)
-        load_q_pair(1, 0)
-        load_q_pair(1, 1)
-        nc.sync.dma_start(out=f_raw[0][:], in_=feat0[0].rearrange("(p t) n -> p t n", t=4))
+        load_q(1, 0)
+        load_q(1, 1)
+        nc.sync.dma_start(out=w_raw[:], in_=Wo.rearrange("(p t) c -> p t c", t=4))
+        load_f(0)
         load_v(1, 0)
         load_v(1, 1)
-        nc.sync.dma_start(out=f_raw[1][:], in_=feat0[1].rearrange("(p t) n -> p t n", t=4))
+        load_f(1)
 
-        def keep_busy():
-            ps = psum.tile([P, 512], F32, name="idle_ps", tag="mx", bufs=NB["mx"])
-            nc.tensor.matmul(out=ps[:], lhsT=idle[:, 0:P], rhs=idle[:], start=True, stop=True)
-
-        for x in range(4):
-            keep_busy()
+        def keep_busy(n=1):
+            for x in range(n):
+                ps = psum.tile([P, 512], F32, name="idle_ps", tag="mx", bufs=NB["mx"])
+                nc.tensor.matmul(out=ps[:], lhsT=idle[:, 0:P], rhs=idle[:], start=True, stop=True)
 
         def copy_on(eng, dst, src):
             if eng == "s":
@@ -113,57 +106,35 @@ def tile_i2p_crossattention_pa_kernel(tc, q, k, v, Wo, bo, feat0, out):
             else:
                 nc.vector.tensor_copy(out=dst, in_=src)
 
-        def word_job(raw, dst, r0, rows, eng, tag, c0, mix):
+        def word_job(raw, dst, eng, tag="tp", order="p u (n r) -> p u n r", src="p u r n -> p u n r"):
             hold = []
 
             def run(x):
                 if not hold:
-                    hold.append(psum.tile([P, 2, rows, P], F32, name="wps", tag=tag, bufs=NB[tag]))
-                u, r = divmod(x, rows)
-                nc.tensor.transpose(
-                    hold[0][:, u, r, :],
-                    raw[:, r0 + r, :].bitcast(F32)[:, P * u : P * u + P],
-                    ident_f[:],
-                )
-                if x == 2 * rows - 1:
-                    cols = dst[:, :, c0 : c0 + rows * P]
-                    if mix:
-                        copy_on(
-                            eng,
-                            cols.rearrange("p u (n r) -> p u n r", r=rows),
-                            hold[0][:].rearrange("p u r n -> p u n r"),
-                        )
-                    else:
-                        copy_on(eng, cols, hold[0][:].rearrange("p u r n -> p u (r n)"))
-
-            return [(lambda x=x: run(x)) for x in range(2 * rows)]
-
-        def k_job(b, a, eng="s", tag="tp"):
-            return word_job(k_raw[b], kT[b][a // 2], 2 * a, 2, eng, tag, 2 * P * (a % 2), True)
-
-        def q_job(b, r0, rows, eng="s", tag="tp"):
-            return word_job(q_raw[b], qT[b], r0, rows, eng, tag, P * r0, rows == 2)
-
-        def w_job(a, eng="s"):
-            hold = []
-
-            def run(x):
-                if not hold:
-                    hold.append(psum.tile([P, 2, 2, P], F32, name="wps", tag="tp", bufs=NB["tp"]))
+                    hold.append(psum.tile([P, 2, 2, P], F32, name="wps", tag=tag, bufs=NB[tag]))
                 u, r = divmod(x, 2)
                 nc.tensor.transpose(
-                    hold[0][:, u, r, :],
-                    w_raw[:, 2 * a + r, :].bitcast(F32)[:, P * u : P * u + P],
-                    ident_f[:],
+                    hold[0][:, u, r, :], raw[:, r, :].bitcast(F32)[:, P * u : P * u + P], ident_f[:]
                 )
                 if x == 3:
-                    copy_on(
-                        eng,
-                        wG[:, 2 * P * a : 2 * P * a + 2 * P, :].rearrange("p (r n) u -> p r n u", r=2),
-                        hold[0][:].rearrange("p u r n -> p r n u"),
-                    )
+                    copy_on(eng, dst.rearrange(order, r=2), hold[0][:].rearrange(src))
 
             return [(lambda x=x: run(x)) for x in range(4)]
+
+        def k_job(b, a, eng, tag="tp"):
+            return word_job(k_raw[b][:, 2 * a : 2 * a + 2, :], kT[b][a // 2][:, a % 2, :, :], eng, tag)
+
+        def q_job(b, a, eng, tag="tp"):
+            return word_job(q_raw[b][:, 2 * a : 2 * a + 2, :], qT[b][:, a, :, :], eng, tag)
+
+        def w_job(a, eng):
+            return word_job(
+                w_raw[:, 2 * a : 2 * a + 2, :],
+                wG[:, 2 * P * a : 2 * P * a + 2 * P, :],
+                eng,
+                order="p (r n) u -> p r n u",
+                src="p u r n -> p r n u",
+            )
 
         def w_quant():
             nc.vector.quantize_mx(
@@ -172,52 +143,19 @@ def tile_i2p_crossattention_pa_kernel(tc, q, k, v, Wo, bo, feat0, out):
                 in_=wG[:].rearrange("p o u -> p (o u)").bitcast(BF16),
             )
 
-        def add_bias(b, ot):
-            if b == 0:
-                nc.gpsimd.tensor_scalar(
-                    out=fb[b][:, ot, :],
-                    in0=f_raw[b][:, ot, :],
-                    scalar1=1.0,
-                    scalar2=bo_col[:, ot : ot + 1],
-                    op0=ALU.mult,
-                    op1=ALU.add,
-                )
-            elif b == 0:
-                nc.vector.tensor_scalar(
-                    out=fb[b][:, ot, :],
-                    in0=f_raw[b][:, ot, :],
-                    scalar1=bo_col[:, ot : ot + 1],
-                    scalar2=None,
-                    op0=ALU.add,
-                )
-            else:
-                nc.scalar.activation(
-                    out=fb[b][:, ot, :],
-                    in_=f_raw[b][:, ot, :],
-                    func=ACT.Identity,
-                    bias=bo_col[:, ot : ot + 1],
-                    scale=1.0,
-                )
-
         vG = {}
 
         def v_regroup(b, g, hf, eng):
             if hf == 0:
                 vG[(b, g)] = work.tile([P, C, 4], BF16, name="vG", tag="vG", bufs=4, align_bytes=64)
             c0 = 256 * hf
+            dst = vG[(b, g)][:, c0 : c0 + 256, :].rearrange("p (e q) t -> p e q t", e=2)
+            src = v_raw[b][:, 4 * g : 4 * g + 4, c0 : c0 + 256].rearrange("p t (q e) -> p e q t", e=2)
             if eng == "v":
-                nc.vector.tensor_copy(
-                    out=vG[(b, g)][:, c0 : c0 + 256, :].rearrange("p (e q) t -> p e q t", e=2),
-                    in_=v_raw[b][:, 4 * g : 4 * g + 4, c0 : c0 + 256].rearrange("p t (q e) -> p e q t", e=2),
-                )
+                nc.vector.tensor_copy(out=dst, in_=src)
             else:
                 nc.gpsimd.tensor_scalar(
-                    out=vG[(b, g)][:, c0 : c0 + 256, :].rearrange("p (e q) t -> p e q t", e=2),
-                    in0=v_raw[b][:, 4 * g : 4 * g + 4, c0 : c0 + 256].rearrange("p t (q e) -> p e q t", e=2),
-                    scalar1=1.0,
-                    scalar2=0.0,
-                    op0=ALU.mult,
-                    op1=ALU.add,
+                    out=dst, in0=src, scalar1=1.0, scalar2=0.0, op0=ALU.mult, op1=ALU.add
                 )
 
         def v_quant(b, g):
@@ -227,32 +165,39 @@ def tile_i2p_crossattention_pa_kernel(tc, q, k, v, Wo, bo, feat0, out):
                 in_=vG[(b, g)][:].rearrange("p c t -> p (c t)"),
             )
 
-        kTb = [[t[:].bitcast(BF16).rearrange("p u (m e) -> p u m e", e=2) for t in ts] for ts in kT]
-        qTb = [t[:].bitcast(BF16).rearrange("p u (m e) -> p u m e", e=2) for t in qT]
+        kTb = [[t[:].bitcast(BF16).rearrange("p a u (m e) -> p a u m e", e=2) for t in ts] for ts in kT]
+        qTb = [t[:].bitcast(BF16).rearrange("p a u (m e) -> p a u m e", e=2) for t in qT]
         st = [{} for s in range(NT)]
 
-        def energy(s, h, cc):
+        def q_col(s, cc):
             b, i = divmod(s, 4)
+            u, e2 = divmod(cc, 2)
+            return qTb[b][:, i // 2, u, P * (i % 2) : P * (i % 2) + P, e2]
+
+        def energy(s, h, cc):
+            b = s // 4
             d = st[s]
             if cc == 0:
-                tag = {(0, 1): "mx", (1, 1): "mx", (7, 1): "tp"}.get((s, h), "en")
+                tag = EN_TAG.get((s, h), "en")
                 d["en%d" % h] = psum.tile([P, 512], F32, name="en", tag=tag, bufs=NB[tag])
             u, e2 = divmod(cc, 2)
             nc.tensor.matmul(
-                out=d["en%d" % h][:],
-                lhsT=qTb[b][:, u, P * i : P * i + P, e2],
-                rhs=kTb[b][h][:, u, :, e2],
+                out=d["en%d" % h][:].rearrange("p (a m) -> p a m", a=2),
+                lhsT=q_col(s, cc),
+                rhs=kTb[b][h][:, :, u, :, e2],
                 start=(cc == 0),
                 stop=(cc == 3),
             )
 
         def energy_quarter(s, w, cc):
-            b, i = divmod(s, 4)
+            b = s // 4
             u, e2 = divmod(cc, 2)
+            if cc == 0 and w == 0:
+                st[s]["en0"] = psum.tile([P, 512], F32, name="en", tag="en", bufs=NB["en"])
             nc.tensor.matmul(
                 out=st[s]["en0"][:, 256 * w : 256 * w + 256],
-                lhsT=qTb[b][:, u, P * i : P * i + P, e2],
-                rhs=kTb[b][0][:, u, 256 * w : 256 * w + 256, e2],
+                lhsT=q_col(s, cc),
+                rhs=kTb[b][0][:, w, u, :, e2],
                 start=(cc == 0),
                 stop=(cc == 3),
             )
@@ -260,9 +205,7 @@ def tile_i2p_crossattention_pa_kernel(tc, q, k, v, Wo, bo, feat0, out):
         def max0(s):
             d = st[s]
             d["mx"] = work.tile([P, 1], F32, name="mx", tag="mx", bufs=4)
-            nc.vector.tensor_reduce(
-                out=d["mx"][:], in_=d["en0"][:], axis=AX.X, op=ALU.max, negate=True
-            )
+            nc.vector.tensor_reduce(out=d["mx"][:], in_=d["en0"][:], axis=AX.X, op=ALU.max, negate=True)
 
         def max1(s):
             d = st[s]
@@ -278,19 +221,20 @@ def tile_i2p_crossattention_pa_kernel(tc, q, k, v, Wo, bo, feat0, out):
                 accum_out=d["nm"][:],
             )
 
-        def exps(s):
+        def exp_half(s, h):
             d = st[s]
-            d["e"] = work.tile([P, M], BF16, name="e", tag="e", bufs=3)
-            d["rs"] = work.tile([P, 2], F32, name="rs", tag="rs", bufs=4)
-            for h in range(2):
-                nc.scalar.activation(
-                    out=d["e"][:, 512 * h : 512 * h + 512],
-                    in_=d["en%d" % h][:],
-                    func=ACT.Exp,
-                    bias=d["nm"][:, 0:1],
-                    scale=1.0,
-                    accum_out=d["rs"][:, h : h + 1],
-                )
+            if h == 0:
+                d["e"] = work.tile([P, M], BF16, name="e", tag="e", bufs=3)
+                d["rs"] = work.tile([P, 2], F32, name="rs", tag="rs", bufs=4)
+                d["eG"] = work.tile([P, 2, P, 2], F32, name="eG", tag="eG", bufs=3, align_bytes=64)
+            nc.scalar.activation(
+                out=d["e"][:, 512 * h : 512 * h + 512],
+                in_=d["en%d" % h][:],
+                func=ACT.Exp,
+                bias=d["nm"][:, 0:1],
+                scale=1.0,
+                accum_out=d["rs"][:, h : h + 1],
+            )
 
         def rsum(s):
             d = st[s]
@@ -309,22 +253,27 @@ def tile_i2p_crossattention_pa_kernel(tc, q, k, v, Wo, bo, feat0, out):
             d = st[s]
             nc.vector.reciprocal(out=d["ri"][:], in_=d["rq"][:])
 
-        def te_tile(s):
+        def te_job(s, eng):
             d = st[s]
-            d["eG"] = work.tile([P, 2, P, 2], F32, name="eG", tag="eG", bufs=3, align_bytes=64)
 
-        def te_half(s, g, ps, at):
-            words = st[s]["e"][:].bitcast(F32)
+            def run(x):
+                words = d["e"][:].bitcast(F32)
+                if x == 0:
+                    d["te"] = psum.tile([P, 4, P], F32, name="tes", tag="tp", bufs=NB["tp"])
+                nc.tensor.transpose(d["te"][:, x, :], words[:, P * x : P * x + P], ident_f[:])
+                if x == 3:
+                    copy_on(eng, d["eG"][:], d["te"][:].rearrange("p (g u) n -> p g n u", u=2))
+
+            return [(lambda x=x: run(x)) for x in range(4)]
+
+        def te_half(s, g, eng):
+            d = st[s]
+            words = d["e"][:].bitcast(F32)
+            ps = psum.tile([P, 2, P], F32, name="tel", tag="tp", bufs=NB["tp"])
             for u in range(2):
                 w = P * (2 * g + u)
-                nc.tensor.transpose(ps[:, at + u, :], words[:, w : w + P], ident_f[:])
-
-        def te_copy(s, eng, ps, g0, g1):
-            copy_on(
-                eng,
-                st[s]["eG"][:, g0:g1, :, :],
-                ps.rearrange("p (g u) n -> p g n u", u=2),
-            )
+                nc.tensor.transpose(ps[:, u, :], words[:, w : w + P], ident_f[:])
+            copy_on(eng, d["eG"][:, g, :, :], ps[:].rearrange("p u n -> p n u"))
 
         def quant_e(s, g0=0, g1=2):
             d = st[s]
@@ -337,17 +286,60 @@ def tile_i2p_crossattention_pa_kernel(tc, q, k, v, Wo, bo, feat0, out):
                 in_=d["eG"][:, g0:g1, :, :].rearrange("p g n u -> p (g n u)").bitcast(BF16),
             )
 
+        def mx1(s, tag="mx"):
+            b = s // 4
+            d = st[s]
+            d["c1"] = psum.tile([P, C], F32, name="c1", tag=tag, bufs=NB[tag])
+            for g in range(2):
+                nc.tensor.matmul_mx(
+                    out=d["c1"][:],
+                    lhsT=d["eW"][:, P * g : P * g + P].bitcast(FP8X4),
+                    lhsT_scale=d["eS"][:, P * g : P * g + P],
+                    rhs=vW[b][:, g, :].bitcast(FP8X4),
+                    rhs_scale=vS[b][:, g, :],
+                    start=(g == 0),
+                    stop=(g == 1),
+                )
+
+        def ctx_out(s, h0=0, h1=2, eng="s"):
+            d = st[s]
+            if h0 == 0:
+                d["cx"] = work.tile([P, C], BF16, name="cx", tag="cx", bufs=3)
+            dst = d["cx"][:, 256 * h0 : 256 * h1].rearrange("p (h q e) -> p h q e", q=P, e=2)
+            src = d["c1"][:, 256 * h0 : 256 * h1].rearrange("p (h e q) -> p h q e", q=P, e=2)
+            if eng == "s":
+                nc.scalar.activation(out=dst, in_=src, func=ACT.Copy, scale=d["ri"][:, 0:1])
+            else:
+                nc.vector.tensor_scalar(out=dst, in0=src, scalar1=d["ri"][:, 0:1], scalar2=None, op0=ALU.mult)
+
+        def tc_job(s, eng):
+            d = st[s]
+            d["cG"] = work.tile([P, P, 4], BF16, name="cG", tag="cG", bufs=3, align_bytes=64)
+
+            def run(u):
+                if u == 0:
+                    d["tc"] = psum.tile([P, 2, P], F32, name="tcs", tag="tp", bufs=NB["tp"])
+                nc.tensor.transpose(d["tc"][:, u, :], d["cx"][:].bitcast(F32)[:, P * u : P * u + P], ident_f[:])
+                if u == 1:
+                    copy_on(
+                        eng,
+                        d["cG"][:].rearrange("p n t -> p (n t)").bitcast(F32).rearrange("p (n u) -> p n u", u=2),
+                        d["tc"][:].rearrange("p u n -> p n u"),
+                    )
+
+            return [(lambda u=u: run(u)) for u in range(2)]
+
         def spread_rinv(s):
             d = st[s]
             rbp = psum.tile([P, P], F32, name="rbp", tag="tp", bufs=NB["tp"])
             nc.tensor.transpose(rbp[:], d["ri"][:, 0:1].to_broadcast([P, P]), ident_f[:])
-            d["rb"] = work.tile([P, P], F32, name="rb", tag="rb", bufs=4)
+            d["rb"] = work.tile([P, P], F32, name="rb", tag="rb", bufs=2)
             nc.scalar.copy(out=d["rb"][:], in_=rbp[:])
 
-        def mx1(s, tag="mx"):
+        def mx1_t(s, tag):
             b = s // 4
             d = st[s]
-            d["c1"] = psum.tile([P, 4, P], F32, name="c1", tag=tag, bufs=NB[tag])
+            d["c1"] = psum.tile([P, 4, P], F32, name="c1t", tag=tag, bufs=NB[tag])
             for t in range(4):
                 for g in range(2):
                     nc.tensor.matmul_mx(
@@ -360,7 +352,7 @@ def tile_i2p_crossattention_pa_kernel(tc, q, k, v, Wo, bo, feat0, out):
                         stop=(g == 1),
                     )
 
-        def ctx_out(s):
+        def ctx_out_t(s):
             d = st[s]
             d["cG"] = work.tile([P, P, 4], BF16, name="cG", tag="cG", bufs=3, align_bytes=64)
             nc.vector.tensor_tensor(
@@ -403,145 +395,147 @@ def tile_i2p_crossattention_pa_kernel(tc, q, k, v, Wo, bo, feat0, out):
             n = 4 // len(ys)
             o_sb = work.tile([P, 4, P], F32, name="o_sb", tag="o_sb", bufs=4)
             for x, y in enumerate(ys):
+                for j in range(n):
+                    ot = n * x + j
+                    nc.vector.scalar_tensor_tensor(
+                        out=o_sb[:, ot, :],
+                        in0=y[:, j, :],
+                        scalar=bo_raw[:, ot : ot + 1],
+                        in1=f_raw[b][:, ot, P * i : P * i + P],
+                        op0=ALU.add,
+                        op1=ALU.add,
+                    )
                 ots = slice(n * x, n * x + n)
-                nc.vector.tensor_tensor(
-                    out=o_sb[:, ots, :], in0=y[:], in1=fb[b][:, ots, P * i : P * i + P], op=ALU.add
-                )
                 nc.sync.dma_start(
                     out=out[b].rearrange("(p t) n -> p t n", t=4)[:, ots, P * i : P * i + P],
                     in_=o_sb[:, ots, :],
                 )
 
-        def live(x):
-            return 0 <= x < NT
-
-        def at(s, place):
-            for call in singles.get((s, place), []):
-                call()
-
-        q02 = q_job(0, 2, 2)
-        w0, w1 = w_job(0, "sv"[0]), w_job(1, "sv"[1])
-        k10, k11, k12, k13 = [k_job(1, a, "svsv"[a]) for a in range(4)]
-        q10, q12 = q_job(1, 0, 2), q_job(1, 2, 2)
-        fills = {
-            (2, 6): w0, (2, 7): w1,
-            (3, 1): k10, (3, 2): k11, (3, 4): k12, (3, 5): k13, (3, 7): q10,
-            (4, 3): q12,
-        }
-        singles = {
-            (0, 0): [lambda hf=hf: v_regroup(0, 0, hf, "g") for hf in range(2)],
-            (0, 1): [lambda: nc.vector.tensor_copy(out=bo_col[:], in_=bo_raw[:])],
-            (0, 2): [lambda: v_regroup(0, 1, 0, "v"), lambda: v_regroup(0, 1, 1, "v")],
-            (2, 1): [lambda: v_quant(0, 0), lambda: v_quant(0, 1)],
-            (3, 0): [lambda: add_bias(0, 0), lambda: add_bias(0, 1), lambda: add_bias(0, 2), lambda: add_bias(0, 3), *[lambda g=g, hf=hf: v_regroup(1, g, hf, "g") for g in range(2) for hf in range(2)]],
-            (3, 1): [w_quant],
-            (4, 1): [lambda: add_bias(1, 0), lambda: add_bias(1, 1)],
-            (5, 1): [lambda: v_quant(1, 0), lambda: add_bias(1, 2), lambda: add_bias(1, 3)],
-            (5, 2): [lambda: v_quant(1, 1)],
-        }
+        EN_TAG = {(0, 1): "mx", (1, 1): "mx"}
 
         def ops(*jobs):
             for job in jobs:
                 for op in job:
                     op()
 
-        at(0, 0)
-        ops(q_job(0, 0, 1, "v"), [keep_busy], k_job(0, 0, "s", "en"), [keep_busy], k_job(0, 1, "v", "en"), [keep_busy])
-        st[0]["en0"] = psum.tile([P, 512], F32, name="en", tag="en", bufs=NB["en"])
+        keep_busy(4)
+        for g in range(2):
+            for hf in range(2):
+                v_regroup(0, g, hf, "g")
+        ops(q_job(0, 0, "v", "en"), [keep_busy], k_job(0, 0, "s"), [keep_busy], k_job(0, 1, "v"), [keep_busy])
         for cc in range(4):
             energy_quarter(0, 0, cc)
-        ops(q_job(0, 1, 1, "s"))
+        ops(k_job(0, 2, "s"))
         for cc in range(4):
             energy_quarter(0, 1, cc)
         max0(0)
-        ops(k_job(0, 2, "s"), k_job(0, 3, "v"))
+        ops(k_job(0, 3, "s"))
         for cc in range(4):
             energy(1, 0, cc)
         max0(1)
-        ops(q02)
-        at(0, 1)
+        ops(q_job(0, 1, "s"))
         for cc in range(4):
             energy(0, 1, cc)
         max1(0)
-        exps(0)
+        exp_half(0, 0)
+        exp_half(0, 1)
+        k1 = [k_job(1, a, "svss"[a]) for a in range(4)]
+        q1 = [q_job(1, a, "sv"[a]) for a in range(2)]
+        w = [w_job(a, "vv"[a]) for a in range(2)]
         for cc in range(4):
             energy(1, 1, cc)
         max1(1)
-        at(0, 2)
         rsum(0)
-        rinv(0)
+
+        def due(s, lag):
+            return [r for r in range(NT) if max(r, 1) + lag == s]
+
+        te = [te_job(s, "s") for s in range(NT)]
+        tcj = {}
+        fill = {
+            (2, 0): k1[0], (2, 2): k1[1], (2, 4): te[0], (2, 7): te[1],
+            (3, 0): k1[2], (3, 1): k1[3], (3, 5): q1[0],
+            (4, 0): q1[1], (4, 1): w[0], (4, 2): w[1],
+        }
+        vec = {
+            (2, 0): [lambda: rinv(0)],
+            (3, 1): [lambda: v_quant(0, 0), lambda: v_quant(0, 1)],
+            (4, 1): [w_quant],
+            (5, 1): [lambda: v_quant(1, 0)],
+            (6, 1): [lambda: v_quant(1, 1)],
+        }
         for s in range(2, NT):
-            if live(s - 4):
-                final(s - 4)
-            if live(s - 3):
-                ctx_out(s - 3)
-            if live(s - 1):
-                exps(s - 1)
-                te_tile(s - 1)
-            at(s, 0)
+            if s == 4:
+                for g in range(2):
+                    for hf in range(2):
+                        v_regroup(1, g, hf, "g")
+            exp_half(s - 1, 0)
+            for r in due(s, 3):
+                ctx_out(r)
+            exp_half(s - 1, 1)
+            for r in due(s, 3):
+                tcj[r] = tc_job(r, "s")
+            for call in vec.get((s, 0), []):
+                call()
+            for r in due(s, 2):
+                quant_e(r)
+            for r in due(s, 4):
+                final(r)
             for x in range(8):
                 energy(s, x // 4, x % 4)
-                if s == 2 and x in (2, 3):
-                    if x == 2:
-                        te_tile(0)
-                        te_bank = psum.tile([P, 4, P], F32, name="tes", tag="tp", bufs=NB["tp"])
-                    te_half(0, x - 2, te_bank, 2 * (x - 2))
-                    if x == 3:
-                        te_copy(0, "s", te_bank[:], 0, 2)
-                if x == (4 if s == 2 else 3) and live(s - 2):
-                    spread_rinv(s - 2)
                 if x == 3:
                     max0(s)
-                    if s == 2:
-                        quant_e(0)
-                    if live(s - 3):
-                        ctx_quant(s - 3)
-                    if live(s - 1):
-                        rsum(s - 1)
-                    at(s, 1)
-                if x in (5, 6) and live(s - 1):
-                    if x == 5:
-                        te_bank = psum.tile([P, 4, P], F32, name="tes", tag="tp", bufs=NB["tp"])
-                    te_half(s - 1, x - 5, te_bank, 2 * (x - 5))
-                    if x == 6:
-                        te_copy(s - 1, "s", te_bank[:], 0, 2)
-                for op in fills.get((s, x), []):
+                    for call in vec.get((s, 1), []):
+                        call()
+                if x == 5:
+                    rsum(s - 1)
+                if s > 2 and x in (3, 4):
+                    te[s - 1][x - 3]()
+                if x in (4, 5):
+                    for r in due(s, 3):
+                        tcj[r][x - 4]()
+                if s > 2 and x == 6:
+                    te[s - 1][2]()
+                    te[s - 1][3]()
+                for op in fill.get((s, x), []):
                     op()
+                if x == 6:
+                    for r in due(s, 3):
+                        ctx_quant(r)
+                    rinv(s - 1)
+            for call in vec.get((s, 2), []):
+                call()
             max1(s)
-            if live(s - 1):
-                rinv(s - 1)
-            if live(s - 1):
-                quant_e(s - 1)
-            at(s, 2)
-            if live(s - 3):
-                mx2(s - 3)
-            if live(s - 2):
-                mx1(s - 2)
+            for r in due(s, 2):
+                mx1(r)
+            for r in due(s, 3):
+                mx2(r, "tp" if r == 0 else "mx")
 
-        exps(7)
-        te_tile(7)
-        te_banks = [psum.tile([P, 2, P], F32, name="tel", tag="tp", bufs=NB["tp"]) for g in range(2)]
-        spread_rinv(6)
+        exp_half(7, 0)
+        exp_half(7, 1)
+        quant_e(6)
+        mx1(6, "en")
         final(4)
-        ctx_out(5)
-        te_half(7, 0, te_banks[0], 0)
-        te_copy(7, "v", te_banks[0][:], 0, 1)
-        ctx_quant(5)
-        te_half(7, 1, te_banks[1], 0)
-        te_copy(7, "s", te_banks[1][:], 1, 2)
-        mx1(6)
-        quant_e(7, 0, 1)
+        ctx_out(5, eng="v")
+        ctx_out(6)
+        te_half(7, 0, "v")
+        te_half(7, 1, "s")
+        keep_busy(1)
         rsum(7)
+        ops(tc_job(5, "v"))
+        keep_busy(1)
+        quant_e(7, 0, 1)
         rinv(7)
         quant_e(7, 1, 2)
-        ctx_out(6)
-        mx2(5)
+        ops(tc_job(6, "s"))
         spread_rinv(7)
-        mx1(7, "en")
-        final(5)
+        ctx_quant(5)
+        mx2(5)
+        mx1_t(7, "en")
         ctx_quant(6)
-        ctx_out(7)
         mx2(6)
+        final(5)
+        ctx_out_t(7)
         ctx_quant(7)
         final(6)
         mx2(7, "en", 2)

@@ -66,6 +66,9 @@ def tile_i2p_crossattention_pa_kernel(tc, q, k, v, Wo, bo, feat0, out):
                 in_=q[b, 256 * a : 256 * a + 256, :].rearrange("(p t) c -> p t c", t=2),
             )
 
+        def load_q_single(i):
+            nc.sync.dma_start(out=q_raw[0][:, i, :], in_=q[0, P * i : P * i + P, :])
+
         def load_f(b):
             nc.sync.dma_start(out=f_raw[b][:], in_=feat0[b].rearrange("(p t) n -> p t n", t=4))
 
@@ -77,9 +80,10 @@ def tile_i2p_crossattention_pa_kernel(tc, q, k, v, Wo, bo, feat0, out):
         make_identity(nc, ident_f[:])
 
         nc.scalar.dma_start(out=bo_raw[:], in_=bo.rearrange("(p t) -> p t", t=4))
-        load_q(0, 0)
+        load_q_single(0)
         load_k(0, 0, 0, 2)
         load_k(0, 0, 2, 4)
+        load_q_single(1)
         load_k(0, 1, 0, 2)
         load_k(0, 1, 2, 4)
         load_q(0, 1)
@@ -90,9 +94,9 @@ def tile_i2p_crossattention_pa_kernel(tc, q, k, v, Wo, bo, feat0, out):
         load_q(1, 0)
         load_q(1, 1)
         nc.sync.dma_start(out=w_raw[:], in_=Wo.rearrange("(p t) c -> p t c", t=4))
-        load_f(0)
         load_v(1, 0)
         load_v(1, 1)
+        load_f(0)
         load_f(1)
 
         def keep_busy(n=1):
@@ -121,6 +125,25 @@ def tile_i2p_crossattention_pa_kernel(tc, q, k, v, Wo, bo, feat0, out):
 
             return [(lambda x=x: run(x)) for x in range(4)]
 
+        def half_jobs(raw, dst, engs, tags):
+            def run(u):
+                hold = psum.tile([P, 2, P], F32, name="hps", tag=tags[u], bufs=NB[tags[u]])
+                for r in range(2):
+                    nc.tensor.transpose(
+                        hold[:, r, :], raw[:, r, :].bitcast(F32)[:, P * u : P * u + P], ident_f[:]
+                    )
+                copy_on(engs[u], dst[:, u, :].rearrange("p (n r) -> p r n", r=2), hold[:])
+
+            return [(lambda u=u: run(u)) for u in range(2)]
+
+        def q_single(i, eng, tag):
+            hold = psum.tile([P, 2, P], F32, name="qps", tag=tag, bufs=NB[tag])
+            for u in range(2):
+                nc.tensor.transpose(
+                    hold[:, u, :], q_raw[0][:, i, :].bitcast(F32)[:, P * u : P * u + P], ident_f[:]
+                )
+            copy_on(eng, qT[0][:, 0, :, P * i : P * i + P], hold[:])
+
         def k_job(b, a, eng, tag="tp"):
             return word_job(k_raw[b][:, 2 * a : 2 * a + 2, :], kT[b][a // 2][:, a % 2, :, :], eng, tag)
 
@@ -145,14 +168,16 @@ def tile_i2p_crossattention_pa_kernel(tc, q, k, v, Wo, bo, feat0, out):
 
         vG = {}
 
-        def v_regroup(b, g, hf, eng):
-            if hf == 0:
+        def v_regroup(b, g, hf, eng, q0=0, q1=128):
+            if hf == 0 and q0 == 0:
                 vG[(b, g)] = work.tile([P, C, 4], BF16, name="vG", tag="vG", bufs=4, align_bytes=64)
             c0 = 256 * hf
-            dst = vG[(b, g)][:, c0 : c0 + 256, :].rearrange("p (e q) t -> p e q t", e=2)
-            src = v_raw[b][:, 4 * g : 4 * g + 4, c0 : c0 + 256].rearrange("p t (q e) -> p e q t", e=2)
+            dst = vG[(b, g)][:, c0 : c0 + 256, :].rearrange("p (e q) t -> p e q t", e=2)[:, :, q0:q1, :]
+            src = v_raw[b][:, 4 * g : 4 * g + 4, c0 : c0 + 256].rearrange("p t (q e) -> p e q t", e=2)[:, :, q0:q1, :]
             if eng == "v":
                 nc.vector.tensor_copy(out=dst, in_=src)
+            elif eng == "s":
+                nc.scalar.copy(out=dst, in_=src)
             else:
                 nc.gpsimd.tensor_scalar(
                     out=dst, in0=src, scalar1=1.0, scalar2=0.0, op0=ALU.mult, op1=ALU.add
@@ -411,6 +436,26 @@ def tile_i2p_crossattention_pa_kernel(tc, q, k, v, Wo, bo, feat0, out):
                     in_=o_sb[:, ots, :],
                 )
 
+        def final_sg(s):
+            b, i = divmod(s, 4)
+            y = st[s]["y"][0]
+            yb = work.tile([P, 4, P], F32, name="yb", tag="yb", bufs=1)
+            o_sb = work.tile([P, 4, P], F32, name="o_sb", tag="o_sb", bufs=4)
+            for ot in range(4):
+                nc.scalar.activation(
+                    out=yb[:, ot, :], in_=y[:, ot, :], func=ACT.Identity, bias=bo_raw[:, ot : ot + 1], scale=1.0
+                )
+            nc.gpsimd.tensor_tensor(
+                out=o_sb[:], in0=yb[:], in1=f_raw[b][:, :, P * i : P * i + P], op=ALU.add
+            )
+            st[s]["o"] = o_sb
+
+        def store(s):
+            b, i = divmod(s, 4)
+            nc.sync.dma_start(
+                out=out[b].rearrange("(p t) n -> p t n", t=4)[:, :, P * i : P * i + P], in_=st[s]["o"][:]
+            )
+
         EN_TAG = {(0, 1): "mx", (1, 1): "mx"}
 
         def ops(*jobs):
@@ -418,11 +463,16 @@ def tile_i2p_crossattention_pa_kernel(tc, q, k, v, Wo, bo, feat0, out):
                 for op in job:
                     op()
 
-        keep_busy(4)
+        keep_busy(3)
         for g in range(2):
             for hf in range(2):
                 v_regroup(0, g, hf, "g")
-        ops(q_job(0, 0, "v", "en"), [keep_busy], k_job(0, 0, "s"), [keep_busy], k_job(0, 1, "v"), [keep_busy])
+        q_single(0, "v", "en")
+        keep_busy(1)
+        ops(half_jobs(k_raw[0][:, 0:2, :], kT[0][0][:, 0, :, :], "vs", ("tp", "tp")))
+        keep_busy(1)
+        ops(half_jobs(k_raw[0][:, 2:4, :], kT[0][0][:, 1, :, :], "vs", ("tp", "en")))
+        q_single(1, "v", "mx")
         for cc in range(4):
             energy_quarter(0, 0, cc)
         ops(k_job(0, 2, "s"))
@@ -459,16 +509,15 @@ def tile_i2p_crossattention_pa_kernel(tc, q, k, v, Wo, bo, feat0, out):
         }
         vec = {
             (2, 0): [lambda: rinv(0)],
-            (3, 1): [lambda: v_quant(0, 0), lambda: v_quant(0, 1)],
+            (3, 0): [lambda: v_quant(0, 0), lambda: v_quant(0, 1)],
             (4, 1): [w_quant],
             (5, 1): [lambda: v_quant(1, 0)],
             (6, 1): [lambda: v_quant(1, 1)],
+            (3, 1): [lambda: v_regroup(1, 0, 0, "v"), lambda: v_regroup(1, 0, 1, "v")],
+            (4, 0): [lambda: v_regroup(1, 1, 0, "v")],
+            (6, 0): [lambda: v_regroup(1, 1, 1, "v")],
         }
         for s in range(2, NT):
-            if s == 4:
-                for g in range(2):
-                    for hf in range(2):
-                        v_regroup(1, g, hf, "g")
             exp_half(s - 1, 0)
             for r in due(s, 3):
                 ctx_out(r)
@@ -489,23 +538,24 @@ def tile_i2p_crossattention_pa_kernel(tc, q, k, v, Wo, bo, feat0, out):
                         call()
                 if x == 5:
                     rsum(s - 1)
-                if s > 2 and x in (3, 4):
-                    te[s - 1][x - 3]()
-                if x in (4, 5):
+                if x == (6 if s < LAST else 7):
                     for r in due(s, 3):
-                        tcj[r][x - 4]()
-                if s > 2 and x == 6:
-                    te[s - 1][2]()
-                    te[s - 1][3]()
+                        tcj[r][0]()
+                        tcj[r][1]()
+                    if s > 2:
+                        ops(te[s - 1])
                 for op in fill.get((s, x), []):
                     op()
-                if x == 6:
+                if x == 6 and s < LAST:
                     for r in due(s, 3):
                         ctx_quant(r)
                     rinv(s - 1)
             for call in vec.get((s, 2), []):
                 call()
             max1(s)
+            if s == LAST:
+                ctx_quant(s - 3)
+                rinv(s - 1)
             for r in due(s, 2):
                 mx1(r)
             for r in due(s, 3):
@@ -515,28 +565,26 @@ def tile_i2p_crossattention_pa_kernel(tc, q, k, v, Wo, bo, feat0, out):
         exp_half(7, 1)
         quant_e(6)
         mx1(6, "en")
-        final(4)
         ctx_out(5, eng="v")
+        ops(tc_job(5, "s"))
+        final(4)
+        rsum(7)
         ctx_out(6)
         te_half(7, 0, "v")
-        te_half(7, 1, "s")
+        te_half(7, 1, "v")
         keep_busy(1)
-        rsum(7)
-        ops(tc_job(5, "v"))
-        keep_busy(1)
-        quant_e(7, 0, 1)
         rinv(7)
-        quant_e(7, 1, 2)
-        ops(tc_job(6, "s"))
         spread_rinv(7)
         ctx_quant(5)
         mx2(5)
+        ops(tc_job(6, "s"))
+        quant_e(7)
         mx1_t(7, "en")
+        final(5)
         ctx_quant(6)
         mx2(6)
-        final(5)
         ctx_out_t(7)
-        ctx_quant(7)
         final(6)
+        ctx_quant(7)
         mx2(7, "en", 2)
         final(7)

@@ -430,10 +430,14 @@ def tile_i2p_crossattention_pa_kernel(tc, q, k, v, Wo, bo, feat0, out):
                         op0=ALU.add,
                         op1=ALU.add,
                     )
-                ots = slice(n * x, n * x + n)
+                    if len(ys) > 1:
+                        nc.sync.dma_start(
+                            out=out[b].rearrange("(p t) n -> p t n", t=4)[:, ot, P * i : P * i + P],
+                            in_=o_sb[:, ot, :],
+                        )
+            if len(ys) == 1:
                 nc.sync.dma_start(
-                    out=out[b].rearrange("(p t) n -> p t n", t=4)[:, ots, P * i : P * i + P],
-                    in_=o_sb[:, ots, :],
+                    out=out[b].rearrange("(p t) n -> p t n", t=4)[:, :, P * i : P * i + P], in_=o_sb[:]
                 )
 
         def final_sg(s):
@@ -513,11 +517,13 @@ def tile_i2p_crossattention_pa_kernel(tc, q, k, v, Wo, bo, feat0, out):
             (4, 1): [w_quant],
             (5, 1): [lambda: v_quant(1, 0)],
             (6, 1): [lambda: v_quant(1, 1)],
-            (3, 1): [lambda: v_regroup(1, 0, 0, "v"), lambda: v_regroup(1, 0, 1, "v")],
-            (4, 0): [lambda: v_regroup(1, 1, 0, "v")],
-            (6, 0): [lambda: v_regroup(1, 1, 1, "v")],
         }
         for s in range(2, NT):
+            if s == 4:
+                for g in range(2):
+                    for hf in range(2):
+                        for q0 in range(0, 128, 128):
+                            v_regroup(1, g, hf, "g", q0, q0 + 128)
             exp_half(s - 1, 0)
             for r in due(s, 3):
                 ctx_out(r)
@@ -571,17 +577,17 @@ def tile_i2p_crossattention_pa_kernel(tc, q, k, v, Wo, bo, feat0, out):
         rsum(7)
         ctx_out(6)
         te_half(7, 0, "v")
+        rinv(7)
         te_half(7, 1, "v")
         keep_busy(1)
-        rinv(7)
         spread_rinv(7)
         ctx_quant(5)
-        mx2(5)
         ops(tc_job(6, "s"))
+        mx2(5)
         quant_e(7)
         mx1_t(7, "en")
-        final(5)
         ctx_quant(6)
+        final(5)
         mx2(6)
         ctx_out_t(7)
         final(6)

@@ -80,10 +80,9 @@ def tile_i2p_crossattention_pa_kernel(tc, q, k, v, Wo, bo, feat0, out):
         make_identity(nc, ident_f[:])
 
         nc.scalar.dma_start(out=bo_raw[:], in_=bo.rearrange("(p t) -> p t", t=4))
-        load_q_single(0)
+        load_q(0, 0)
         load_k(0, 0, 0, 2)
         load_k(0, 0, 2, 4)
-        load_q_single(1)
         load_k(0, 1, 0, 2)
         load_k(0, 1, 2, 4)
         load_q(0, 1)
@@ -467,16 +466,11 @@ def tile_i2p_crossattention_pa_kernel(tc, q, k, v, Wo, bo, feat0, out):
                 for op in job:
                     op()
 
-        keep_busy(3)
+        keep_busy(4)
         for g in range(2):
             for hf in range(2):
                 v_regroup(0, g, hf, "g")
-        q_single(0, "v", "en")
-        keep_busy(1)
-        ops(half_jobs(k_raw[0][:, 0:2, :], kT[0][0][:, 0, :, :], "vs", ("tp", "tp")))
-        keep_busy(1)
-        ops(half_jobs(k_raw[0][:, 2:4, :], kT[0][0][:, 1, :, :], "vs", ("tp", "en")))
-        q_single(1, "v", "mx")
+        ops(q_job(0, 0, "v", "en"), [keep_busy], k_job(0, 0, "s"), [keep_busy], k_job(0, 1, "v"), [keep_busy])
         for cc in range(4):
             energy_quarter(0, 0, cc)
         ops(k_job(0, 2, "s"))

@@ -22,7 +22,7 @@ NT = 8
 LAST = NT - 1
 FLOPS = 2 * B * (N * M * C + N * M * C + N * C * C)
 
-NB = {"en": 3, "tp": 3, "mx": 2}
+NB = {"en": 3, "tp": 2, "mx": 2, "xt": 1}
 
 
 def tile_i2p_crossattention_pa_kernel(tc, q, k, v, Wo, bo, feat0, out):
@@ -103,18 +103,27 @@ def tile_i2p_crossattention_pa_kernel(tc, q, k, v, Wo, bo, feat0, out):
                 ps = psum.tile([P, 512], F32, name="idle_ps", tag="mx", bufs=NB["mx"])
                 nc.tensor.matmul(out=ps[:], lhsT=idle[:, 0:P], rhs=idle[:], start=True, stop=True)
 
+        turns = []
+
+        def tp_tag():
+            turns.append(0)
+            return "xt" if len(turns) % 3 == 0 and spare[0] else "tp"
+
+        spare = [True]
+
         def copy_on(eng, dst, src):
             if eng == "s":
                 nc.scalar.copy(out=dst, in_=src)
             else:
                 nc.vector.tensor_copy(out=dst, in_=src)
 
-        def word_job(raw, dst, eng, tag="tp", order="p u (n r) -> p u n r", src="p u r n -> p u n r"):
+        def word_job(raw, dst, eng, tag=None, order="p u (n r) -> p u n r", src="p u r n -> p u n r"):
             hold = []
 
             def run(x):
                 if not hold:
-                    hold.append(psum.tile([P, 2, 2, P], F32, name="wps", tag=tag, bufs=NB[tag]))
+                    tg = tag or tp_tag()
+                    hold.append(psum.tile([P, 2, 2, P], F32, name="wps", tag=tg, bufs=NB[tg]))
                 u, r = divmod(x, 2)
                 nc.tensor.transpose(
                     hold[0][:, u, r, :], raw[:, r, :].bitcast(F32)[:, P * u : P * u + P], ident_f[:]
@@ -126,7 +135,8 @@ def tile_i2p_crossattention_pa_kernel(tc, q, k, v, Wo, bo, feat0, out):
 
         def half_jobs(raw, dst, engs, tags):
             def run(u):
-                hold = psum.tile([P, 2, P], F32, name="hps", tag=tags[u], bufs=NB[tags[u]])
+                tg = tags[u] or tp_tag()
+                hold = psum.tile([P, 2, P], F32, name="hps", tag=tg, bufs=NB[tg])
                 for r in range(2):
                     nc.tensor.transpose(
                         hold[:, r, :], raw[:, r, :].bitcast(F32)[:, P * u : P * u + P], ident_f[:]
@@ -143,10 +153,10 @@ def tile_i2p_crossattention_pa_kernel(tc, q, k, v, Wo, bo, feat0, out):
                 )
             copy_on(eng, qT[0][:, 0, :, P * i : P * i + P], hold[:])
 
-        def k_job(b, a, eng, tag="tp"):
+        def k_job(b, a, eng, tag=None):
             return word_job(k_raw[b][:, 2 * a : 2 * a + 2, :], kT[b][a // 2][:, a % 2, :, :], eng, tag)
 
-        def q_job(b, a, eng, tag="tp"):
+        def q_job(b, a, eng, tag=None):
             return word_job(q_raw[b][:, 2 * a : 2 * a + 2, :], qT[b][:, a, :, :], eng, tag)
 
         def w_job(a, eng):
@@ -283,7 +293,8 @@ def tile_i2p_crossattention_pa_kernel(tc, q, k, v, Wo, bo, feat0, out):
             def run(x):
                 words = d["e"][:].bitcast(F32)
                 if x == 0:
-                    d["te"] = psum.tile([P, 4, P], F32, name="tes", tag="tp", bufs=NB["tp"])
+                    tg = tp_tag()
+                    d["te"] = psum.tile([P, 4, P], F32, name="tes", tag=tg, bufs=NB[tg])
                 nc.tensor.transpose(d["te"][:, x, :], words[:, P * x : P * x + P], ident_f[:])
                 if x == 3:
                     copy_on(eng, d["eG"][:], d["te"][:].rearrange("p (g u) n -> p g n u", u=2))
@@ -293,7 +304,8 @@ def tile_i2p_crossattention_pa_kernel(tc, q, k, v, Wo, bo, feat0, out):
         def te_half(s, g, eng):
             d = st[s]
             words = d["e"][:].bitcast(F32)
-            ps = psum.tile([P, 2, P], F32, name="tel", tag="tp", bufs=NB["tp"])
+            tg = tp_tag()
+            ps = psum.tile([P, 2, P], F32, name="tel", tag=tg, bufs=NB[tg])
             for u in range(2):
                 w = P * (2 * g + u)
                 nc.tensor.transpose(ps[:, u, :], words[:, w : w + P], ident_f[:])
@@ -342,7 +354,8 @@ def tile_i2p_crossattention_pa_kernel(tc, q, k, v, Wo, bo, feat0, out):
 
             def run(u):
                 if u == 0:
-                    d["tc"] = psum.tile([P, 2, P], F32, name="tcs", tag="tp", bufs=NB["tp"])
+                    tg = tp_tag()
+                    d["tc"] = psum.tile([P, 2, P], F32, name="tcs", tag=tg, bufs=NB[tg])
                 nc.tensor.transpose(d["tc"][:, u, :], d["cx"][:].bitcast(F32)[:, P * u : P * u + P], ident_f[:])
                 if u == 1:
                     copy_on(
@@ -355,7 +368,8 @@ def tile_i2p_crossattention_pa_kernel(tc, q, k, v, Wo, bo, feat0, out):
 
         def spread_rinv(s):
             d = st[s]
-            rbp = psum.tile([P, P], F32, name="rbp", tag="tp", bufs=NB["tp"])
+            tg = tp_tag()
+            rbp = psum.tile([P, P], F32, name="rbp", tag=tg, bufs=NB[tg])
             nc.tensor.transpose(rbp[:], d["ri"][:, 0:1].to_broadcast([P, P]), ident_f[:])
             d["rb"] = work.tile([P, P], F32, name="rb", tag="rb", bufs=2)
             nc.scalar.copy(out=d["rb"][:], in_=rbp[:])
@@ -459,7 +473,7 @@ def tile_i2p_crossattention_pa_kernel(tc, q, k, v, Wo, bo, feat0, out):
                 out=out[b].rearrange("(p t) n -> p t n", t=4)[:, :, P * i : P * i + P], in_=st[s]["o"][:]
             )
 
-        EN_TAG = {(0, 1): "mx", (1, 1): "mx"}
+        EN_TAG = {(0, 1): "mx", (1, 1): "mx", (5, 1): "xt", (7, 1): "xt"}
 
         def ops(*jobs):
             for job in jobs:
@@ -518,9 +532,15 @@ def tile_i2p_crossattention_pa_kernel(tc, q, k, v, Wo, bo, feat0, out):
                     for hf in range(2):
                         for q0 in range(0, 128, 128):
                             v_regroup(1, g, hf, "g", q0, q0 + 128)
+            if s == 5:
+                spare[0] = False
+            if s >= 5:
+                for r in due(s, 3):
+                    ctx_out(r)
             exp_half(s - 1, 0)
-            for r in due(s, 3):
-                ctx_out(r)
+            if s < 5:
+                for r in due(s, 3):
+                    ctx_out(r)
             exp_half(s - 1, 1)
             for r in due(s, 3):
                 tcj[r] = tc_job(r, "s")
@@ -538,10 +558,11 @@ def tile_i2p_crossattention_pa_kernel(tc, q, k, v, Wo, bo, feat0, out):
                         call()
                 if x == 5:
                     rsum(s - 1)
-                if x == (6 if s < LAST else 7):
+                if x == 4:
                     for r in due(s, 3):
                         tcj[r][0]()
                         tcj[r][1]()
+                if x == (6 if s < LAST else 7):
                     if s > 2:
                         ops(te[s - 1])
                 for op in fill.get((s, x), []):
@@ -563,6 +584,7 @@ def tile_i2p_crossattention_pa_kernel(tc, q, k, v, Wo, bo, feat0, out):
 
         exp_half(7, 0)
         exp_half(7, 1)
+        spare[0] = True
         quant_e(6)
         mx1(6, "en")
         ctx_out(5, eng="v")

@@ -530,8 +530,8 @@ def tile_i2p_crossattention_pa_kernel(tc, q, k, v, Wo, bo, feat0, out):
             if s == 4:
                 for g in range(2):
                     for hf in range(2):
-                        for q0 in range(0, 128, 128):
-                            v_regroup(1, g, hf, "g", q0, q0 + 128)
+                        for q0 in range(0, 128, 64):
+                            v_regroup(1, g, hf, "g", q0, q0 + 64)
             if s == 5:
                 spare[0] = False
             if s >= 5:

from contextlib import ExitStack
import math

import concourse.mybir as mybir
from concourse.masks import make_identity

F32 = mybir.dt.float32
BF16 = mybir.dt.bfloat16
U32 = mybir.dt.uint32
U8 = mybir.dt.uint8
FP8X4 = mybir.dt.float8_e4m3fn_x4
ALU = mybir.AluOpType
ACT = mybir.ActivationFunctionType
AX = mybir.AxisListType

P = 128
B = 2
C = 512
N = 512
M = 1024
NT = 8
LAST = NT - 1
FLOPS = 2 * B * (N * M * C + N * M * C + N * C * C)

NB = {"en": 3, "tp": 2, "mx": 2, "xt": 1}


def tile_i2p_crossattention_pa_kernel(tc, q, k, v, Wo, bo, feat0, out):
    nc = tc.nc
    with ExitStack() as ctx:
        ctx.enter_context(tc.manual_schedule())
        keep = ctx.enter_context(tc.tile_pool(name="keep", bufs=1))
        work = ctx.enter_context(tc.tile_pool(name="work", bufs=2))
        psum = ctx.enter_context(tc.psum_pool(name="psum", bufs=1))

        k_raw = [keep.tile([P, 8, C], BF16, name="k_raw%d" % b) for b in range(B)]
        q_raw = [keep.tile([P, 4, C], BF16, name="q_raw%d" % b) for b in range(B)]
        v_raw = [keep.tile([P, 8, C], BF16, name="v_raw%d" % b) for b in range(B)]
        f_raw = [keep.tile([P, 4, N], BF16, name="f_raw%d" % b) for b in range(B)]
        w_raw = keep.tile([P, 4, C], BF16, name="w_raw")
        bo_raw = keep.tile([P, 4], BF16, name="bo_raw")
        ident_f = keep.tile([P, P], F32, name="ident_f")
        kT = [[keep.tile([P, 2, 2, 256], F32, name="kT%d%d" % (b, h)) for h in range(2)] for b in range(B)]
        qT = [keep.tile([P, 2, 2, 256], F32, name="qT%d" % b) for b in range(B)]
        vW = [keep.tile([P, 2, C], U32, name="vW%d" % b, align_bytes=64) for b in range(B)]
        vS = [keep.tile([P, 2, C], U8, name="vS%d" % b, align_bytes=64) for b in range(B)]
        wG = keep.tile([P, C, 2], F32, name="wG", align_bytes=64)
        wW = keep.tile([P, C], U32, name="wW", align_bytes=64)
        wS = keep.tile([P, C], U8, name="wS", align_bytes=64)

        def load_k(b, g, t0=0, t1=4):
            nc.sync.dma_start(
                out=k_raw[b][:, 4 * g + t0 : 4 * g + t1, :],
                in_=k[b, 512 * g : 512 * g + 512, :].rearrange("(p t) c -> p t c", t=4)[:, t0:t1, :],
            )

        def load_v(b, g):
            nc.sync.dma_start(
                out=v_raw[b][:, 4 * g : 4 * g + 4, :],
                in_=v[b, 512 * g : 512 * g + 512, :].rearrange("(p t) c -> p t c", t=4),
            )

        def load_q(b, a):
            nc.sync.dma_start(
                out=q_raw[b][:, 2 * a : 2 * a + 2, :],
                in_=q[b, 256 * a : 256 * a + 256, :].rearrange("(p t) c -> p t c", t=2),
            )

        def load_q_single(i):
            nc.sync.dma_start(out=q_raw[0][:, i, :], in_=q[0, P * i : P * i + P, :])

        def load_f(b):
            nc.sync.dma_start(out=f_raw[b][:], in_=feat0[b].rearrange("(p t) n -> p t n", t=4))

        idle = keep.tile([P, 512], BF16, name="idle")
        nc.vector.memset(idle[:], 0.0)
        warm = keep.tile([P, 1], F32, name="warm")
        nc.vector.memset(warm[:], 0.0)
        nc.scalar.activation(out=warm[:], in_=warm[:], func=ACT.Exp, bias=0.0, scale=1.0)
        make_identity(nc, ident_f[:])

        nc.scalar.dma_start(out=bo_raw[:], in_=bo.rearrange("(p t) -> p t", t=4))
        load_q(0, 0)
        load_k(0, 0, 0, 2)
        load_k(0, 0, 2, 4)
        load_k(0, 1, 0, 2)
        load_k(0, 1, 2, 4)
        load_q(0, 1)
        load_k(1, 0)
        load_v(0, 0)
        load_v(0, 1)
        load_k(1, 1)
        load_q(1, 0)
        load_q(1, 1)
        nc.sync.dma_start(out=w_raw[:], in_=Wo.rearrange("(p t) c -> p t c", t=4))
        load_v(1, 0)
        load_v(1, 1)
        load_f(0)
        load_f(1)

        def keep_busy(n=1):
            for x in range(n):
                ps = psum.tile([P, 512], F32, name="idle_ps", tag="mx", bufs=NB["mx"])
                nc.tensor.matmul(out=ps[:], lhsT=idle[:, 0:P], rhs=idle[:], start=True, stop=True)

        turns = []

        def tp_tag():
            turns.append(0)
            return "xt" if len(turns) % 3 == 0 and spare[0] else "tp"

        spare = [True]

        def copy_on(eng, dst, src):
            if eng == "s":
                nc.scalar.copy(out=dst, in_=src)
            else:
                nc.vector.tensor_copy(out=dst, in_=src)

        def word_job(raw, dst, eng, tag=None, order="p u (n r) -> p u n r", src="p u r n -> p u n r"):
            hold = []

            def run(x):
                if not hold:
                    tg = tag or tp_tag()
                    hold.append(psum.tile([P, 2, 2, P], F32, name="wps", tag=tg, bufs=NB[tg]))
                u, r = divmod(x, 2)
                nc.tensor.transpose(
                    hold[0][:, u, r, :], raw[:, r, :].bitcast(F32)[:, P * u : P * u + P], ident_f[:]
                )
                if x == 3:
                    copy_on(eng, dst.rearrange(order, r=2), hold[0][:].rearrange(src))

            return [(lambda x=x: run(x)) for x in range(4)]

        def half_jobs(raw, dst, engs, tags):
            def run(u):
                tg = tags[u] or tp_tag()
                hold = psum.tile([P, 2, P], F32, name="hps", tag=tg, bufs=NB[tg])
                for r in range(2):
                    nc.tensor.transpose(
                        hold[:, r, :], raw[:, r, :].bitcast(F32)[:, P * u : P * u + P], ident_f[:]
                    )
                copy_on(engs[u], dst[:, u, :].rearrange("p (n r) -> p r n", r=2), hold[:])

            return [(lambda u=u: run(u)) for u in range(2)]

        def q_single(i, eng, tag):
            hold = psum.tile([P, 2, P], F32, name="qps", tag=tag, bufs=NB[tag])
            for u in range(2):
                nc.tensor.transpose(
                    hold[:, u, :], q_raw[0][:, i, :].bitcast(F32)[:, P * u : P * u + P], ident_f[:]
                )
            copy_on(eng, qT[0][:, 0, :, P * i : P * i + P], hold[:])

        def k_job(b, a, eng, tag=None):
            return word_job(k_raw[b][:, 2 * a : 2 * a + 2, :], kT[b][a // 2][:, a % 2, :, :], eng, tag)

        def q_job(b, a, eng, tag=None):
            return word_job(q_raw[b][:, 2 * a : 2 * a + 2, :], qT[b][:, a, :, :], eng, tag)

        def w_job(a, eng):
            return word_job(
                w_raw[:, 2 * a : 2 * a + 2, :],
                wG[:, 2 * P * a : 2 * P * a + 2 * P, :],
                eng,
                order="p (r n) u -> p r n u",
                src="p u r n -> p r n u",
            )

        def w_quant():
            nc.vector.quantize_mx(
                out=wW[:].bitcast(FP8X4),
                scales=wS[:],
                in_=wG[:].rearrange("p o u -> p (o u)").bitcast(BF16),
            )

        vG = {}

        def v_regroup(b, g, hf, eng, q0=0, q1=128):
            if hf == 0 and q0 == 0:
                vG[(b, g)] = work.tile([P, C, 4], BF16, name="vG", tag="vG", bufs=4, align_bytes=64)
            c0 = 256 * hf
            dst = vG[(b, g)][:, c0 : c0 + 256, :].rearrange("p (e q) t -> p e q t", e=2)[:, :, q0:q1, :]
            src = v_raw[b][:, 4 * g : 4 * g + 4, c0 : c0 + 256].rearrange("p t (q e) -> p e q t", e=2)[:, :, q0:q1, :]
            if eng == "v":
                nc.vector.tensor_copy(out=dst, in_=src)
            elif eng == "s":
                nc.scalar.copy(out=dst, in_=src)
            else:
                nc.gpsimd.tensor_scalar(
                    out=dst, in0=src, scalar1=1.0, scalar2=0.0, op0=ALU.mult, op1=ALU.add
                )

        def v_quant(b, g):
            nc.vector.quantize_mx(
                out=vW[b][:, g, :].bitcast(FP8X4),
                scales=vS[b][:, g, :],
                in_=vG[(b, g)][:].rearrange("p c t -> p (c t)"),
            )

        kTb = [[t[:].bitcast(BF16).rearrange("p a u (m e) -> p a u m e", e=2) for t in ts] for ts in kT]
        qTb = [t[:].bitcast(BF16).rearrange("p a u (m e) -> p a u m e", e=2) for t in qT]
        st = [{} for s in range(NT)]

        def q_col(s, cc):
            b, i = divmod(s, 4)
            u, e2 = divmod(cc, 2)
            return qTb[b][:, i // 2, u, P * (i % 2) : P * (i % 2) + P, e2]

        def energy(s, h, cc):
            b = s // 4
            d = st[s]
            if cc == 0:
                tag = EN_TAG.get((s, h), "en")
                d["en%d" % h] = psum.tile([P, 512], F32, name="en", tag=tag, bufs=NB[tag])
            u, e2 = divmod(cc, 2)
            nc.tensor.matmul(
                out=d["en%d" % h][:].rearrange("p (a m) -> p a m", a=2),
                lhsT=q_col(s, cc),
                rhs=kTb[b][h][:, :, u, :, e2],
                start=(cc == 0),
                stop=(cc == 3),
            )

        def energy_quarter(s, w, cc):
            b = s // 4
            u, e2 = divmod(cc, 2)
            if cc == 0 and w == 0:
                st[s]["en0"] = psum.tile([P, 512], F32, name="en", tag="en", bufs=NB["en"])
            nc.tensor.matmul(
                out=st[s]["en0"][:, 256 * w : 256 * w + 256],
                lhsT=q_col(s, cc),
                rhs=kTb[b][0][:, w, u, :, e2],
                start=(cc == 0),
                stop=(cc == 3),
            )

        def max0(s):
            d = st[s]
            d["mx"] = work.tile([P, 1], F32, name="mx", tag="mx", bufs=4)
            nc.vector.tensor_reduce(out=d["mx"][:], in_=d["en0"][:], axis=AX.X, op=ALU.max, negate=True)

        def max1(s):
            d = st[s]
            d["nm"] = work.tile([P, 1], F32, name="nm", tag="nm", bufs=4)
            junk = work.tile([P, 512], BF16, name="junk", tag="junk", bufs=2)
            nc.vector.tensor_scalar(
                out=junk[:],
                in0=d["en1"][:],
                scalar1=-1.0,
                scalar2=d["mx"][:, 0:1],
                op0=ALU.mult,
                op1=ALU.min,
                accum_out=d["nm"][:],
            )

        def exp_half(s, h):
            d = st[s]
            if h == 0:
                d["e"] = work.tile([P, M], BF16, name="e", tag="e", bufs=3)
                d["rs"] = work.tile([P, 2], F32, name="rs", tag="rs", bufs=4)
                d["eG"] = work.tile([P, 2, P, 2], F32, name="eG", tag="eG", bufs=3, align_bytes=64)
            nc.scalar.activation(
                out=d["e"][:, 512 * h : 512 * h + 512],
                in_=d["en%d" % h][:],
                func=ACT.Exp,
                bias=d["nm"][:, 0:1],
                scale=1.0,
                accum_out=d["rs"][:, h : h + 1],
            )

        def rsum(s):
            d = st[s]
            d["rq"] = work.tile([P, 1], F32, name="rq", tag="rq", bufs=4)
            d["ri"] = work.tile([P, 1], F32, name="ri", tag="ri", bufs=4)
            nc.vector.tensor_scalar(
                out=d["rq"][:],
                in0=d["rs"][:, 0:1],
                scalar1=d["rs"][:, 1:2],
                scalar2=math.sqrt(C),
                op0=ALU.add,
                op1=ALU.mult,
            )

        def rinv(s):
            d = st[s]
            nc.vector.reciprocal(out=d["ri"][:], in_=d["rq"][:])

        def te_job(s, eng):
            d = st[s]

            def run(x):
                words = d["e"][:].bitcast(F32)
                if x == 0:
                    tg = tp_tag()
                    d["te"] = psum.tile([P, 4, P], F32, name="tes", tag=tg, bufs=NB[tg])
                nc.tensor.transpose(d["te"][:, x, :], words[:, P * x : P * x + P], ident_f[:])
                if x == 3:
                    copy_on(eng, d["eG"][:], d["te"][:].rearrange("p (g u) n -> p g n u", u=2))

            return [(lambda x=x: run(x)) for x in range(4)]

        def te_half(s, g, eng):
            d = st[s]
            words = d["e"][:].bitcast(F32)
            tg = tp_tag()
            ps = psum.tile([P, 2, P], F32, name="tel", tag=tg, bufs=NB[tg])
            for u in range(2):
                w = P * (2 * g + u)
                nc.tensor.transpose(ps[:, u, :], words[:, w : w + P], ident_f[:])
            copy_on(eng, d["eG"][:, g, :, :], ps[:].rearrange("p u n -> p n u"))

        def quant_e(s, g0=0, g1=2):
            d = st[s]
            if g0 == 0:
                d["eW"] = work.tile([P, 2 * P], U32, name="eW", tag="eW", bufs=4, align_bytes=64)
                d["eS"] = work.tile([P, 2 * P], U8, name="eS", tag="eS", bufs=4, align_bytes=64)
            nc.vector.quantize_mx(
                out=d["eW"][:, P * g0 : P * g1].bitcast(FP8X4),
                scales=d["eS"][:, P * g0 : P * g1],
                in_=d["eG"][:, g0:g1, :, :].rearrange("p g n u -> p (g n u)").bitcast(BF16),
            )

        def mx1(s, tag="mx"):
            b = s // 4
            d = st[s]
            d["c1"] = psum.tile([P, C], F32, name="c1", tag=tag, bufs=NB[tag])
            for g in range(2):
                nc.tensor.matmul_mx(
                    out=d["c1"][:],
                    lhsT=d["eW"][:, P * g : P * g + P].bitcast(FP8X4),
                    lhsT_scale=d["eS"][:, P * g : P * g + P],
                    rhs=vW[b][:, g, :].bitcast(FP8X4),
                    rhs_scale=vS[b][:, g, :],
                    start=(g == 0),
                    stop=(g == 1),
                )

        def ctx_out(s, h0=0, h1=2, eng="s"):
            d = st[s]
            if h0 == 0:
                d["cx"] = work.tile([P, C], BF16, name="cx", tag="cx", bufs=3)
            dst = d["cx"][:, 256 * h0 : 256 * h1].rearrange("p (h q e) -> p h q e", q=P, e=2)
            src = d["c1"][:, 256 * h0 : 256 * h1].rearrange("p (h e q) -> p h q e", q=P, e=2)
            if eng == "s":
                nc.scalar.activation(out=dst, in_=src, func=ACT.Copy, scale=d["ri"][:, 0:1])
            else:
                nc.vector.tensor_scalar(out=dst, in0=src, scalar1=d["ri"][:, 0:1], scalar2=None, op0=ALU.mult)

        def tc_job(s, eng):
            d = st[s]
            d["cG"] = work.tile([P, P, 4], BF16, name="cG", tag="cG", bufs=3, align_bytes=64)

            def run(u):
                if u == 0:
                    tg = tp_tag()
                    d["tc"] = psum.tile([P, 2, P], F32, name="tcs", tag=tg, bufs=NB[tg])
                nc.tensor.transpose(d["tc"][:, u, :], d["cx"][:].bitcast(F32)[:, P * u : P * u + P], ident_f[:])
                if u == 1:
                    copy_on(
                        eng,
                        d["cG"][:].rearrange("p n t -> p (n t)").bitcast(F32).rearrange("p (n u) -> p n u", u=2),
                        d["tc"][:].rearrange("p u n -> p n u"),
                    )

            return [(lambda u=u: run(u)) for u in range(2)]

        def spread_rinv(s):
            d = st[s]
            tg = tp_tag()
            rbp = psum.tile([P, P], F32, name="rbp", tag=tg, bufs=NB[tg])
            nc.tensor.transpose(rbp[:], d["ri"][:, 0:1].to_broadcast([P, P]), ident_f[:])
            d["rb"] = work.tile([P, P], F32, name="rb", tag="rb", bufs=2)
            nc.scalar.copy(out=d["rb"][:], in_=rbp[:])

        def mx1_t(s, tag):
            b = s // 4
            d = st[s]
            d["c1"] = psum.tile([P, 4, P], F32, name="c1t", tag=tag, bufs=NB[tag])
            for t in range(4):
                for g in range(2):
                    nc.tensor.matmul_mx(
                        out=d["c1"][:, t, :],
                        lhsT=vW[b][:, g, P * t : P * t + P].bitcast(FP8X4),
                        lhsT_scale=vS[b][:, g, P * t : P * t + P],
                        rhs=d["eW"][:, P * g : P * g + P].bitcast(FP8X4),
                        rhs_scale=d["eS"][:, P * g : P * g + P],
                        start=(g == 0),
                        stop=(g == 1),
                    )

        def ctx_out_t(s):
            d = st[s]
            d["cG"] = work.tile([P, P, 4], BF16, name="cG", tag="cG", bufs=3, align_bytes=64)
            nc.vector.tensor_tensor(
                out=d["cG"][:],
                in0=d["c1"][:].rearrange("p t n -> p n t"),
                in1=d["rb"][:].unsqueeze(2).to_broadcast([P, P, 4]),
                op=ALU.mult,
            )

        def ctx_quant(s):
            d = st[s]
            d["cW"] = work.tile([P, P], U32, name="cW", tag="cW", bufs=3, align_bytes=64)
            d["cS"] = work.tile([P, P], U8, name="cS", tag="cS", bufs=3, align_bytes=64)
            nc.vector.quantize_mx(
                out=d["cW"][:].bitcast(FP8X4),
                scales=d["cS"][:],
                in_=d["cG"][:].rearrange("p n t -> p (n t)"),
            )

        def mx2(s, tag="mx", parts=1):
            d = st[s]
            n = 4 // parts
            d["y"] = []
            for ot in range(4):
                if ot % n == 0:
                    d["y"].append(psum.tile([P, n, P], F32, name="y", tag=tag, bufs=NB[tag]))
                nc.tensor.matmul_mx(
                    out=d["y"][-1][:, ot % n, :],
                    lhsT=wW[:, P * ot : P * ot + P].bitcast(FP8X4),
                    lhsT_scale=wS[:, P * ot : P * ot + P],
                    rhs=d["cW"][:].bitcast(FP8X4),
                    rhs_scale=d["cS"][:],
                    start=True,
                    stop=True,
                )

        def final(s):
            b, i = divmod(s, 4)
            ys = st[s]["y"]
            n = 4 // len(ys)
            o_sb = work.tile([P, 4, P], F32, name="o_sb", tag="o_sb", bufs=4)
            for x, y in enumerate(ys):
                for j in range(n):
                    ot = n * x + j
                    nc.vector.scalar_tensor_tensor(
                        out=o_sb[:, ot, :],
                        in0=y[:, j, :],
                        scalar=bo_raw[:, ot : ot + 1],
                        in1=f_raw[b][:, ot, P * i : P * i + P],
                        op0=ALU.add,
                        op1=ALU.add,
                    )
                    if len(ys) > 1:
                        nc.sync.dma_start(
                            out=out[b].rearrange("(p t) n -> p t n", t=4)[:, ot, P * i : P * i + P],
                            in_=o_sb[:, ot, :],
                        )
            if len(ys) == 1:
                nc.sync.dma_start(
                    out=out[b].rearrange("(p t) n -> p t n", t=4)[:, :, P * i : P * i + P], in_=o_sb[:]
                )

        def final_sg(s):
            b, i = divmod(s, 4)
            y = st[s]["y"][0]
            yb = work.tile([P, 4, P], F32, name="yb", tag="yb", bufs=1)
            o_sb = work.tile([P, 4, P], F32, name="o_sb", tag="o_sb", bufs=4)
            for ot in range(4):
                nc.scalar.activation(
                    out=yb[:, ot, :], in_=y[:, ot, :], func=ACT.Identity, bias=bo_raw[:, ot : ot + 1], scale=1.0
                )
            nc.gpsimd.tensor_tensor(
                out=o_sb[:], in0=yb[:], in1=f_raw[b][:, :, P * i : P * i + P], op=ALU.add
            )
            st[s]["o"] = o_sb

        def store(s):
            b, i = divmod(s, 4)
            nc.sync.dma_start(
                out=out[b].rearrange("(p t) n -> p t n", t=4)[:, :, P * i : P * i + P], in_=st[s]["o"][:]
            )

        EN_TAG = {(0, 1): "mx", (1, 1): "mx", (5, 1): "xt", (7, 1): "xt"}

        def ops(*jobs):
            for job in jobs:
                for op in job:
                    op()

        keep_busy(4)
        for g in range(2):
            for hf in range(2):
                v_regroup(0, g, hf, "g")
        ops(q_job(0, 0, "v", "en"), [keep_busy], k_job(0, 0, "s"), [keep_busy], k_job(0, 1, "v"), [keep_busy])
        for cc in range(4):
            energy_quarter(0, 0, cc)
        ops(k_job(0, 2, "s"))
        for cc in range(4):
            energy_quarter(0, 1, cc)
        max0(0)
        ops(k_job(0, 3, "s"))
        for cc in range(4):
            energy(1, 0, cc)
        max0(1)
        ops(q_job(0, 1, "s"))
        for cc in range(4):
            energy(0, 1, cc)
        max1(0)
        exp_half(0, 0)
        exp_half(0, 1)
        k1 = [k_job(1, a, "svss"[a]) for a in range(4)]
        q1 = [q_job(1, a, "sv"[a]) for a in range(2)]
        w = [w_job(a, "vv"[a]) for a in range(2)]
        for cc in range(4):
            energy(1, 1, cc)
        max1(1)
        rsum(0)

        def due(s, lag):
            return [r for r in range(NT) if max(r, 1) + lag == s]

        te = [te_job(s, "s") for s in range(NT)]
        tcj = {}
        fill = {
            (2, 0): k1[0], (2, 2): k1[1], (2, 4): te[0], (2, 7): te[1],
            (3, 0): k1[2], (3, 1): k1[3], (3, 5): q1[0],
            (4, 0): q1[1], (4, 1): w[0], (4, 2): w[1],
        }
        vec = {
            (2, 0): [lambda: rinv(0)],
            (3, 0): [lambda: v_quant(0, 0), lambda: v_quant(0, 1)],
            (4, 1): [w_quant],
            (5, 1): [lambda: v_quant(1, 0)],
            (6, 1): [lambda: v_quant(1, 1)],
        }
        for s in range(2, NT):
            if s == 4:
                for g in range(2):
                    for hf in range(2):
                        for q0 in range(0, 128, 64):
                            v_regroup(1, g, hf, "g", q0, q0 + 64)
            if s == 5:
                spare[0] = False
            if s >= 5:
                for r in due(s, 3):
                    ctx_out(r)
            exp_half(s - 1, 0)
            if s < 5:
                for r in due(s, 3):
                    ctx_out(r)
            exp_half(s - 1, 1)
            for r in due(s, 3):
                tcj[r] = tc_job(r, "s")
            for call in vec.get((s, 0), []):
                call()
            for r in due(s, 2):
                quant_e(r)
            for r in due(s, 4):
                final(r)
            for x in range(8):
                energy(s, x // 4, x % 4)
                if x == 3:
                    max0(s)
                    for call in vec.get((s, 1), []):
                        call()
                if x == 5:
                    rsum(s - 1)
                if x == 4:
                    for r in due(s, 3):
                        tcj[r][0]()
                        tcj[r][1]()
                if x == (6 if s < LAST else 7):
                    if s > 2:
                        ops(te[s - 1])
                for op in fill.get((s, x), []):
                    op()
                if x == 6 and s < LAST:
                    for r in due(s, 3):
                        ctx_quant(r)
                    rinv(s - 1)
            for call in vec.get((s, 2), []):
                call()
            max1(s)
            if s == LAST:
                ctx_quant(s - 3)
                rinv(s - 1)
            for r in due(s, 2):
                mx1(r)
            for r in due(s, 3):
                mx2(r, "tp" if r == 0 else "mx")

        exp_half(7, 0)
        exp_half(7, 1)
        spare[0] = True
        quant_e(6)
        mx1(6, "en")
        ctx_out(5, eng="v")
        ops(tc_job(5, "s"))
        final(4)
        rsum(7)
        ctx_out(6)
        te_half(7, 0, "v")
        rinv(7)
        te_half(7, 1, "v")
        keep_busy(1)
        spread_rinv(7)
        ctx_quant(5)
        ops(tc_job(6, "s"))
        mx2(5)
        quant_e(7)
        mx1_t(7, "en")
        ctx_quant(6)
        final(5)
        mx2(6)
        ctx_out_t(7)
        final(6)
        ctx_quant(7)
        mx2(7, "en", 2)
        final(7)
